import numpy as np
import ml_dtypes


def mxq(x, axis, fmt="e4m3"):
    dtype, down = {"e4m3": (ml_dtypes.float8_e4m3fn, 7), "e5m2": (ml_dtypes.float8_e5m2, 14)}[fmt]
    v = np.moveaxis(np.asarray(x, np.float32).astype(ml_dtypes.bfloat16).astype(np.float64), axis, -1)
    blocks = v.reshape(v.shape[:-1] + (-1, 32))
    amax = np.abs(blocks).max(-1, keepdims=True)
    byte = np.maximum(np.where(amax > 0, np.frexp(amax)[1] - 1 + 127, 0) - down, 1)
    scale = np.exp2(byte - 127.0)
    codes = (blocks / scale).astype(np.float32).astype(dtype).astype(np.float64)
    return np.moveaxis((codes * scale).reshape(v.shape), -1, axis)


WIDE = False


def mx_kscale(k):
    if not WIDE:
        return np.ones(k)
    levels = np.array([10, -10, 5, -5, 0])
    a = np.random.permutation(np.resize(levels, k // 512 * 4)).reshape(k // 512, 4)
    idx = np.arange(k)
    return np.exp2(a[idx // 512, idx % 128 // 32])


BF16 = ml_dtypes.bfloat16


def bf(x):
    return np.asarray(x, np.float32).astype(BF16)


def f64(x):
    return np.asarray(x).astype(np.float64)


B, S, IN, OUT, GROUP = 4, 256, 2048, 2048, 128
SCALE_RATIO = 1.4171
EPS = 1e-6


def softplus(v):
    return np.logaddexp(v, 0.0)


def inv_softplus(b):
    return np.where(b > 30.0, b, np.log(np.expm1(np.minimum(b, 30.0)) + EPS))


def setup_inputs():
    s = mx_kscale(IN)
    hi, lo = s.max(), s.min()
    sg = np.resize(np.array([hi, lo, np.sqrt(hi), np.sqrt(lo)]) / hi, IN // GROUP)
    x = np.random.standard_normal((B, S, IN)) * np.repeat(sg, GROUP)
    latent = np.random.standard_normal((OUT, IN)) / np.sqrt(IN)
    base_scale = np.abs(latent.reshape(OUT, IN // GROUP, GROUP)).mean(axis=-1) * SCALE_RATIO
    base_scale = base_scale * np.exp2(np.random.uniform(-1.0, 1.0, (OUT, IN // GROUP)))
    raw_scales = inv_softplus(base_scale / sg)
    return {"x": bf(x), "weight_logits": bf(latent), "raw_scales": bf(raw_scales)}


def reference(x, weight_logits, raw_scales):
    wl = f64(weight_logits)
    rows, cols = wl.shape
    g = wl.reshape(rows, cols // GROUP, GROUP)
    q = np.where(g >= 0, 1.0, -1.0)
    signed = g + (q - g)
    scales = softplus(f64(raw_scales)) + EPS
    w = (signed * scales[:, :, None]).reshape(rows, cols)
    return mxq(f64(x), 2, "e4m3") @ mxq(w, 1, "e4m3").T

@@ -1,0 +1,339 @@
+from contextlib import ExitStack
+
+import concourse.mybir as mybir
+from concourse.masks import make_identity
+
+F32 = mybir.dt.float32
+BF16 = mybir.dt.bfloat16
+U8 = mybir.dt.uint8
+U32 = mybir.dt.uint32
+FP8X4 = mybir.dt.float8_e4m3fn_x4
+ALU = mybir.AluOpType
+ACT = mybir.ActivationFunctionType
+
+P = 128
+TOK = 1024
+IN = 2048
+OUT = 2048
+NG = 16
+NPASS = 4
+FLOPS = 2 * TOK * IN * OUT
+
+I32 = mybir.dt.int32
+LOG2E = 1.4426950408889634
+MAGIC = 12582912.0
+LN2_HI = 0.693145751953125
+LN2_LO = 1.4286068203094172e-06
+ATANH = (
+    0.3333333781096117,
+    0.19999438873142902,
+    0.14308442370236296,
+    0.10713829121815853,
+    0.12150466887516932,
+)
+
+
+def tile_groupedstelinear_kernel(tc, x, weight_logits, raw_scales, out):
+    nc = tc.nc
+    xf = x.flatten_outer_dims()
+    of = out.flatten_outer_dims().rearrange("(m p) o -> p m o", p=P)
+    wl = weight_logits
+
+    with ExitStack() as ctx:
+        const = ctx.enter_context(tc.tile_pool(name="const", bufs=1))
+        small = ctx.enter_context(tc.tile_pool(name="small", bufs=1))
+        chn = ctx.enter_context(tc.tile_pool(name="chn", bufs=1))
+        keep = ctx.enter_context(tc.tile_pool(name="keep", bufs=1))
+        xraw = ctx.enter_context(tc.tile_pool(name="xraw", bufs=4))
+        xwork = ctx.enter_context(tc.tile_pool(name="xwork", bufs=2))
+        wraw = ctx.enter_context(tc.tile_pool(name="wraw", bufs=8))
+        wsign = ctx.enter_context(tc.tile_pool(name="wsign", bufs=4))
+        wwork = ctx.enter_context(tc.tile_pool(name="wwork", bufs=2))
+        obuf = ctx.enter_context(tc.tile_pool(name="obuf", bufs=2))
+        ps_t = ctx.enter_context(tc.psum_pool(name="ps_t", bufs=4))
+        ps_s = ctx.enter_context(tc.psum_pool(name="ps_s", bufs=2))
+        ps_a = ctx.enter_context(tc.psum_pool(name="ps_a", bufs=2))
+
+        ident_f = const.tile([P, P], F32, name="ident_f")
+        make_identity(nc, ident_f[:])
+        ident_b = const.tile([P, P], BF16, name="ident_b")
+        make_identity(nc, ident_b[:])
+        sel = const.tile([P, P * 32], BF16, name="sel")
+        nc.gpsimd.tensor_scalar(
+            out=sel[:].rearrange("p (c r) -> p c r", r=32),
+            in0=ident_b[:].unsqueeze(2).to_broadcast([P, P, 32]),
+            scalar1=1.0,
+            scalar2=0.0,
+            op0=ALU.mult,
+            op1=ALU.add,
+        )
+        warm = small.tile([P, 1], F32, name="warm")
+        nc.vector.memset(warm[:], 0.0)
+        warm2 = small.tile([P, 1], F32, name="warm2")
+        nc.scalar.activation(out=warm2[:], in_=warm[:], func=ACT.Tanh)
+
+        xc = keep.tile([P, 8, 512], U32, name="xc", align_bytes=64)
+        xs = keep.tile([P, 8, 512], U8, name="xs", align_bytes=64)
+        wc = []
+        ws = []
+        for k in range(8):
+            wck = keep.tile([P, NPASS, 256], U32, name="wc%d" % k, align_bytes=64)
+            wsk = keep.tile([P, NPASS, 256], U8, name="ws%d" % k, align_bytes=64)
+            wc.append(wck)
+            ws.append(wsk)
+
+        xr = {}
+        wr = {}
+        sg = {}
+        st2 = {}
+        ob = {}
+
+        def load_x(m):
+            t = xraw.tile([P, IN], BF16, name="xr")
+            nc.sync.dma_start(out=t[:], in_=xf[m * P : (m + 1) * P, :])
+            xr[m] = t
+
+        def load_w(a):
+            t = wraw.tile([P, IN], BF16, name="wr")
+            nc.sync.dma_start(out=t[:], in_=wl[a * P : (a + 1) * P, :])
+            wr[a] = t
+
+        sraw = small.tile([P, 256], BF16, name="sraw")
+        nc.sync.dma_start(
+            out=sraw[:].rearrange("p (a g) -> p a g", g=NG),
+            in_=raw_scales.rearrange("(a p) g -> p a g", p=P),
+        )
+        for m in range(2):
+            load_x(m)
+        for a in range(2):
+            load_w(a)
+        for m in range(2, 4):
+            load_x(m)
+        for a in range(2, 8):
+            load_w(a)
+
+        rows = {}
+
+        def chain(h):
+            v = sraw[:, h * P : (h + 1) * P]
+
+            def f32_tile(name):
+                t = chn.tile([P, P], F32, name=name)
+                return t
+
+            absv = f32_tile("absv")
+            nc.scalar.activation(out=absv[:], in_=v, func=ACT.Abs)
+            relu = f32_tile("relu")
+            nc.scalar.activation(out=relu[:], in_=v, func=ACT.Relu)
+            xm = f32_tile("xm")
+            nc.vector.tensor_scalar(
+                out=xm[:], in0=absv[:], scalar1=-LOG2E, scalar2=MAGIC, op0=ALU.mult, op1=ALU.add
+            )
+            ni = chn.tile([P, P], I32, name="ni")
+            nc.vector.tensor_scalar(
+                out=ni[:], in0=xm[:], scalar1=MAGIC, scalar2=-120.0, op0=ALU.subtract, op1=ALU.max
+            )
+            p2 = chn.tile([P, P], I32, name="p2")
+            nc.vector.tensor_scalar(
+                out=p2[:], in0=ni[:], scalar1=127.0, scalar2=8388608.0, op0=ALU.add, op1=ALU.mult
+            )
+            r1 = f32_tile("r1")
+            nc.vector.scalar_tensor_tensor(
+                out=r1[:], in0=ni[:], scalar=-LN2_HI, in1=absv[:], op0=ALU.mult, op1=ALU.subtract
+            )
+            rr = f32_tile("rr")
+            nc.vector.scalar_tensor_tensor(
+                out=rr[:], in0=ni[:], scalar=-LN2_LO, in1=r1[:], op0=ALU.mult, op1=ALU.add
+            )
+            th = f32_tile("th")
+            nc.scalar.activation(out=th[:], in_=rr[:], func=ACT.Tanh, scale=0.5)
+            c1 = f32_tile("c1")
+            nc.scalar.activation(out=c1[:], in_=th[:], func=ACT.Identity, scale=-2.0, bias=2.0)
+            a1 = f32_tile("a1")
+            nc.vector.scalar_tensor_tensor(
+                out=a1[:], in0=th[:], scalar=1.0, in1=p2[:].bitcast(F32), op0=ALU.add, op1=ALU.mult
+            )
+            bb = f32_tile("bb")
+            nc.vector.tensor_tensor(out=bb[:], in0=a1[:], in1=c1[:], op=ALU.add)
+            rb = f32_tile("rb")
+            nc.vector.reciprocal(out=rb[:], in_=bb[:])
+            zz = f32_tile("zz")
+            nc.vector.tensor_tensor(out=zz[:], in0=a1[:], in1=rb[:], op=ALU.mult)
+            tt = f32_tile("tt")
+            nc.vector.tensor_tensor(out=tt[:], in0=zz[:], in1=zz[:], op=ALU.mult)
+            pa = f32_tile("pa")
+            nc.vector.tensor_scalar(
+                out=pa[:], in0=tt[:], scalar1=ATANH[4], scalar2=None, op0=ALU.mult
+            )
+            pb = f32_tile("pb")
+            cur, nxt = pa, pb
+            for k in (3, 2, 1, 0):
+                nc.vector.scalar_tensor_tensor(
+                    out=nxt[:], in0=cur[:], scalar=ATANH[k], in1=tt[:], op0=ALU.add, op1=ALU.mult
+                )
+                cur, nxt = nxt, cur
+            nc.vector.scalar_tensor_tensor(
+                out=nxt[:], in0=cur[:], scalar=1.0, in1=zz[:], op0=ALU.add, op1=ALU.mult
+            )
+            sp = f32_tile("sp")
+            nc.vector.scalar_tensor_tensor(
+                out=sp[:], in0=nxt[:], scalar=2.0, in1=relu[:], op0=ALU.mult, op1=ALU.add
+            )
+            st_t = ps_s.tile([P, P], F32, name="stp")
+            nc.tensor.transpose(st_t[:], sp[:], ident_f[:])
+            rw = small.tile([P, P], BF16, name="rows%d" % h)
+            nc.scalar.activation(out=rw[:], in_=st_t[:], func=ACT.Identity, scale=2.0, bias=2e-6)
+            rows[h] = rw
+
+        chain(0)
+
+        def prep_x(m):
+            xp = xwork.tile([P, IN], BF16, name="xp")
+            nc.vector.tensor_copy(
+                out=xp[:].rearrange("p (u g j) -> p g u j", u=2, g=NG),
+                in_=xr[m][:].rearrange("p (g u j) -> p g u j", g=NG, u=2),
+            )
+            if m + 4 < 8:
+                load_x(m + 4)
+            xw = xp[:].bitcast(F32)
+            xg = xwork.tile([P, IN], BF16, name="xg", align_bytes=64)
+            xgw = xg[:].bitcast(F32).rearrange("p (c r u) -> p c r u", c=NPASS, u=2)
+            for cp in range(2):
+                tp = ps_t.tile([P, 2, 2, P], F32, name="tp")
+                for ci in range(2):
+                    c = 2 * cp + ci
+                    for u in range(2):
+                        lo = u * 512 + c * P
+                        nc.tensor.transpose(tp[:, ci, u, :], xw[:, lo : lo + P], ident_f[:])
+                nc.scalar.copy(
+                    out=xgw[:, 2 * cp : 2 * cp + 2, :, :],
+                    in_=tp[:].rearrange("p c u r -> p c r u"),
+                )
+            nc.vector.quantize_mx(
+                out=xc[:, m, :].bitcast(FP8X4), scales=xs[:, m, :], in_=xg[:]
+            )
+
+        def stage_a(k):
+            s2 = wwork.tile([P, NPASS, 2, P, 2], BF16, name="st2")
+            st2[k] = s2
+            for a2 in range(2):
+                a = 2 * k + a2
+                t = wsign.tile([P, IN], BF16, name="sg")
+                nc.vector.tensor_scalar(
+                    out=t[:].rearrange("p (u g j) -> p g u j", u=2, g=NG),
+                    in0=wr[a][:].rearrange("p (g u j) -> p g u j", g=NG, u=2),
+                    scalar1=0.0,
+                    scalar2=0.5,
+                    op0=ALU.is_ge,
+                    op1=ALU.subtract,
+                )
+                sg[a] = t
+                if a + 8 < 16:
+                    load_w(a + 8)
+                stp = ps_s.tile([P, NPASS, P], F32, name="stp")
+                for c in range(NPASS):
+                    lo = ((a % 8) * NG + 4 * c) * 32
+                    nc.tensor.matmul(
+                        stp[:, c, :],
+                        lhsT=sel[:, lo : lo + P],
+                        rhs=rows[a // 8][:],
+                        start=True,
+                        stop=True,
+                    )
+                nc.scalar.copy(
+                    out=s2[:, :, a2, :, :],
+                    in_=stp[:].unsqueeze(3).to_broadcast([P, NPASS, P, 2]),
+                )
+
+        def stage_b(k):
+            wg = wwork.tile([P, NPASS, 1024], BF16, name="wg", align_bytes=64)
+            for c in range(NPASS):
+                tp = ps_t.tile([P, 2, 2, P], F32, name="tp")
+                for u in range(2):
+                    for a2 in range(2):
+                        lo = u * 512 + c * P
+                        nc.tensor.transpose(
+                            tp[:, u, a2, :],
+                            sg[2 * k + a2][:].bitcast(F32)[:, lo : lo + P],
+                            ident_f[:],
+                        )
+                nc.vector.tensor_tensor(
+                    out=wg[:, c, :].rearrange("p (o u e) -> p o u e", u=2, e=2),
+                    in0=tp[:].bitcast(BF16).rearrange("p u a (o e) -> p (a o) u e", e=2),
+                    in1=st2[k][:, c]
+                    .rearrange("p a o e -> p (a o) e")
+                    .unsqueeze(2)
+                    .to_broadcast([P, 256, 2, 2]),
+                    op=ALU.mult,
+                )
+            for c in range(NPASS):
+                nc.vector.quantize_mx(
+                    out=wc[k][:, c, :].bitcast(FP8X4), scales=ws[k][:, c, :], in_=wg[:, c, :]
+                )
+
+        def stage_m(k, mp):
+            n = k // 2
+            acc = ps_a.tile([P, 2, 256], F32, name="acc")
+            for mi in range(2):
+                m = 2 * mp + mi
+                for c in range(NPASS):
+                    nc.tensor.matmul_mx(
+                        out=acc[:, mi, :],
+                        lhsT=xc[:, m, c * P : (c + 1) * P].bitcast(FP8X4),
+                        lhsT_scale=xs[:, m, c * P : (c + 1) * P],
+                        rhs=wc[k][:, c, :].bitcast(FP8X4),
+                        rhs_scale=ws[k][:, c, :],
+                        start=(c == 0),
+                        stop=(c == NPASS - 1),
+                    )
+            lo = (k % 2) * 256
+            nc.scalar.copy(out=ob[n][:, 2 * mp : 2 * mp + 2, lo : lo + 256], in_=acc[:])
+
+        def new_ob(n):
+            t = obuf.tile([P, 8, 512], F32, name="ob")
+            ob[n] = t
+
+        def store(n, mp):
+            nc.sync.dma_start(
+                out=of[:, 2 * mp : 2 * mp + 2, n * 512 : (n + 1) * 512],
+                in_=ob[n][:, 2 * mp : 2 * mp + 2, :],
+            )
+
+        new_ob(0)
+        stage_a(0)
+        prep_x(0)
+        prep_x(1)
+        stage_b(0)
+        stage_a(1)
+        prep_x(2)
+        prep_x(3)
+        stage_m(0, 0)
+        stage_m(0, 1)
+        prep_x(4)
+        prep_x(5)
+        stage_b(1)
+        stage_a(2)
+        stage_m(0, 2)
+        stage_m(1, 0)
+        stage_m(1, 1)
+        stage_m(1, 2)
+        prep_x(6)
+        prep_x(7)
+        chain(1)
+        stage_b(2)
+        stage_a(3)
+        stage_m(0, 3)
+        stage_m(1, 3)
+        for mp in range(4):
+            store(0, mp)
+        for k in range(2, 8):
+            if k % 2 == 0:
+                new_ob(k // 2)
+            if k + 1 < 8:
+                stage_b(k + 1)
+            if k + 2 < 8:
+                stage_a(k + 2)
+            for mp in range(4):
+                stage_m(k, mp)
+                if k % 2 == 1:
+                    store(k // 2, mp)

@@ -5,6 +5,7 @@ from concourse.masks import make_identity
 
 F32 = mybir.dt.float32
 BF16 = mybir.dt.bfloat16
+I32 = mybir.dt.int32
 U8 = mybir.dt.uint8
 U32 = mybir.dt.uint32
 FP8X4 = mybir.dt.float8_e4m3fn_x4
@@ -19,7 +20,6 @@ NG = 16
 NPASS = 4
 FLOPS = 2 * TOK * IN * OUT
 
-I32 = mybir.dt.int32
 LOG2E = 1.4426950408889634
 MAGIC = 12582912.0
 LN2_HI = 0.693145751953125
@@ -30,6 +30,67 @@ ATANH = (
     0.14308442370236296,
     0.10713829121815853,
     0.12150466887516932,
+)
+
+ORDER = (
+    ("LDS",), ("LX", 0), ("LX", 1), ("LX", 2), ("C", "abs", 0), ("C", "relu", 0),
+    ("C", "xm", 0), ("C", "ni", 0), ("LX", 3), ("C", "r1", 0), ("C", "p2", 0), ("X1", 0),
+    ("C", "abs", 1), ("LW", 0), ("C", "rr", 0), ("X2", 0, 0), ("X1", 1), ("C", "th", 0),
+    ("X2", 0, 1), ("X3", 0, 0), ("C", "a1", 0), ("X2", 1, 0), ("C", "xm", 1), ("LX", 4),
+    ("C", "c1", 0), ("X2", 1, 1), ("X1", 2), ("X3", 0, 1), ("C", "bb", 0), ("X3", 1, 0),
+    ("X2", 2, 0), ("X4", 0), ("LW", 1), ("X2", 2, 1), ("X3", 1, 1), ("C", "rb", 0),
+    ("X3", 2, 0), ("LX", 5), ("X3", 2, 1), ("X4", 1), ("LX", 6), ("C", "zz", 0),
+    ("X1", 3), ("C", "tt", 0), ("X2", 3, 0), ("LX", 7), ("X4", 2), ("X2", 3, 1),
+    ("X3", 3, 0), ("C", "pa", 0), ("X1", 4), ("X3", 3, 1), ("LW", 2), ("C", "h3", 0),
+    ("X2", 4, 0), ("W1", 0), ("X2", 4, 1), ("X3", 4, 0), ("LW", 3), ("C", "h2", 0),
+    ("X4", 3), ("X3", 4, 1), ("C", "h1", 0), ("W1", 1), ("LW", 4), ("C", "h0", 0),
+    ("W2", 0, 0), ("X4", 4), ("W2", 0, 1), ("LW", 5), ("W2", 0, 2), ("C", "y2", 0),
+    ("X1", 5), ("W2", 0, 3), ("LW", 6), ("C", "sp", 0), ("C", "ni", 1), ("X1", 6),
+    ("CT", 0), ("C", "relu", 1), ("CR", 0), ("C", "r1", 1), ("WS", 0), ("LW", 7),
+    ("C", "p2", 1), ("WS", 1), ("X1", 7), ("W3", 0), ("C", "rr", 1), ("W1", 2),
+    ("W3", 1), ("WS", 2), ("W1", 3), ("LW", 8), ("W1", 4), ("C", "th", 1),
+    ("WS", 3), ("W3", 2), ("W4", 0, 0), ("LW", 9), ("W4", 0, 1), ("X2", 5, 0),
+    ("C", "c1", 1), ("LW", 10), ("WS", 4), ("W3", 3), ("W5", 0, 0), ("X2", 5, 1),
+    ("W5", 0, 1), ("W4", 0, 2), ("X3", 5, 0), ("WS", 5), ("W4", 0, 3), ("X2", 6, 0),
+    ("X3", 5, 1), ("W5", 0, 2), ("X2", 6, 1), ("X3", 6, 0), ("W5", 0, 3), ("X2", 7, 0),
+    ("C", "a1", 1), ("X2", 7, 1), ("X4", 5), ("X3", 6, 1), ("W2", 1, 0), ("C", "bb", 1),
+    ("W3", 4), ("MX", 0, 0), ("X4", 6), ("C", "rb", 1), ("X3", 7, 0), ("MX", 0, 1),
+    ("MC", 0, 0), ("W1", 5), ("X3", 7, 1), ("W2", 1, 1), ("C", "zz", 1), ("LW", 11),
+    ("W4", 1, 0), ("MC", 0, 1), ("W2", 1, 2), ("W2", 1, 3), ("W3", 5), ("C", "tt", 1),
+    ("WS", 6), ("X4", 7), ("W2", 2, 0), ("MX", 0, 2), ("C", "pa", 1), ("W5", 1, 0),
+    ("C", "h3", 1), ("W4", 1, 1), ("MX", 0, 3), ("C", "h2", 1), ("MC", 0, 2), ("W5", 1, 1),
+    ("C", "h1", 1), ("W4", 1, 2), ("W2", 2, 1), ("MC", 0, 3), ("C", "h0", 1), ("WS", 7),
+    ("W5", 1, 2), ("W2", 2, 2), ("C", "y2", 1), ("W4", 1, 3), ("C", "sp", 1), ("W2", 2, 3),
+    ("W3", 6), ("W5", 1, 3), ("W1", 6), ("MX", 1, 0), ("W1", 7), ("W3", 7),
+    ("LW", 12), ("W4", 2, 0), ("MX", 1, 1), ("MC", 1, 0), ("W4", 2, 1), ("LW", 13),
+    ("W5", 2, 0), ("CT", 1), ("MC", 1, 1), ("W2", 3, 0), ("W5", 2, 1), ("ST", 0, 0),
+    ("W2", 3, 1), ("W4", 2, 2), ("CR", 1), ("MX", 1, 2), ("W4", 2, 3), ("ST", 0, 1),
+    ("W5", 2, 2), ("MX", 1, 3), ("W5", 2, 3), ("MC", 1, 2), ("W1", 8), ("ST", 0, 2),
+    ("W1", 9), ("MX", 2, 0), ("MC", 1, 3), ("W4", 3, 0), ("LW", 14), ("W4", 3, 1),
+    ("MX", 2, 1), ("MC", 2, 0), ("W5", 3, 0), ("LW", 15), ("W5", 3, 1), ("MX", 2, 2),
+    ("W1", 10), ("MC", 2, 1), ("W1", 11), ("ST", 0, 3), ("MX", 2, 3), ("MC", 2, 2),
+    ("W2", 3, 2), ("MC", 2, 3), ("W2", 3, 3), ("W4", 3, 2), ("W2", 4, 0), ("W2", 4, 1),
+    ("W4", 3, 3), ("W2", 4, 2), ("WS", 8), ("W5", 3, 2), ("W2", 4, 3), ("W5", 3, 3),
+    ("W3", 8), ("WS", 9), ("W1", 12), ("MX", 3, 0), ("W1", 13), ("W3", 9),
+    ("W1", 14), ("MX", 3, 1), ("W1", 15), ("MC", 3, 0), ("WS", 10), ("W4", 4, 0),
+    ("MC", 3, 1), ("ST", 1, 0), ("WS", 11), ("MX", 3, 2), ("W4", 4, 1), ("W3", 10),
+    ("W5", 4, 0), ("ST", 1, 1), ("W5", 4, 1), ("MX", 3, 3), ("W3", 11), ("W4", 4, 2),
+    ("W4", 4, 3), ("W2", 5, 0), ("MC", 3, 2), ("W5", 4, 2), ("W2", 5, 1), ("W5", 4, 3),
+    ("MC", 3, 3), ("W2", 5, 2), ("ST", 1, 2), ("W4", 5, 0), ("W2", 5, 3), ("WS", 12),
+    ("W4", 5, 1), ("WS", 13), ("W3", 12), ("ST", 1, 3), ("W2", 6, 0), ("W5", 5, 0),
+    ("MX", 4, 0), ("W5", 5, 1), ("W4", 5, 2), ("W3", 13), ("W4", 5, 3), ("MX", 4, 1),
+    ("MC", 4, 0), ("W5", 5, 2), ("W5", 5, 3), ("W2", 6, 1), ("W4", 6, 0), ("MC", 4, 1),
+    ("W2", 6, 2), ("W4", 6, 1), ("W2", 6, 3), ("W2", 7, 0), ("W5", 6, 0), ("W2", 7, 1),
+    ("W5", 6, 1), ("WS", 14), ("W4", 6, 2), ("WS", 15), ("W3", 14), ("MX", 4, 2),
+    ("W4", 6, 3), ("W5", 6, 2), ("W3", 15), ("MX", 4, 3), ("W5", 6, 3), ("MC", 4, 2),
+    ("W2", 7, 2), ("W4", 7, 0), ("MC", 4, 3), ("W2", 7, 3), ("W4", 7, 1), ("MX", 5, 0),
+    ("W5", 7, 0), ("W5", 7, 1), ("W4", 7, 2), ("MX", 5, 1), ("MC", 5, 0), ("W4", 7, 3),
+    ("ST", 2, 0), ("W5", 7, 2), ("MX", 5, 2), ("MC", 5, 1), ("W5", 7, 3), ("ST", 2, 1),
+    ("MX", 5, 3), ("MC", 5, 2), ("ST", 2, 2), ("MX", 6, 0), ("MC", 5, 3), ("ST", 2, 3),
+    ("MX", 6, 1), ("MC", 6, 0), ("MX", 6, 2), ("MC", 6, 1), ("MX", 6, 3), ("MC", 6, 2),
+    ("MX", 7, 0), ("MC", 6, 3), ("MX", 7, 1), ("MC", 7, 0), ("ST", 3, 0), ("MX", 7, 2),
+    ("MC", 7, 1), ("ST", 3, 1), ("MX", 7, 3), ("MC", 7, 2), ("ST", 3, 2), ("MC", 7, 3),
+    ("ST", 3, 3),
 )
 
 
@@ -45,14 +106,16 @@ def tile_groupedstelinear_kernel(tc, x, weight_logits, raw_scales, out):
         chn = ctx.enter_context(tc.tile_pool(name="chn", bufs=1))
         keep = ctx.enter_context(tc.tile_pool(name="keep", bufs=1))
         xraw = ctx.enter_context(tc.tile_pool(name="xraw", bufs=4))
-        xwork = ctx.enter_context(tc.tile_pool(name="xwork", bufs=2))
-        wraw = ctx.enter_context(tc.tile_pool(name="wraw", bufs=8))
-        wsign = ctx.enter_context(tc.tile_pool(name="wsign", bufs=4))
+        xperm = ctx.enter_context(tc.tile_pool(name="xperm", bufs=3))
+        xgrp = ctx.enter_context(tc.tile_pool(name="xgrp", bufs=2))
+        wraw = ctx.enter_context(tc.tile_pool(name="wraw", bufs=6))
+        wsign = ctx.enter_context(tc.tile_pool(name="wsign", bufs=6))
         wwork = ctx.enter_context(tc.tile_pool(name="wwork", bufs=2))
-        obuf = ctx.enter_context(tc.tile_pool(name="obuf", bufs=2))
+        obuf = ctx.enter_context(tc.tile_pool(name="obuf", bufs=8))
         ps_t = ctx.enter_context(tc.psum_pool(name="ps_t", bufs=4))
         ps_s = ctx.enter_context(tc.psum_pool(name="ps_s", bufs=2))
         ps_a = ctx.enter_context(tc.psum_pool(name="ps_a", bufs=2))
+        ctx.enter_context(tc.manual_schedule())
 
         ident_f = const.tile([P, P], F32, name="ident_f")
         make_identity(nc, ident_f[:])
@@ -81,198 +144,228 @@ def tile_groupedstelinear_kernel(tc, x, weight_logits, raw_scales, out):
             wsk = keep.tile([P, NPASS, 256], U8, name="ws%d" % k, align_bytes=64)
             wc.append(wck)
             ws.append(wsk)
+        sraw = small.tile([P, 256], BF16, name="sraw")
 
         xr = {}
+        xp = {}
+        xg = {}
         wr = {}
         sg = {}
         st2 = {}
+        wg = {}
         ob = {}
+        tps = {}
+        stps = {}
+        accs = {}
+        rows = {}
+        ch = {}
 
-        def load_x(m):
+        def st_lds():
+            nc.sync.dma_start(
+                out=sraw[:].rearrange("p (a g) -> p a g", g=NG),
+                in_=raw_scales.rearrange("(a p) g -> p a g", p=P),
+            )
+
+        def cht(h, name, dtype=F32):
+            t = chn.tile([P, P], dtype, name=name)
+            ch[(h, name)] = t
+            return t
+
+        def stt(h, dst, in0, scalar, in1, op0, op1, dtype=F32):
+            nc.vector.scalar_tensor_tensor(
+                out=cht(h, dst, dtype)[:] if (h, dst) not in ch else ch[(h, dst)][:],
+                in0=ch[(h, in0)][:],
+                scalar=scalar,
+                in1=in1,
+                op0=op0,
+                op1=op1,
+            )
+
+        def tsc(h, dst, in0, s1, s2, op0, op1, dtype=F32):
+            nc.vector.tensor_scalar(
+                out=cht(h, dst, dtype)[:], in0=ch[(h, in0)][:], scalar1=s1, scalar2=s2, op0=op0, op1=op1
+            )
+
+        def st_c(name, h):
+            v = sraw[:, h * P : (h + 1) * P]
+            if name == "abs":
+                nc.scalar.activation(out=cht(h, "abs")[:], in_=v, func=ACT.Abs)
+            elif name == "relu":
+                nc.scalar.activation(out=cht(h, "relu")[:], in_=v, func=ACT.Relu)
+            elif name == "xm":
+                tsc(h, "xm", "abs", -LOG2E, MAGIC, ALU.mult, ALU.add)
+            elif name == "ni":
+                tsc(h, "ni", "xm", MAGIC, -120.0, ALU.subtract, ALU.max, I32)
+            elif name == "r1":
+                stt(h, "r1", "ni", -LN2_HI, ch[(h, "abs")][:], ALU.mult, ALU.subtract)
+            elif name == "rr":
+                stt(h, "rr", "ni", -LN2_LO, ch[(h, "r1")][:], ALU.mult, ALU.add)
+            elif name == "p2":
+                tsc(h, "p2", "ni", 127.0, 8388608.0, ALU.add, ALU.mult, I32)
+            elif name == "th":
+                nc.scalar.activation(
+                    out=cht(h, "th")[:], in_=ch[(h, "rr")][:], func=ACT.Tanh, scale=0.5
+                )
+            elif name == "c1":
+                nc.scalar.activation(
+                    out=cht(h, "c1")[:], in_=ch[(h, "th")][:], func=ACT.Identity, scale=-2.0, bias=2.0
+                )
+            elif name == "a1":
+                stt(h, "a1", "th", 1.0, ch[(h, "p2")][:].bitcast(F32), ALU.add, ALU.mult)
+            elif name == "bb":
+                nc.vector.tensor_tensor(
+                    out=cht(h, "bb")[:], in0=ch[(h, "a1")][:], in1=ch[(h, "c1")][:], op=ALU.add
+                )
+            elif name == "rb":
+                nc.vector.reciprocal(out=cht(h, "rb")[:], in_=ch[(h, "bb")][:])
+            elif name == "zz":
+                nc.vector.tensor_tensor(
+                    out=cht(h, "zz")[:], in0=ch[(h, "a1")][:], in1=ch[(h, "rb")][:], op=ALU.mult
+                )
+            elif name == "tt":
+                nc.vector.tensor_tensor(
+                    out=cht(h, "tt")[:], in0=ch[(h, "zz")][:], in1=ch[(h, "zz")][:], op=ALU.mult
+                )
+            elif name == "pa":
+                nc.vector.tensor_scalar(
+                    out=cht(h, "pa")[:],
+                    in0=ch[(h, "tt")][:],
+                    scalar1=ATANH[4],
+                    scalar2=None,
+                    op0=ALU.mult,
+                )
+            elif name == "h3":
+                stt(h, "pb", "pa", ATANH[3], ch[(h, "tt")][:], ALU.add, ALU.mult)
+            elif name == "h2":
+                stt(h, "pa", "pb", ATANH[2], ch[(h, "tt")][:], ALU.add, ALU.mult)
+            elif name == "h1":
+                stt(h, "pb", "pa", ATANH[1], ch[(h, "tt")][:], ALU.add, ALU.mult)
+            elif name == "h0":
+                stt(h, "pa", "pb", ATANH[0], ch[(h, "tt")][:], ALU.add, ALU.mult)
+            elif name == "y2":
+                stt(h, "pb", "pa", 1.0, ch[(h, "zz")][:], ALU.add, ALU.mult)
+            else:
+                stt(h, "sp", "pb", 2.0, ch[(h, "relu")][:], ALU.mult, ALU.add)
+
+        def st_ct(h):
+            t = ps_s.tile([P, P], F32, name="stp")
+            nc.tensor.transpose(t[:], ch[(h, "sp")][:], ident_f[:])
+            stps[("c", h)] = t
+
+        def st_cr(h):
+            rw = small.tile([P, P], BF16, name="rows%d" % h)
+            nc.scalar.activation(
+                out=rw[:], in_=stps[("c", h)][:], func=ACT.Identity, scale=2.0, bias=2e-6
+            )
+            rows[h] = rw
+
+        def st_lx(m):
             t = xraw.tile([P, IN], BF16, name="xr")
             nc.sync.dma_start(out=t[:], in_=xf[m * P : (m + 1) * P, :])
             xr[m] = t
 
-        def load_w(a):
+        def st_x1(m):
+            t = xperm.tile([P, IN], BF16, name="xp")
+            nc.vector.tensor_copy(
+                out=t[:].rearrange("p (u g j) -> p g u j", u=2, g=NG),
+                in_=xr[m][:].rearrange("p (g u j) -> p g u j", g=NG, u=2),
+            )
+            xp[m] = t
+
+        def st_x2(m, cp):
+            xw = xp[m][:].bitcast(F32)
+            tp = ps_t.tile([P, 2, 2, P], F32, name="tp")
+            for ci in range(2):
+                for u in range(2):
+                    lo = u * 512 + (2 * cp + ci) * P
+                    nc.tensor.transpose(tp[:, ci, u, :], xw[:, lo : lo + P], ident_f[:])
+            tps[("x", m, cp)] = tp
+
+        def st_x3(m, cp):
+            if m not in xg:
+                t = xgrp.tile([P, IN], BF16, name="xg", align_bytes=64)
+                xg[m] = t
+            xgw = xg[m][:].bitcast(F32).rearrange("p (c r u) -> p c r u", c=NPASS, u=2)
+            nc.scalar.copy(
+                out=xgw[:, 2 * cp : 2 * cp + 2, :, :],
+                in_=tps[("x", m, cp)][:].rearrange("p c u r -> p c r u"),
+            )
+
+        def st_x4(m):
+            nc.vector.quantize_mx(
+                out=xc[:, m, :].bitcast(FP8X4), scales=xs[:, m, :], in_=xg[m][:]
+            )
+
+        def st_lw(a):
             t = wraw.tile([P, IN], BF16, name="wr")
             nc.sync.dma_start(out=t[:], in_=wl[a * P : (a + 1) * P, :])
             wr[a] = t
 
-        sraw = small.tile([P, 256], BF16, name="sraw")
-        nc.sync.dma_start(
-            out=sraw[:].rearrange("p (a g) -> p a g", g=NG),
-            in_=raw_scales.rearrange("(a p) g -> p a g", p=P),
-        )
-        for m in range(2):
-            load_x(m)
-        for a in range(2):
-            load_w(a)
-        for m in range(2, 4):
-            load_x(m)
-        for a in range(2, 8):
-            load_w(a)
-
-        rows = {}
-
-        def chain(h):
-            v = sraw[:, h * P : (h + 1) * P]
-
-            def f32_tile(name):
-                t = chn.tile([P, P], F32, name=name)
-                return t
-
-            absv = f32_tile("absv")
-            nc.scalar.activation(out=absv[:], in_=v, func=ACT.Abs)
-            relu = f32_tile("relu")
-            nc.scalar.activation(out=relu[:], in_=v, func=ACT.Relu)
-            xm = f32_tile("xm")
+        def st_w1(a):
+            t = wsign.tile([P, IN], BF16, name="sg")
             nc.vector.tensor_scalar(
-                out=xm[:], in0=absv[:], scalar1=-LOG2E, scalar2=MAGIC, op0=ALU.mult, op1=ALU.add
+                out=t[:].rearrange("p (u g j) -> p g u j", u=2, g=NG),
+                in0=wr[a][:].rearrange("p (g u j) -> p g u j", g=NG, u=2),
+                scalar1=0.0,
+                scalar2=0.5,
+                op0=ALU.is_ge,
+                op1=ALU.subtract,
             )
-            ni = chn.tile([P, P], I32, name="ni")
-            nc.vector.tensor_scalar(
-                out=ni[:], in0=xm[:], scalar1=MAGIC, scalar2=-120.0, op0=ALU.subtract, op1=ALU.max
-            )
-            p2 = chn.tile([P, P], I32, name="p2")
-            nc.vector.tensor_scalar(
-                out=p2[:], in0=ni[:], scalar1=127.0, scalar2=8388608.0, op0=ALU.add, op1=ALU.mult
-            )
-            r1 = f32_tile("r1")
-            nc.vector.scalar_tensor_tensor(
-                out=r1[:], in0=ni[:], scalar=-LN2_HI, in1=absv[:], op0=ALU.mult, op1=ALU.subtract
-            )
-            rr = f32_tile("rr")
-            nc.vector.scalar_tensor_tensor(
-                out=rr[:], in0=ni[:], scalar=-LN2_LO, in1=r1[:], op0=ALU.mult, op1=ALU.add
-            )
-            th = f32_tile("th")
-            nc.scalar.activation(out=th[:], in_=rr[:], func=ACT.Tanh, scale=0.5)
-            c1 = f32_tile("c1")
-            nc.scalar.activation(out=c1[:], in_=th[:], func=ACT.Identity, scale=-2.0, bias=2.0)
-            a1 = f32_tile("a1")
-            nc.vector.scalar_tensor_tensor(
-                out=a1[:], in0=th[:], scalar=1.0, in1=p2[:].bitcast(F32), op0=ALU.add, op1=ALU.mult
-            )
-            bb = f32_tile("bb")
-            nc.vector.tensor_tensor(out=bb[:], in0=a1[:], in1=c1[:], op=ALU.add)
-            rb = f32_tile("rb")
-            nc.vector.reciprocal(out=rb[:], in_=bb[:])
-            zz = f32_tile("zz")
-            nc.vector.tensor_tensor(out=zz[:], in0=a1[:], in1=rb[:], op=ALU.mult)
-            tt = f32_tile("tt")
-            nc.vector.tensor_tensor(out=tt[:], in0=zz[:], in1=zz[:], op=ALU.mult)
-            pa = f32_tile("pa")
-            nc.vector.tensor_scalar(
-                out=pa[:], in0=tt[:], scalar1=ATANH[4], scalar2=None, op0=ALU.mult
-            )
-            pb = f32_tile("pb")
-            cur, nxt = pa, pb
-            for k in (3, 2, 1, 0):
-                nc.vector.scalar_tensor_tensor(
-                    out=nxt[:], in0=cur[:], scalar=ATANH[k], in1=tt[:], op0=ALU.add, op1=ALU.mult
+            sg[a] = t
+
+        def st_ws(a):
+            stp = ps_s.tile([P, NPASS, P], F32, name="stp")
+            for c in range(NPASS):
+                lo = ((a % 8) * NG + 4 * c) * 32
+                nc.tensor.matmul(
+                    stp[:, c, :],
+                    lhsT=sel[:, lo : lo + P],
+                    rhs=rows[a // 8][:],
+                    start=True,
+                    stop=True,
                 )
-                cur, nxt = nxt, cur
-            nc.vector.scalar_tensor_tensor(
-                out=nxt[:], in0=cur[:], scalar=1.0, in1=zz[:], op0=ALU.add, op1=ALU.mult
-            )
-            sp = f32_tile("sp")
-            nc.vector.scalar_tensor_tensor(
-                out=sp[:], in0=nxt[:], scalar=2.0, in1=relu[:], op0=ALU.mult, op1=ALU.add
-            )
-            st_t = ps_s.tile([P, P], F32, name="stp")
-            nc.tensor.transpose(st_t[:], sp[:], ident_f[:])
-            rw = small.tile([P, P], BF16, name="rows%d" % h)
-            nc.scalar.activation(out=rw[:], in_=st_t[:], func=ACT.Identity, scale=2.0, bias=2e-6)
-            rows[h] = rw
+            stps[("w", a)] = stp
 
-        chain(0)
-
-        def prep_x(m):
-            xp = xwork.tile([P, IN], BF16, name="xp")
-            nc.vector.tensor_copy(
-                out=xp[:].rearrange("p (u g j) -> p g u j", u=2, g=NG),
-                in_=xr[m][:].rearrange("p (g u j) -> p g u j", g=NG, u=2),
-            )
-            if m + 4 < 8:
-                load_x(m + 4)
-            xw = xp[:].bitcast(F32)
-            xg = xwork.tile([P, IN], BF16, name="xg", align_bytes=64)
-            xgw = xg[:].bitcast(F32).rearrange("p (c r u) -> p c r u", c=NPASS, u=2)
-            for cp in range(2):
-                tp = ps_t.tile([P, 2, 2, P], F32, name="tp")
-                for ci in range(2):
-                    c = 2 * cp + ci
-                    for u in range(2):
-                        lo = u * 512 + c * P
-                        nc.tensor.transpose(tp[:, ci, u, :], xw[:, lo : lo + P], ident_f[:])
-                nc.scalar.copy(
-                    out=xgw[:, 2 * cp : 2 * cp + 2, :, :],
-                    in_=tp[:].rearrange("p c u r -> p c r u"),
-                )
-            nc.vector.quantize_mx(
-                out=xc[:, m, :].bitcast(FP8X4), scales=xs[:, m, :], in_=xg[:]
+        def st_w3(a):
+            k = a // 2
+            if k not in st2:
+                t = wwork.tile([P, NPASS, 2, P, 2], BF16, name="st2")
+                st2[k] = t
+            nc.scalar.copy(
+                out=st2[k][:, :, a % 2, :, :],
+                in_=stps[("w", a)][:].unsqueeze(3).to_broadcast([P, NPASS, P, 2]),
             )
 
-        def stage_a(k):
-            s2 = wwork.tile([P, NPASS, 2, P, 2], BF16, name="st2")
-            st2[k] = s2
-            for a2 in range(2):
-                a = 2 * k + a2
-                t = wsign.tile([P, IN], BF16, name="sg")
-                nc.vector.tensor_scalar(
-                    out=t[:].rearrange("p (u g j) -> p g u j", u=2, g=NG),
-                    in0=wr[a][:].rearrange("p (g u j) -> p g u j", g=NG, u=2),
-                    scalar1=0.0,
-                    scalar2=0.5,
-                    op0=ALU.is_ge,
-                    op1=ALU.subtract,
-                )
-                sg[a] = t
-                if a + 8 < 16:
-                    load_w(a + 8)
-                stp = ps_s.tile([P, NPASS, P], F32, name="stp")
-                for c in range(NPASS):
-                    lo = ((a % 8) * NG + 4 * c) * 32
-                    nc.tensor.matmul(
-                        stp[:, c, :],
-                        lhsT=sel[:, lo : lo + P],
-                        rhs=rows[a // 8][:],
-                        start=True,
-                        stop=True,
+        def st_w2(k, c):
+            tp = ps_t.tile([P, 2, 2, P], F32, name="tp")
+            for u in range(2):
+                for a2 in range(2):
+                    lo = u * 512 + c * P
+                    nc.tensor.transpose(
+                        tp[:, u, a2, :], sg[2 * k + a2][:].bitcast(F32)[:, lo : lo + P], ident_f[:]
                     )
-                nc.scalar.copy(
-                    out=s2[:, :, a2, :, :],
-                    in_=stp[:].unsqueeze(3).to_broadcast([P, NPASS, P, 2]),
-                )
+            tps[("w", k, c)] = tp
 
-        def stage_b(k):
-            wg = wwork.tile([P, NPASS, 1024], BF16, name="wg", align_bytes=64)
-            for c in range(NPASS):
-                tp = ps_t.tile([P, 2, 2, P], F32, name="tp")
-                for u in range(2):
-                    for a2 in range(2):
-                        lo = u * 512 + c * P
-                        nc.tensor.transpose(
-                            tp[:, u, a2, :],
-                            sg[2 * k + a2][:].bitcast(F32)[:, lo : lo + P],
-                            ident_f[:],
-                        )
-                nc.vector.tensor_tensor(
-                    out=wg[:, c, :].rearrange("p (o u e) -> p o u e", u=2, e=2),
-                    in0=tp[:].bitcast(BF16).rearrange("p u a (o e) -> p (a o) u e", e=2),
-                    in1=st2[k][:, c]
-                    .rearrange("p a o e -> p (a o) e")
-                    .unsqueeze(2)
-                    .to_broadcast([P, 256, 2, 2]),
-                    op=ALU.mult,
-                )
-            for c in range(NPASS):
-                nc.vector.quantize_mx(
-                    out=wc[k][:, c, :].bitcast(FP8X4), scales=ws[k][:, c, :], in_=wg[:, c, :]
-                )
+        def st_w4(k, c):
+            if k not in wg:
+                t = wwork.tile([P, NPASS, 1024], BF16, name="wg", align_bytes=64)
+                wg[k] = t
+            nc.vector.tensor_tensor(
+                out=wg[k][:, c, :].rearrange("p (o u e) -> p o u e", u=2, e=2),
+                in0=tps[("w", k, c)][:].bitcast(BF16).rearrange("p u a (o e) -> p (a o) u e", e=2),
+                in1=st2[k][:, c]
+                .rearrange("p a o e -> p (a o) e")
+                .unsqueeze(2)
+                .to_broadcast([P, 256, 2, 2]),
+                op=ALU.mult,
+            )
 
-        def stage_m(k, mp):
-            n = k // 2
+        def st_w5(k, c):
+            nc.vector.quantize_mx(
+                out=wc[k][:, c, :].bitcast(FP8X4), scales=ws[k][:, c, :], in_=wg[k][:, c, :]
+            )
+
+        def st_mx(k, mp):
             acc = ps_a.tile([P, 2, 256], F32, name="acc")
             for mi in range(2):
                 m = 2 * mp + mi
@@ -286,54 +379,26 @@ def tile_groupedstelinear_kernel(tc, x, weight_logits, raw_scales, out):
                         start=(c == 0),
                         stop=(c == NPASS - 1),
                     )
+            accs[(k, mp)] = acc
+
+        def st_mc(k, mp):
+            n = k // 2
+            if (n, mp) not in ob:
+                t = obuf.tile([P, 2, 512], F32, name="ob")
+                ob[(n, mp)] = t
             lo = (k % 2) * 256
-            nc.scalar.copy(out=ob[n][:, 2 * mp : 2 * mp + 2, lo : lo + 256], in_=acc[:])
+            nc.scalar.copy(out=ob[(n, mp)][:, :, lo : lo + 256], in_=accs[(k, mp)][:])
 
-        def new_ob(n):
-            t = obuf.tile([P, 8, 512], F32, name="ob")
-            ob[n] = t
-
-        def store(n, mp):
+        def st_st(n, mp):
             nc.sync.dma_start(
-                out=of[:, 2 * mp : 2 * mp + 2, n * 512 : (n + 1) * 512],
-                in_=ob[n][:, 2 * mp : 2 * mp + 2, :],
+                out=of[:, 2 * mp : 2 * mp + 2, n * 512 : (n + 1) * 512], in_=ob[(n, mp)][:]
             )
 
-        new_ob(0)
-        stage_a(0)
-        prep_x(0)
-        prep_x(1)
-        stage_b(0)
-        stage_a(1)
-        prep_x(2)
-        prep_x(3)
-        stage_m(0, 0)
-        stage_m(0, 1)
-        prep_x(4)
-        prep_x(5)
-        stage_b(1)
-        stage_a(2)
-        stage_m(0, 2)
-        stage_m(1, 0)
-        stage_m(1, 1)
-        stage_m(1, 2)
-        prep_x(6)
-        prep_x(7)
-        chain(1)
-        stage_b(2)
-        stage_a(3)
-        stage_m(0, 3)
-        stage_m(1, 3)
-        for mp in range(4):
-            store(0, mp)
-        for k in range(2, 8):
-            if k % 2 == 0:
-                new_ob(k // 2)
-            if k + 1 < 8:
-                stage_b(k + 1)
-            if k + 2 < 8:
-                stage_a(k + 2)
-            for mp in range(4):
-                stage_m(k, mp)
-                if k % 2 == 1:
-                    store(k // 2, mp)
+        stages = {
+            "LDS": st_lds, "C": st_c,
+            "CT": st_ct, "CR": st_cr, "LX": st_lx, "X1": st_x1, "X2": st_x2, "X3": st_x3,
+            "X4": st_x4, "LW": st_lw, "W1": st_w1, "WS": st_ws, "W3": st_w3, "W2": st_w2,
+            "W4": st_w4, "W5": st_w5, "MX": st_mx, "MC": st_mc, "ST": st_st,
+        }
+        for op in ORDER:
+            stages[op[0]](*op[1:])

@@ -32,60 +32,55 @@ ATANH = (
     0.12150466887516932,
 )
 
+X_BY_DMA = (2, 3)
+
 ORDER = (
-    ("LDS",), ("LX", 0), ("LX", 1), ("LX", 2), ("C", "abs", 0), ("C", "relu", 0),
-    ("C", "xm", 0), ("C", "ni", 0), ("LX", 3), ("C", "r1", 0), ("C", "p2", 0), ("X1", 0),
-    ("C", "abs", 1), ("LW", 0), ("C", "rr", 0), ("X2", 0, 0), ("X1", 1), ("C", "th", 0),
-    ("X2", 0, 1), ("X3", 0, 0), ("C", "a1", 0), ("X2", 1, 0), ("C", "xm", 1), ("LX", 4),
-    ("C", "c1", 0), ("X2", 1, 1), ("X1", 2), ("X3", 0, 1), ("C", "bb", 0), ("X3", 1, 0),
-    ("X2", 2, 0), ("X4", 0), ("LW", 1), ("X2", 2, 1), ("X3", 1, 1), ("C", "rb", 0),
-    ("X3", 2, 0), ("LX", 5), ("X3", 2, 1), ("X4", 1), ("LX", 6), ("C", "zz", 0),
-    ("X1", 3), ("C", "tt", 0), ("X2", 3, 0), ("LX", 7), ("X4", 2), ("X2", 3, 1),
-    ("X3", 3, 0), ("C", "pa", 0), ("X1", 4), ("X3", 3, 1), ("LW", 2), ("C", "h3", 0),
-    ("X2", 4, 0), ("W1", 0), ("X2", 4, 1), ("X3", 4, 0), ("LW", 3), ("C", "h2", 0),
-    ("X4", 3), ("X3", 4, 1), ("C", "h1", 0), ("W1", 1), ("LW", 4), ("C", "h0", 0),
-    ("W2", 0, 0), ("X4", 4), ("W2", 0, 1), ("LW", 5), ("W2", 0, 2), ("C", "y2", 0),
-    ("X1", 5), ("W2", 0, 3), ("LW", 6), ("C", "sp", 0), ("C", "ni", 1), ("X1", 6),
-    ("CT", 0), ("C", "relu", 1), ("CR", 0), ("C", "r1", 1), ("WS", 0), ("LW", 7),
-    ("C", "p2", 1), ("WS", 1), ("X1", 7), ("W3", 0), ("C", "rr", 1), ("W1", 2),
-    ("W3", 1), ("WS", 2), ("W1", 3), ("LW", 8), ("W1", 4), ("C", "th", 1),
-    ("WS", 3), ("W3", 2), ("W4", 0, 0), ("LW", 9), ("W4", 0, 1), ("X2", 5, 0),
-    ("C", "c1", 1), ("LW", 10), ("WS", 4), ("W3", 3), ("W5", 0, 0), ("X2", 5, 1),
-    ("W5", 0, 1), ("W4", 0, 2), ("X3", 5, 0), ("WS", 5), ("W4", 0, 3), ("X2", 6, 0),
-    ("X3", 5, 1), ("W5", 0, 2), ("X2", 6, 1), ("X3", 6, 0), ("W5", 0, 3), ("X2", 7, 0),
-    ("C", "a1", 1), ("X2", 7, 1), ("X4", 5), ("X3", 6, 1), ("W2", 1, 0), ("C", "bb", 1),
-    ("W3", 4), ("MX", 0, 0), ("X4", 6), ("C", "rb", 1), ("X3", 7, 0), ("MX", 0, 1),
-    ("MC", 0, 0), ("W1", 5), ("X3", 7, 1), ("W2", 1, 1), ("C", "zz", 1), ("LW", 11),
-    ("W4", 1, 0), ("MC", 0, 1), ("W2", 1, 2), ("W2", 1, 3), ("W3", 5), ("C", "tt", 1),
-    ("WS", 6), ("X4", 7), ("W2", 2, 0), ("MX", 0, 2), ("C", "pa", 1), ("W5", 1, 0),
-    ("C", "h3", 1), ("W4", 1, 1), ("MX", 0, 3), ("C", "h2", 1), ("MC", 0, 2), ("W5", 1, 1),
-    ("C", "h1", 1), ("W4", 1, 2), ("W2", 2, 1), ("MC", 0, 3), ("C", "h0", 1), ("WS", 7),
-    ("W5", 1, 2), ("W2", 2, 2), ("C", "y2", 1), ("W4", 1, 3), ("C", "sp", 1), ("W2", 2, 3),
-    ("W3", 6), ("W5", 1, 3), ("W1", 6), ("MX", 1, 0), ("W1", 7), ("W3", 7),
-    ("LW", 12), ("W4", 2, 0), ("MX", 1, 1), ("MC", 1, 0), ("W4", 2, 1), ("LW", 13),
-    ("W5", 2, 0), ("CT", 1), ("MC", 1, 1), ("W2", 3, 0), ("W5", 2, 1), ("ST", 0, 0),
-    ("W2", 3, 1), ("W4", 2, 2), ("CR", 1), ("MX", 1, 2), ("W4", 2, 3), ("ST", 0, 1),
-    ("W5", 2, 2), ("MX", 1, 3), ("W5", 2, 3), ("MC", 1, 2), ("W1", 8), ("ST", 0, 2),
-    ("W1", 9), ("MX", 2, 0), ("MC", 1, 3), ("W4", 3, 0), ("LW", 14), ("W4", 3, 1),
-    ("MX", 2, 1), ("MC", 2, 0), ("W5", 3, 0), ("LW", 15), ("W5", 3, 1), ("MX", 2, 2),
-    ("W1", 10), ("MC", 2, 1), ("W1", 11), ("ST", 0, 3), ("MX", 2, 3), ("MC", 2, 2),
-    ("W2", 3, 2), ("MC", 2, 3), ("W2", 3, 3), ("W4", 3, 2), ("W2", 4, 0), ("W2", 4, 1),
-    ("W4", 3, 3), ("W2", 4, 2), ("WS", 8), ("W5", 3, 2), ("W2", 4, 3), ("W5", 3, 3),
-    ("W3", 8), ("WS", 9), ("W1", 12), ("MX", 3, 0), ("W1", 13), ("W3", 9),
-    ("W1", 14), ("MX", 3, 1), ("W1", 15), ("MC", 3, 0), ("WS", 10), ("W4", 4, 0),
-    ("MC", 3, 1), ("ST", 1, 0), ("WS", 11), ("MX", 3, 2), ("W4", 4, 1), ("W3", 10),
-    ("W5", 4, 0), ("ST", 1, 1), ("W5", 4, 1), ("MX", 3, 3), ("W3", 11), ("W4", 4, 2),
-    ("W4", 4, 3), ("W2", 5, 0), ("MC", 3, 2), ("W5", 4, 2), ("W2", 5, 1), ("W5", 4, 3),
-    ("MC", 3, 3), ("W2", 5, 2), ("ST", 1, 2), ("W4", 5, 0), ("W2", 5, 3), ("WS", 12),
-    ("W4", 5, 1), ("WS", 13), ("W3", 12), ("ST", 1, 3), ("W2", 6, 0), ("W5", 5, 0),
-    ("MX", 4, 0), ("W5", 5, 1), ("W4", 5, 2), ("W3", 13), ("W4", 5, 3), ("MX", 4, 1),
-    ("MC", 4, 0), ("W5", 5, 2), ("W5", 5, 3), ("W2", 6, 1), ("W4", 6, 0), ("MC", 4, 1),
-    ("W2", 6, 2), ("W4", 6, 1), ("W2", 6, 3), ("W2", 7, 0), ("W5", 6, 0), ("W2", 7, 1),
-    ("W5", 6, 1), ("WS", 14), ("W4", 6, 2), ("WS", 15), ("W3", 14), ("MX", 4, 2),
-    ("W4", 6, 3), ("W5", 6, 2), ("W3", 15), ("MX", 4, 3), ("W5", 6, 3), ("MC", 4, 2),
-    ("W2", 7, 2), ("W4", 7, 0), ("MC", 4, 3), ("W2", 7, 3), ("W4", 7, 1), ("MX", 5, 0),
-    ("W5", 7, 0), ("W5", 7, 1), ("W4", 7, 2), ("MX", 5, 1), ("MC", 5, 0), ("W4", 7, 3),
-    ("ST", 2, 0), ("W5", 7, 2), ("MX", 5, 2), ("MC", 5, 1), ("W5", 7, 3), ("ST", 2, 1),
+    ("LDS",), ("LX", 0), ("LX", 1), ("LW", 0), ("C", "abs", 0), ("C", "relu", 0),
+    ("C", "xm", 0), ("LW", 1), ("C", "ni", 0), ("C", "r1", 0), ("C", "p2", 0), ("C", "rr", 0),
+    ("LX", 2), ("C", "abs", 1), ("C", "xm", 1), ("C", "th", 0), ("X1", 0), ("C", "c1", 0),
+    ("LX", 3), ("C", "a1", 0), ("X2", 0, 0), ("C", "ni", 1), ("LW", 2), ("C", "bb", 0),
+    ("X2", 0, 1), ("C", "r1", 1), ("X3", 0, 0), ("X2", 0, 2), ("C", "rb", 0), ("X2", 0, 3),
+    ("LW", 3), ("X3", 0, 1), ("X3", 0, 2), ("C", "rr", 1), ("LX", 4), ("C", "zz", 0),
+    ("X3", 0, 3), ("C", "p2", 1), ("C", "tt", 0), ("C", "th", 1), ("C", "pa", 0), ("C", "c1", 1),
+    ("C", "h3", 0), ("C", "a1", 1), ("C", "h2", 0), ("C", "bb", 1), ("C", "h1", 0), ("C", "rb", 1),
+    ("LX", 5), ("C", "h0", 0), ("C", "y2", 0), ("C", "sp", 0), ("C", "zz", 1), ("CT", 0),
+    ("C", "relu", 1), ("X4", 0), ("CR", 0), ("WS", 0), ("WS", 1), ("W1", 0),
+    ("W3", 0), ("LW", 4), ("X1", 1), ("LW", 5), ("W3", 1), ("W2", 0, 0),
+    ("W2", 0, 1), ("W2", 0, 2), ("LW", 6), ("W1", 1), ("W2", 0, 3), ("WS", 2),
+    ("WS", 3), ("W3", 2), ("LX", 6), ("W4", 0, 0), ("W4", 0, 1), ("W3", 3),
+    ("X2", 1, 0), ("WS", 4), ("W4", 0, 2), ("X2", 1, 1), ("X3", 1, 0), ("W4", 0, 3),
+    ("WS", 5), ("X2", 1, 2), ("X3", 1, 1), ("C", "tt", 1), ("X2", 1, 3), ("W5", 0),
+    ("LX", 7), ("X3", 1, 2), ("W2", 1, 0), ("W2", 1, 1), ("X3", 1, 3), ("W2", 1, 2),
+    ("W4", 1, 0), ("W3", 4), ("MX", 0, 0), ("X4", 1), ("W3", 5), ("W2", 1, 3),
+    ("W4", 1, 1), ("X2", 2, 0), ("LW", 7), ("WS", 6), ("MC", 0, 0), ("MX", 0, 1),
+    ("W4", 1, 2), ("X3", 2, 0), ("LW", 8), ("W4", 1, 3), ("X2", 2, 1), ("MC", 0, 1),
+    ("C", "pa", 1), ("X2", 2, 2), ("W5", 1), ("LW", 9), ("X2", 2, 3), ("X3", 2, 1),
+    ("X2", 3, 0), ("WS", 7), ("X3", 2, 2), ("C", "h3", 1), ("X2", 3, 1), ("W1", 2),
+    ("MX", 1, 0), ("X3", 2, 3), ("X3", 3, 0), ("X4", 2), ("X2", 3, 2), ("X3", 3, 1),
+    ("LW", 10), ("X2", 3, 3), ("MC", 1, 0), ("W2", 2, 0), ("C", "h2", 1), ("W2", 2, 1),
+    ("LW", 11), ("X3", 3, 2), ("W4", 2, 0), ("MX", 0, 2), ("X3", 3, 3), ("C", "h1", 1),
+    ("ST", 0, 0), ("W4", 2, 1), ("W3", 6), ("W2", 2, 2), ("C", "h0", 1), ("W2", 2, 3),
+    ("X4", 3), ("MX", 1, 1), ("MC", 0, 2), ("W3", 7), ("C", "y2", 1), ("MX", 1, 2),
+    ("W4", 2, 2), ("MC", 1, 1), ("C", "sp", 1), ("W4", 2, 3), ("CT", 1), ("MC", 1, 2),
+    ("MX", 0, 3), ("ST", 0, 1), ("W1", 3), ("CR", 1), ("ST", 0, 2), ("WS", 8),
+    ("W5", 2), ("MC", 0, 3), ("WS", 9), ("W2", 3, 0), ("W3", 8), ("W2", 3, 1),
+    ("LW", 12), ("W2", 3, 2), ("W4", 3, 0), ("W2", 3, 3), ("MX", 1, 3), ("W4", 3, 1),
+    ("W3", 9), ("LW", 13), ("W4", 3, 2), ("WS", 10), ("W4", 3, 3), ("MC", 1, 3),
+    ("MX", 2, 0), ("W1", 4), ("ST", 0, 3), ("W3", 10), ("WS", 11), ("MX", 2, 1),
+    ("W5", 3), ("MC", 2, 0), ("LW", 14), ("W2", 4, 0), ("W3", 11), ("W2", 4, 1),
+    ("W1", 5), ("LW", 15), ("W2", 4, 2), ("W2", 4, 3), ("MC", 2, 1), ("WS", 12),
+    ("WS", 13), ("W4", 4, 0), ("MX", 2, 2), ("W4", 4, 1), ("W2", 5, 0), ("W4", 4, 2),
+    ("MC", 2, 2), ("W2", 5, 1), ("W4", 4, 3), ("MX", 2, 3), ("W4", 5, 0), ("W3", 12),
+    ("W2", 5, 2), ("W5", 4), ("W2", 5, 3), ("MC", 2, 3), ("MX", 3, 0), ("W4", 5, 1),
+    ("W3", 13), ("W4", 5, 2), ("WS", 14), ("MX", 3, 1), ("MC", 3, 0), ("W4", 5, 3),
+    ("W1", 6), ("ST", 1, 0), ("WS", 15), ("W3", 14), ("MX", 3, 2), ("W5", 5),
+    ("MC", 3, 1), ("W2", 6, 0), ("W2", 6, 1), ("MC", 3, 2), ("ST", 1, 1), ("W2", 6, 2),
+    ("W4", 6, 0), ("W3", 15), ("W2", 6, 3), ("MX", 3, 3), ("W4", 6, 1), ("ST", 1, 2),
+    ("W4", 6, 2), ("MX", 4, 0), ("W4", 6, 3), ("MC", 3, 3), ("W1", 7), ("ST", 1, 3),
+    ("MX", 4, 1), ("MC", 4, 0), ("W5", 6), ("MX", 4, 2), ("MC", 4, 1), ("W2", 7, 0),
+    ("MC", 4, 2), ("W2", 7, 1), ("W4", 7, 0), ("W2", 7, 2), ("W2", 7, 3), ("W4", 7, 1),
+    ("MX", 4, 3), ("W4", 7, 2), ("MX", 5, 0), ("W4", 7, 3), ("MC", 4, 3), ("W5", 7),
+    ("MX", 5, 1), ("MC", 5, 0), ("ST", 2, 0), ("MX", 5, 2), ("MC", 5, 1), ("ST", 2, 1),
     ("MX", 5, 3), ("MC", 5, 2), ("ST", 2, 2), ("MX", 6, 0), ("MC", 5, 3), ("ST", 2, 3),
     ("MX", 6, 1), ("MC", 6, 0), ("MX", 6, 2), ("MC", 6, 1), ("MX", 6, 3), ("MC", 6, 2),
     ("MX", 7, 0), ("MC", 6, 3), ("MX", 7, 1), ("MC", 7, 0), ("ST", 3, 0), ("MX", 7, 2),
@@ -105,13 +100,13 @@ def tile_groupedstelinear_kernel(tc, x, weight_logits, raw_scales, out):
         small = ctx.enter_context(tc.tile_pool(name="small", bufs=1))
         chn = ctx.enter_context(tc.tile_pool(name="chn", bufs=1))
         keep = ctx.enter_context(tc.tile_pool(name="keep", bufs=1))
-        xraw = ctx.enter_context(tc.tile_pool(name="xraw", bufs=4))
-        xperm = ctx.enter_context(tc.tile_pool(name="xperm", bufs=3))
+        xraw = ctx.enter_context(tc.tile_pool(name="xraw", bufs=2))
+        xperm = ctx.enter_context(tc.tile_pool(name="xperm", bufs=2))
         xgrp = ctx.enter_context(tc.tile_pool(name="xgrp", bufs=2))
-        wraw = ctx.enter_context(tc.tile_pool(name="wraw", bufs=6))
-        wsign = ctx.enter_context(tc.tile_pool(name="wsign", bufs=6))
+        wraw = ctx.enter_context(tc.tile_pool(name="wraw", bufs=3))
+        wsign = ctx.enter_context(tc.tile_pool(name="wsign", bufs=2))
         wwork = ctx.enter_context(tc.tile_pool(name="wwork", bufs=2))
-        obuf = ctx.enter_context(tc.tile_pool(name="obuf", bufs=8))
+        obuf = ctx.enter_context(tc.tile_pool(name="obuf", bufs=6))
         ps_t = ctx.enter_context(tc.psum_pool(name="ps_t", bufs=4))
         ps_s = ctx.enter_context(tc.psum_pool(name="ps_s", bufs=2))
         ps_a = ctx.enter_context(tc.psum_pool(name="ps_a", bufs=2))
@@ -260,58 +255,74 @@ def tile_groupedstelinear_kernel(tc, x, weight_logits, raw_scales, out):
             rows[h] = rw
 
         def st_lx(m):
-            t = xraw.tile([P, IN], BF16, name="xr")
-            nc.sync.dma_start(out=t[:], in_=xf[m * P : (m + 1) * P, :])
-            xr[m] = t
+            q = m // 2
+            if q not in xr:
+                t = xraw.tile([P, 2 * IN], BF16, name="xr")
+                xr[q] = t
+            rows_m = xf[m * P : (m + 1) * P, :]
+            if q in X_BY_DMA:
+                src = rows_m.rearrange("p (g u j) -> p g u j", g=NG, u=2)
+                dst = xr[q][:].rearrange("p (u m g j) -> p u m g j", u=2, m=2, g=NG)
+                for u in range(2):
+                    nc.sync.dma_start(out=dst[:, u, m % 2, :, :], in_=src[:, :, u, :])
+                xp[q] = xr[q]
+            else:
+                lo = (m % 2) * IN
+                nc.sync.dma_start(out=xr[q][:, lo : lo + IN], in_=rows_m)
 
-        def st_x1(m):
-            t = xperm.tile([P, IN], BF16, name="xp")
+        def st_x1(q):
+            t = xperm.tile([P, 2 * IN], BF16, name="xp")
             nc.vector.tensor_copy(
-                out=t[:].rearrange("p (u g j) -> p g u j", u=2, g=NG),
-                in_=xr[m][:].rearrange("p (g u j) -> p g u j", g=NG, u=2),
+                out=t[:].rearrange("p (u g j) -> p g u j", u=2, g=2 * NG),
+                in_=xr[q][:].rearrange("p (g u j) -> p g u j", g=2 * NG, u=2),
             )
-            xp[m] = t
+            xp[q] = t
 
-        def st_x2(m, cp):
-            xw = xp[m][:].bitcast(F32)
+        def st_x2(q, b):
+            xw = xp[q][:].bitcast(F32)
             tp = ps_t.tile([P, 2, 2, P], F32, name="tp")
             for ci in range(2):
                 for u in range(2):
-                    lo = u * 512 + (2 * cp + ci) * P
+                    lo = u * 1024 + (b // 2) * 512 + (2 * (b % 2) + ci) * P
                     nc.tensor.transpose(tp[:, ci, u, :], xw[:, lo : lo + P], ident_f[:])
-            tps[("x", m, cp)] = tp
+            tps[("x", q, b)] = tp
 
-        def st_x3(m, cp):
-            if m not in xg:
-                t = xgrp.tile([P, IN], BF16, name="xg", align_bytes=64)
-                xg[m] = t
-            xgw = xg[m][:].bitcast(F32).rearrange("p (c r u) -> p c r u", c=NPASS, u=2)
+        def st_x3(q, b):
+            if q not in xg:
+                t = xgrp.tile([P, 2 * IN], BF16, name="xg", align_bytes=64)
+                xg[q] = t
+            xgw = xg[q][:].bitcast(F32).rearrange("p (c r u) -> p c r u", c=2 * NPASS, u=2)
             nc.scalar.copy(
-                out=xgw[:, 2 * cp : 2 * cp + 2, :, :],
-                in_=tps[("x", m, cp)][:].rearrange("p c u r -> p c r u"),
+                out=xgw[:, 2 * b : 2 * b + 2, :, :],
+                in_=tps[("x", q, b)][:].rearrange("p c u r -> p c r u"),
             )
 
-        def st_x4(m):
+        def st_x4(q):
             nc.vector.quantize_mx(
-                out=xc[:, m, :].bitcast(FP8X4), scales=xs[:, m, :], in_=xg[m][:]
+                out=xc[:, 2 * q : 2 * q + 2, :].rearrange("p a b -> p (a b)").bitcast(FP8X4),
+                scales=xs[:, 2 * q : 2 * q + 2, :].rearrange("p a b -> p (a b)"),
+                in_=xg[q][:],
             )
 
         def st_lw(a):
-            t = wraw.tile([P, IN], BF16, name="wr")
-            nc.sync.dma_start(out=t[:], in_=wl[a * P : (a + 1) * P, :])
-            wr[a] = t
+            k = a // 2
+            if k not in wr:
+                t = wraw.tile([P, 2 * IN], BF16, name="wr")
+                wr[k] = t
+            lo = (a % 2) * IN
+            nc.sync.dma_start(out=wr[k][:, lo : lo + IN], in_=wl[a * P : (a + 1) * P, :])
 
-        def st_w1(a):
-            t = wsign.tile([P, IN], BF16, name="sg")
+        def st_w1(k):
+            t = wsign.tile([P, 2 * IN], BF16, name="sg")
             nc.vector.tensor_scalar(
-                out=t[:].rearrange("p (u g j) -> p g u j", u=2, g=NG),
-                in0=wr[a][:].rearrange("p (g u j) -> p g u j", g=NG, u=2),
+                out=t[:].rearrange("p (u g j) -> p g u j", u=2, g=2 * NG),
+                in0=wr[k][:].rearrange("p (g u j) -> p g u j", g=2 * NG, u=2),
                 scalar1=0.0,
                 scalar2=0.5,
                 op0=ALU.is_ge,
                 op1=ALU.subtract,
             )
-            sg[a] = t
+            sg[k] = t
 
         def st_ws(a):
             stp = ps_s.tile([P, NPASS, P], F32, name="stp")
@@ -338,12 +349,11 @@ def tile_groupedstelinear_kernel(tc, x, weight_logits, raw_scales, out):
 
         def st_w2(k, c):
             tp = ps_t.tile([P, 2, 2, P], F32, name="tp")
+            sgw = sg[k][:].bitcast(F32)
             for u in range(2):
                 for a2 in range(2):
-                    lo = u * 512 + c * P
-                    nc.tensor.transpose(
-                        tp[:, u, a2, :], sg[2 * k + a2][:].bitcast(F32)[:, lo : lo + P], ident_f[:]
-                    )
+                    lo = u * 1024 + a2 * 512 + c * P
+                    nc.tensor.transpose(tp[:, u, a2, :], sgw[:, lo : lo + P], ident_f[:])
             tps[("w", k, c)] = tp
 
         def st_w4(k, c):
@@ -360,9 +370,11 @@ def tile_groupedstelinear_kernel(tc, x, weight_logits, raw_scales, out):
                 op=ALU.mult,
             )
 
-        def st_w5(k, c):
+        def st_w5(k):
             nc.vector.quantize_mx(
-                out=wc[k][:, c, :].bitcast(FP8X4), scales=ws[k][:, c, :], in_=wg[k][:, c, :]
+                out=wc[k][:].rearrange("p c o -> p (c o)").bitcast(FP8X4),
+                scales=ws[k][:].rearrange("p c o -> p (c o)"),
+                in_=wg[k][:].rearrange("p c o -> p (c o)"),
             )
 
         def st_mx(k, mp):

@@ -24,68 +24,56 @@ LOG2E = 1.4426950408889634
 MAGIC = 12582912.0
 LN2_HI = 0.693145751953125
 LN2_LO = 1.4286068203094172e-06
-ATANH = (
-    0.3333333781096117,
-    0.19999438873142902,
-    0.14308442370236296,
-    0.10713829121815853,
-    0.12150466887516932,
-)
-
 X_BY_DMA = (2, 3)
 
 ORDER = (
-    ("LDS",), ("LX", 0), ("LX", 1), ("LW", 0), ("C", "abs", 0), ("C", "relu", 0),
-    ("C", "xm", 0), ("LW", 1), ("C", "ni", 0), ("C", "r1", 0), ("C", "p2", 0), ("C", "rr", 0),
-    ("LX", 2), ("C", "abs", 1), ("C", "xm", 1), ("C", "th", 0), ("X1", 0), ("C", "c1", 0),
-    ("LX", 3), ("C", "a1", 0), ("X2", 0, 0), ("C", "ni", 1), ("LW", 2), ("C", "bb", 0),
-    ("X2", 0, 1), ("C", "r1", 1), ("X3", 0, 0), ("X2", 0, 2), ("C", "rb", 0), ("X2", 0, 3),
-    ("LW", 3), ("X3", 0, 1), ("X3", 0, 2), ("C", "rr", 1), ("LX", 4), ("C", "zz", 0),
-    ("X3", 0, 3), ("C", "p2", 1), ("C", "tt", 0), ("C", "th", 1), ("C", "pa", 0), ("C", "c1", 1),
-    ("C", "h3", 0), ("C", "a1", 1), ("C", "h2", 0), ("C", "bb", 1), ("C", "h1", 0), ("C", "rb", 1),
-    ("LX", 5), ("C", "h0", 0), ("C", "y2", 0), ("C", "sp", 0), ("C", "zz", 1), ("CT", 0),
-    ("C", "relu", 1), ("X4", 0), ("CR", 0), ("WS", 0), ("WS", 1), ("W1", 0),
-    ("W3", 0), ("LW", 4), ("X1", 1), ("LW", 5), ("W3", 1), ("W2", 0, 0),
-    ("W2", 0, 1), ("W2", 0, 2), ("LW", 6), ("W1", 1), ("W2", 0, 3), ("WS", 2),
-    ("WS", 3), ("W3", 2), ("LX", 6), ("W4", 0, 0), ("W4", 0, 1), ("W3", 3),
-    ("X2", 1, 0), ("WS", 4), ("W4", 0, 2), ("X2", 1, 1), ("X3", 1, 0), ("W4", 0, 3),
-    ("WS", 5), ("X2", 1, 2), ("X3", 1, 1), ("C", "tt", 1), ("X2", 1, 3), ("W5", 0),
-    ("LX", 7), ("X3", 1, 2), ("W2", 1, 0), ("W2", 1, 1), ("X3", 1, 3), ("W2", 1, 2),
-    ("W4", 1, 0), ("W3", 4), ("MX", 0, 0), ("X4", 1), ("W3", 5), ("W2", 1, 3),
-    ("W4", 1, 1), ("X2", 2, 0), ("LW", 7), ("WS", 6), ("MC", 0, 0), ("MX", 0, 1),
-    ("W4", 1, 2), ("X3", 2, 0), ("LW", 8), ("W4", 1, 3), ("X2", 2, 1), ("MC", 0, 1),
-    ("C", "pa", 1), ("X2", 2, 2), ("W5", 1), ("LW", 9), ("X2", 2, 3), ("X3", 2, 1),
-    ("X2", 3, 0), ("WS", 7), ("X3", 2, 2), ("C", "h3", 1), ("X2", 3, 1), ("W1", 2),
-    ("MX", 1, 0), ("X3", 2, 3), ("X3", 3, 0), ("X4", 2), ("X2", 3, 2), ("X3", 3, 1),
-    ("LW", 10), ("X2", 3, 3), ("MC", 1, 0), ("W2", 2, 0), ("C", "h2", 1), ("W2", 2, 1),
-    ("LW", 11), ("X3", 3, 2), ("W4", 2, 0), ("MX", 0, 2), ("X3", 3, 3), ("C", "h1", 1),
-    ("ST", 0, 0), ("W4", 2, 1), ("W3", 6), ("W2", 2, 2), ("C", "h0", 1), ("W2", 2, 3),
-    ("X4", 3), ("MX", 1, 1), ("MC", 0, 2), ("W3", 7), ("C", "y2", 1), ("MX", 1, 2),
-    ("W4", 2, 2), ("MC", 1, 1), ("C", "sp", 1), ("W4", 2, 3), ("CT", 1), ("MC", 1, 2),
-    ("MX", 0, 3), ("ST", 0, 1), ("W1", 3), ("CR", 1), ("ST", 0, 2), ("WS", 8),
-    ("W5", 2), ("MC", 0, 3), ("WS", 9), ("W2", 3, 0), ("W3", 8), ("W2", 3, 1),
-    ("LW", 12), ("W2", 3, 2), ("W4", 3, 0), ("W2", 3, 3), ("MX", 1, 3), ("W4", 3, 1),
-    ("W3", 9), ("LW", 13), ("W4", 3, 2), ("WS", 10), ("W4", 3, 3), ("MC", 1, 3),
-    ("MX", 2, 0), ("W1", 4), ("ST", 0, 3), ("W3", 10), ("WS", 11), ("MX", 2, 1),
-    ("W5", 3), ("MC", 2, 0), ("LW", 14), ("W2", 4, 0), ("W3", 11), ("W2", 4, 1),
-    ("W1", 5), ("LW", 15), ("W2", 4, 2), ("W2", 4, 3), ("MC", 2, 1), ("WS", 12),
-    ("WS", 13), ("W4", 4, 0), ("MX", 2, 2), ("W4", 4, 1), ("W2", 5, 0), ("W4", 4, 2),
-    ("MC", 2, 2), ("W2", 5, 1), ("W4", 4, 3), ("MX", 2, 3), ("W4", 5, 0), ("W3", 12),
-    ("W2", 5, 2), ("W5", 4), ("W2", 5, 3), ("MC", 2, 3), ("MX", 3, 0), ("W4", 5, 1),
-    ("W3", 13), ("W4", 5, 2), ("WS", 14), ("MX", 3, 1), ("MC", 3, 0), ("W4", 5, 3),
-    ("W1", 6), ("ST", 1, 0), ("WS", 15), ("W3", 14), ("MX", 3, 2), ("W5", 5),
-    ("MC", 3, 1), ("W2", 6, 0), ("W2", 6, 1), ("MC", 3, 2), ("ST", 1, 1), ("W2", 6, 2),
-    ("W4", 6, 0), ("W3", 15), ("W2", 6, 3), ("MX", 3, 3), ("W4", 6, 1), ("ST", 1, 2),
-    ("W4", 6, 2), ("MX", 4, 0), ("W4", 6, 3), ("MC", 3, 3), ("W1", 7), ("ST", 1, 3),
-    ("MX", 4, 1), ("MC", 4, 0), ("W5", 6), ("MX", 4, 2), ("MC", 4, 1), ("W2", 7, 0),
-    ("MC", 4, 2), ("W2", 7, 1), ("W4", 7, 0), ("W2", 7, 2), ("W2", 7, 3), ("W4", 7, 1),
-    ("MX", 4, 3), ("W4", 7, 2), ("MX", 5, 0), ("W4", 7, 3), ("MC", 4, 3), ("W5", 7),
-    ("MX", 5, 1), ("MC", 5, 0), ("ST", 2, 0), ("MX", 5, 2), ("MC", 5, 1), ("ST", 2, 1),
-    ("MX", 5, 3), ("MC", 5, 2), ("ST", 2, 2), ("MX", 6, 0), ("MC", 5, 3), ("ST", 2, 3),
-    ("MX", 6, 1), ("MC", 6, 0), ("MX", 6, 2), ("MC", 6, 1), ("MX", 6, 3), ("MC", 6, 2),
-    ("MX", 7, 0), ("MC", 6, 3), ("MX", 7, 1), ("MC", 7, 0), ("ST", 3, 0), ("MX", 7, 2),
-    ("MC", 7, 1), ("ST", 3, 1), ("MX", 7, 3), ("MC", 7, 2), ("ST", 3, 2), ("MC", 7, 3),
-    ("ST", 3, 3),
+    ("LDS",), ("LX", 0), ("LX", 1), ("LX", 2), ("C", "abs"), ("LX", 3),
+    ("C", "e0"), ("C", "xm"), ("C", "y0"), ("C", "ni"), ("C", "r1"), ("LW", 0),
+    ("C", "p2"), ("C", "rr"), ("X1", 0), ("LW", 1), ("C", "th"), ("LW", 2),
+    ("X2", 0, 0), ("X2", 0, 1), ("X1", 1), ("X2", 0, 2), ("LX", 4), ("X2", 0, 3),
+    ("X3", 0, 0), ("C", "a1"), ("C", "c1"), ("X2", 1, 0), ("X3", 0, 1), ("C", "bb"),
+    ("C", "t2"), ("W1", 0), ("X2", 1, 1), ("X3", 0, 2), ("C", "rx"), ("X2", 1, 2),
+    ("C", "mm"), ("X3", 0, 3), ("LX", 5), ("C", "rs"), ("C", "xx"), ("X2", 1, 3),
+    ("X4", 0), ("X3", 1, 0), ("C", "x1"), ("W2", 0, 0), ("X3", 1, 1), ("C", "g4"),
+    ("C", "relu"), ("C", "cr"), ("W2", 0, 1), ("X3", 1, 2), ("C", "yr"), ("X3", 1, 3),
+    ("LW", 3), ("C", "sp"), ("W2", 0, 2), ("W2", 0, 3), ("X4", 1), ("LX", 6),
+    ("CT", 0), ("CT", 1), ("CR", 0), ("CR", 1), ("WS", 0), ("WS", 1),
+    ("W3", 0), ("W3", 1), ("W1", 1), ("WS", 2), ("LX", 7), ("W3", 2),
+    ("WS", 3), ("W4", 0, 0), ("W4", 0, 1), ("W3", 3), ("X2", 2, 0), ("W4", 0, 2),
+    ("WS", 4), ("X2", 2, 1), ("W4", 0, 3), ("X3", 2, 0), ("X2", 2, 2), ("LW", 4),
+    ("WS", 5), ("X3", 2, 1), ("W5", 0), ("X2", 2, 3), ("X3", 2, 2), ("W2", 1, 0),
+    ("LW", 5), ("W2", 1, 1), ("X3", 2, 3), ("W4", 1, 0), ("W2", 1, 2), ("W3", 4),
+    ("MX", 0, 0), ("LW", 6), ("W4", 1, 1), ("X4", 2), ("W3", 5), ("LW", 7),
+    ("MX", 0, 1), ("W4", 1, 2), ("MC", 0, 0), ("LW", 8), ("W2", 1, 3), ("MC", 0, 1),
+    ("X2", 3, 0), ("W1", 2), ("X2", 3, 1), ("LW", 9), ("X3", 3, 0), ("X2", 3, 2),
+    ("WS", 6), ("W4", 1, 3), ("X3", 3, 1), ("WS", 7), ("MX", 0, 2), ("LW", 10),
+    ("X3", 3, 2), ("W5", 1), ("W3", 6), ("LW", 11), ("X2", 3, 3), ("W2", 2, 0),
+    ("W1", 3), ("W2", 2, 1), ("MC", 0, 2), ("W2", 2, 2), ("WS", 8), ("X3", 3, 3),
+    ("W4", 2, 0), ("MX", 1, 0), ("LW", 12), ("W3", 7), ("W4", 2, 1), ("MX", 1, 1),
+    ("X4", 3), ("LW", 13), ("MC", 1, 0), ("W2", 2, 3), ("W4", 2, 2), ("ST", 0, 0),
+    ("MC", 1, 1), ("W2", 3, 0), ("W4", 2, 3), ("W2", 3, 1), ("W2", 3, 2), ("ST", 0, 1),
+    ("W1", 4), ("WS", 9), ("MX", 0, 3), ("W3", 8), ("W5", 2), ("MX", 1, 2),
+    ("W3", 9), ("LW", 14), ("W4", 3, 0), ("W2", 3, 3), ("LW", 15), ("MC", 0, 3),
+    ("W4", 3, 1), ("WS", 10), ("MC", 1, 2), ("W2", 4, 0), ("W4", 3, 2), ("WS", 11),
+    ("MX", 1, 3), ("ST", 0, 2), ("W4", 3, 3), ("W1", 5), ("MX", 2, 0), ("W3", 10),
+    ("W5", 3), ("W2", 4, 1), ("MC", 1, 3), ("W2", 4, 2), ("MC", 2, 0), ("W2", 4, 3),
+    ("W4", 4, 0), ("ST", 0, 3), ("WS", 12), ("W3", 11), ("MX", 2, 1), ("W4", 4, 1),
+    ("W4", 4, 2), ("MX", 2, 2), ("MC", 2, 1), ("W4", 4, 3), ("W1", 6), ("W2", 5, 0),
+    ("W3", 12), ("W2", 5, 1), ("W2", 5, 2), ("W5", 4), ("W2", 5, 3), ("MC", 2, 2),
+    ("WS", 13), ("WS", 14), ("MX", 2, 3), ("W3", 13), ("W4", 5, 0), ("W4", 5, 1),
+    ("MX", 3, 0), ("MC", 2, 3), ("W4", 5, 2), ("W4", 5, 3), ("W2", 6, 0), ("MC", 3, 0),
+    ("W2", 6, 1), ("W1", 7), ("W2", 6, 2), ("W3", 14), ("W2", 6, 3), ("ST", 1, 0),
+    ("WS", 15), ("W5", 5), ("MX", 3, 1), ("W3", 15), ("MX", 3, 2), ("W4", 6, 0),
+    ("MC", 3, 1), ("W4", 6, 1), ("W2", 7, 0), ("ST", 1, 1), ("W4", 6, 2), ("MC", 3, 2),
+    ("MX", 3, 3), ("W4", 6, 3), ("ST", 1, 2), ("W4", 7, 0), ("MX", 4, 0), ("W5", 6),
+    ("MC", 3, 3), ("W2", 7, 1), ("ST", 1, 3), ("MC", 4, 0), ("W2", 7, 2), ("W4", 7, 1),
+    ("W2", 7, 3), ("MX", 4, 1), ("W4", 7, 2), ("W4", 7, 3), ("MX", 4, 2), ("MC", 4, 1),
+    ("W5", 7), ("MX", 4, 3), ("MC", 4, 2), ("MX", 5, 0), ("MC", 4, 3), ("MX", 5, 1),
+    ("MC", 5, 0), ("MX", 5, 2), ("ST", 2, 0), ("MC", 5, 1), ("MX", 5, 3), ("ST", 2, 1),
+    ("MC", 5, 2), ("MX", 6, 0), ("ST", 2, 2), ("MC", 5, 3), ("MX", 6, 1), ("ST", 2, 3),
+    ("MC", 6, 0), ("MX", 6, 2), ("MC", 6, 1), ("MX", 6, 3), ("MC", 6, 2), ("MX", 7, 0),
+    ("MC", 6, 3), ("MX", 7, 1), ("MC", 7, 0), ("MX", 7, 2), ("ST", 3, 0), ("MC", 7, 1),
+    ("MX", 7, 3), ("ST", 3, 1), ("MC", 7, 2), ("ST", 3, 2), ("MC", 7, 3), ("ST", 3, 3),
 )
 
 
@@ -128,7 +116,7 @@ def tile_groupedstelinear_kernel(tc, x, weight_logits, raw_scales, out):
         warm = small.tile([P, 1], F32, name="warm")
         nc.vector.memset(warm[:], 0.0)
         warm2 = small.tile([P, 1], F32, name="warm2")
-        nc.scalar.activation(out=warm2[:], in_=warm[:], func=ACT.Tanh)
+        nc.scalar.activation(out=warm2[:], in_=warm[:], func=ACT.Exp)
 
         xc = keep.tile([P, 8, 512], U32, name="xc", align_bytes=64)
         xs = keep.tile([P, 8, 512], U8, name="xs", align_bytes=64)
@@ -161,90 +149,80 @@ def tile_groupedstelinear_kernel(tc, x, weight_logits, raw_scales, out):
                 in_=raw_scales.rearrange("(a p) g -> p a g", p=P),
             )
 
-        def cht(h, name, dtype=F32):
-            t = chn.tile([P, P], dtype, name=name)
-            ch[(h, name)] = t
+        slot_of = {"a1": "xm", "bb": "r1", "mm": "e0", "cr": "xx"}
+
+        def cht(name, dtype=F32):
+            t = chn.tile([P, 256], dtype, name=slot_of.get(name, name))
+            ch[name] = t
             return t
 
-        def stt(h, dst, in0, scalar, in1, op0, op1, dtype=F32):
+        def act(dst, src, func, scale=1.0, bias=0.0):
+            nc.scalar.activation(out=cht(dst)[:], in_=src, func=func, scale=scale, bias=bias)
+
+        def stt(dst, in0, scalar, in1, op0, op1):
             nc.vector.scalar_tensor_tensor(
-                out=cht(h, dst, dtype)[:] if (h, dst) not in ch else ch[(h, dst)][:],
-                in0=ch[(h, in0)][:],
-                scalar=scalar,
-                in1=in1,
-                op0=op0,
-                op1=op1,
+                out=cht(dst)[:], in0=ch[in0][:], scalar=scalar, in1=in1, op0=op0, op1=op1
             )
 
-        def tsc(h, dst, in0, s1, s2, op0, op1, dtype=F32):
+        def tsc(dst, in0, s1, s2, op0, op1, dtype=F32):
             nc.vector.tensor_scalar(
-                out=cht(h, dst, dtype)[:], in0=ch[(h, in0)][:], scalar1=s1, scalar2=s2, op0=op0, op1=op1
+                out=cht(dst, dtype)[:], in0=ch[in0][:], scalar1=s1, scalar2=s2, op0=op0, op1=op1
             )
 
-        def st_c(name, h):
-            v = sraw[:, h * P : (h + 1) * P]
+        def ttt(dst, in0, in1, op):
+            nc.vector.tensor_tensor(out=cht(dst)[:], in0=ch[in0][:], in1=ch[in1][:], op=op)
+
+        def st_c(name):
             if name == "abs":
-                nc.scalar.activation(out=cht(h, "abs")[:], in_=v, func=ACT.Abs)
+                act("abs", sraw[:], ACT.Abs)
             elif name == "relu":
-                nc.scalar.activation(out=cht(h, "relu")[:], in_=v, func=ACT.Relu)
+                act("relu", sraw[:], ACT.Relu)
+            elif name == "e0":
+                act("e0", ch["abs"][:], ACT.Exp, scale=-1.0)
+            elif name == "y0":
+                act("y0", ch["e0"][:], ACT.Ln, bias=1.0)
             elif name == "xm":
-                tsc(h, "xm", "abs", -LOG2E, MAGIC, ALU.mult, ALU.add)
+                tsc("xm", "abs", -LOG2E, MAGIC, ALU.mult, ALU.add)
             elif name == "ni":
-                tsc(h, "ni", "xm", MAGIC, -120.0, ALU.subtract, ALU.max, I32)
+                tsc("ni", "xm", MAGIC, -120.0, ALU.subtract, ALU.max, I32)
             elif name == "r1":
-                stt(h, "r1", "ni", -LN2_HI, ch[(h, "abs")][:], ALU.mult, ALU.subtract)
+                stt("r1", "ni", -LN2_HI, ch["abs"][:], ALU.mult, ALU.subtract)
             elif name == "rr":
-                stt(h, "rr", "ni", -LN2_LO, ch[(h, "r1")][:], ALU.mult, ALU.add)
+                stt("rr", "ni", -LN2_LO, ch["r1"][:], ALU.mult, ALU.add)
             elif name == "p2":
-                tsc(h, "p2", "ni", 127.0, 8388608.0, ALU.add, ALU.mult, I32)
+                tsc("p2", "ni", 127.0, 8388608.0, ALU.add, ALU.mult, I32)
             elif name == "th":
-                nc.scalar.activation(
-                    out=cht(h, "th")[:], in_=ch[(h, "rr")][:], func=ACT.Tanh, scale=0.5
-                )
+                act("th", ch["rr"][:], ACT.Tanh, scale=0.5)
             elif name == "c1":
-                nc.scalar.activation(
-                    out=cht(h, "c1")[:], in_=ch[(h, "th")][:], func=ACT.Identity, scale=-2.0, bias=2.0
-                )
+                act("c1", ch["th"][:], ACT.Identity, scale=-2.0, bias=2.0)
+            elif name == "t2":
+                act("t2", ch["y0"][:], ACT.Tanh, scale=0.5)
+            elif name == "rx":
+                act("rx", ch["rr"][:], ACT.Exp)
+            elif name == "xx":
+                act("xx", ch["y0"][:], ACT.Exp, scale=-1.0)
+            elif name == "x1":
+                act("x1", ch["xx"][:], ACT.Identity, bias=1.0)
             elif name == "a1":
-                stt(h, "a1", "th", 1.0, ch[(h, "p2")][:].bitcast(F32), ALU.add, ALU.mult)
+                stt("a1", "th", 1.0, ch["p2"][:].bitcast(F32), ALU.add, ALU.mult)
             elif name == "bb":
-                nc.vector.tensor_tensor(
-                    out=cht(h, "bb")[:], in0=ch[(h, "a1")][:], in1=ch[(h, "c1")][:], op=ALU.add
-                )
-            elif name == "rb":
-                nc.vector.reciprocal(out=cht(h, "rb")[:], in_=ch[(h, "bb")][:])
-            elif name == "zz":
-                nc.vector.tensor_tensor(
-                    out=cht(h, "zz")[:], in0=ch[(h, "a1")][:], in1=ch[(h, "rb")][:], op=ALU.mult
-                )
-            elif name == "tt":
-                nc.vector.tensor_tensor(
-                    out=cht(h, "tt")[:], in0=ch[(h, "zz")][:], in1=ch[(h, "zz")][:], op=ALU.mult
-                )
-            elif name == "pa":
-                nc.vector.tensor_scalar(
-                    out=cht(h, "pa")[:],
-                    in0=ch[(h, "tt")][:],
-                    scalar1=ATANH[4],
-                    scalar2=None,
-                    op0=ALU.mult,
-                )
-            elif name == "h3":
-                stt(h, "pb", "pa", ATANH[3], ch[(h, "tt")][:], ALU.add, ALU.mult)
-            elif name == "h2":
-                stt(h, "pa", "pb", ATANH[2], ch[(h, "tt")][:], ALU.add, ALU.mult)
-            elif name == "h1":
-                stt(h, "pb", "pa", ATANH[1], ch[(h, "tt")][:], ALU.add, ALU.mult)
-            elif name == "h0":
-                stt(h, "pa", "pb", ATANH[0], ch[(h, "tt")][:], ALU.add, ALU.mult)
-            elif name == "y2":
-                stt(h, "pb", "pa", 1.0, ch[(h, "zz")][:], ALU.add, ALU.mult)
+                ttt("bb", "a1", "c1", ALU.add)
+            elif name == "mm":
+                ttt("mm", "bb", "t2", ALU.mult)
+            elif name == "rs":
+                ttt("rs", "mm", "a1", ALU.subtract)
+            elif name == "g4":
+                stt("g4", "rx", 1.0, ch["x1"][:], ALU.add, ALU.mult)
+            elif name == "yr":
+                ttt("yr", "y0", "relu", ALU.add)
+            elif name == "cr":
+                ttt("cr", "rs", "g4", ALU.mult)
             else:
-                stt(h, "sp", "pb", 2.0, ch[(h, "relu")][:], ALU.mult, ALU.add)
+                stt("sp", "cr", -0.25, ch["yr"][:], ALU.mult, ALU.add)
 
         def st_ct(h):
             t = ps_s.tile([P, P], F32, name="stp")
-            nc.tensor.transpose(t[:], ch[(h, "sp")][:], ident_f[:])
+            nc.tensor.transpose(t[:], ch["sp"][:, h * P : (h + 1) * P], ident_f[:])
             stps[("c", h)] = t
 
         def st_cr(h):
@@ -273,8 +251,8 @@ def tile_groupedstelinear_kernel(tc, x, weight_logits, raw_scales, out):
         def st_x1(q):
             t = xperm.tile([P, 2 * IN], BF16, name="xp")
             nc.vector.tensor_copy(
-                out=t[:].rearrange("p (u g j) -> p g u j", u=2, g=2 * NG),
-                in_=xr[q][:].rearrange("p (g u j) -> p g u j", g=2 * NG, u=2),
+                out=t[:].rearrange("p (u g j) -> p u g j", u=2, g=2 * NG),
+                in_=xr[q][:].rearrange("p (g u j) -> p u g j", g=2 * NG, u=2),
             )
             xp[q] = t
 
@@ -315,8 +293,8 @@ def tile_groupedstelinear_kernel(tc, x, weight_logits, raw_scales, out):
         def st_w1(k):
             t = wsign.tile([P, 2 * IN], BF16, name="sg")
             nc.vector.tensor_scalar(
-                out=t[:].rearrange("p (u g j) -> p g u j", u=2, g=2 * NG),
-                in0=wr[k][:].rearrange("p (g u j) -> p g u j", g=2 * NG, u=2),
+                out=t[:].rearrange("p (u g j) -> p u g j", u=2, g=2 * NG),
+                in0=wr[k][:].rearrange("p (g u j) -> p u g j", g=2 * NG, u=2),
                 scalar1=0.0,
                 scalar2=0.5,
                 op0=ALU.is_ge,

@@ -18,63 +18,14 @@ IN = 2048
 OUT = 2048
 NG = 16
 NPASS = 4
+NK = 8
+NQ = 4
 FLOPS = 2 * TOK * IN * OUT
 
 LOG2E = 1.4426950408889634
 MAGIC = 12582912.0
 LN2_HI = 0.693145751953125
 LN2_LO = 1.4286068203094172e-06
-X_BY_DMA = (2, 3)
-
-ORDER = (
-    ("LDS",), ("LX", 0), ("LX", 1), ("LX", 2), ("C", "abs"), ("LX", 3),
-    ("C", "e0"), ("C", "xm"), ("C", "y0"), ("C", "ni"), ("C", "r1"), ("LW", 0),
-    ("C", "p2"), ("C", "rr"), ("X1", 0), ("LW", 1), ("C", "th"), ("LW", 2),
-    ("X2", 0, 0), ("X2", 0, 1), ("X1", 1), ("X2", 0, 2), ("LX", 4), ("X2", 0, 3),
-    ("X3", 0, 0), ("C", "a1"), ("C", "c1"), ("X2", 1, 0), ("X3", 0, 1), ("C", "bb"),
-    ("C", "t2"), ("W1", 0), ("X2", 1, 1), ("X3", 0, 2), ("C", "rx"), ("X2", 1, 2),
-    ("C", "mm"), ("X3", 0, 3), ("LX", 5), ("C", "rs"), ("C", "xx"), ("X2", 1, 3),
-    ("X4", 0), ("X3", 1, 0), ("C", "x1"), ("W2", 0, 0), ("X3", 1, 1), ("C", "g4"),
-    ("C", "relu"), ("C", "cr"), ("W2", 0, 1), ("X3", 1, 2), ("C", "yr"), ("X3", 1, 3),
-    ("LW", 3), ("C", "sp"), ("W2", 0, 2), ("W2", 0, 3), ("X4", 1), ("LX", 6),
-    ("CT", 0), ("CT", 1), ("CR", 0), ("CR", 1), ("WS", 0), ("WS", 1),
-    ("W3", 0), ("W3", 1), ("W1", 1), ("WS", 2), ("LX", 7), ("W3", 2),
-    ("WS", 3), ("W4", 0, 0), ("W4", 0, 1), ("W3", 3), ("X2", 2, 0), ("W4", 0, 2),
-    ("WS", 4), ("X2", 2, 1), ("W4", 0, 3), ("X3", 2, 0), ("X2", 2, 2), ("LW", 4),
-    ("WS", 5), ("X3", 2, 1), ("W5", 0), ("X2", 2, 3), ("X3", 2, 2), ("W2", 1, 0),
-    ("LW", 5), ("W2", 1, 1), ("X3", 2, 3), ("W4", 1, 0), ("W2", 1, 2), ("W3", 4),
-    ("MX", 0, 0), ("LW", 6), ("W4", 1, 1), ("X4", 2), ("W3", 5), ("LW", 7),
-    ("MX", 0, 1), ("W4", 1, 2), ("MC", 0, 0), ("LW", 8), ("W2", 1, 3), ("MC", 0, 1),
-    ("X2", 3, 0), ("W1", 2), ("X2", 3, 1), ("LW", 9), ("X3", 3, 0), ("X2", 3, 2),
-    ("WS", 6), ("W4", 1, 3), ("X3", 3, 1), ("WS", 7), ("MX", 0, 2), ("LW", 10),
-    ("X3", 3, 2), ("W5", 1), ("W3", 6), ("LW", 11), ("X2", 3, 3), ("W2", 2, 0),
-    ("W1", 3), ("W2", 2, 1), ("MC", 0, 2), ("W2", 2, 2), ("WS", 8), ("X3", 3, 3),
-    ("W4", 2, 0), ("MX", 1, 0), ("LW", 12), ("W3", 7), ("W4", 2, 1), ("MX", 1, 1),
-    ("X4", 3), ("LW", 13), ("MC", 1, 0), ("W2", 2, 3), ("W4", 2, 2), ("ST", 0, 0),
-    ("MC", 1, 1), ("W2", 3, 0), ("W4", 2, 3), ("W2", 3, 1), ("W2", 3, 2), ("ST", 0, 1),
-    ("W1", 4), ("WS", 9), ("MX", 0, 3), ("W3", 8), ("W5", 2), ("MX", 1, 2),
-    ("W3", 9), ("LW", 14), ("W4", 3, 0), ("W2", 3, 3), ("LW", 15), ("MC", 0, 3),
-    ("W4", 3, 1), ("WS", 10), ("MC", 1, 2), ("W2", 4, 0), ("W4", 3, 2), ("WS", 11),
-    ("MX", 1, 3), ("ST", 0, 2), ("W4", 3, 3), ("W1", 5), ("MX", 2, 0), ("W3", 10),
-    ("W5", 3), ("W2", 4, 1), ("MC", 1, 3), ("W2", 4, 2), ("MC", 2, 0), ("W2", 4, 3),
-    ("W4", 4, 0), ("ST", 0, 3), ("WS", 12), ("W3", 11), ("MX", 2, 1), ("W4", 4, 1),
-    ("W4", 4, 2), ("MX", 2, 2), ("MC", 2, 1), ("W4", 4, 3), ("W1", 6), ("W2", 5, 0),
-    ("W3", 12), ("W2", 5, 1), ("W2", 5, 2), ("W5", 4), ("W2", 5, 3), ("MC", 2, 2),
-    ("WS", 13), ("WS", 14), ("MX", 2, 3), ("W3", 13), ("W4", 5, 0), ("W4", 5, 1),
-    ("MX", 3, 0), ("MC", 2, 3), ("W4", 5, 2), ("W4", 5, 3), ("W2", 6, 0), ("MC", 3, 0),
-    ("W2", 6, 1), ("W1", 7), ("W2", 6, 2), ("W3", 14), ("W2", 6, 3), ("ST", 1, 0),
-    ("WS", 15), ("W5", 5), ("MX", 3, 1), ("W3", 15), ("MX", 3, 2), ("W4", 6, 0),
-    ("MC", 3, 1), ("W4", 6, 1), ("W2", 7, 0), ("ST", 1, 1), ("W4", 6, 2), ("MC", 3, 2),
-    ("MX", 3, 3), ("W4", 6, 3), ("ST", 1, 2), ("W4", 7, 0), ("MX", 4, 0), ("W5", 6),
-    ("MC", 3, 3), ("W2", 7, 1), ("ST", 1, 3), ("MC", 4, 0), ("W2", 7, 2), ("W4", 7, 1),
-    ("W2", 7, 3), ("MX", 4, 1), ("W4", 7, 2), ("W4", 7, 3), ("MX", 4, 2), ("MC", 4, 1),
-    ("W5", 7), ("MX", 4, 3), ("MC", 4, 2), ("MX", 5, 0), ("MC", 4, 3), ("MX", 5, 1),
-    ("MC", 5, 0), ("MX", 5, 2), ("ST", 2, 0), ("MC", 5, 1), ("MX", 5, 3), ("ST", 2, 1),
-    ("MC", 5, 2), ("MX", 6, 0), ("ST", 2, 2), ("MC", 5, 3), ("MX", 6, 1), ("ST", 2, 3),
-    ("MC", 6, 0), ("MX", 6, 2), ("MC", 6, 1), ("MX", 6, 3), ("MC", 6, 2), ("MX", 7, 0),
-    ("MC", 6, 3), ("MX", 7, 1), ("MC", 7, 0), ("MX", 7, 2), ("ST", 3, 0), ("MC", 7, 1),
-    ("MX", 7, 3), ("ST", 3, 1), ("MC", 7, 2), ("ST", 3, 2), ("MC", 7, 3), ("ST", 3, 3),
-)
 
 
 def tile_groupedstelinear_kernel(tc, x, weight_logits, raw_scales, out):
@@ -85,280 +36,228 @@ def tile_groupedstelinear_kernel(tc, x, weight_logits, raw_scales, out):
 
     with ExitStack() as ctx:
         const = ctx.enter_context(tc.tile_pool(name="const", bufs=1))
-        small = ctx.enter_context(tc.tile_pool(name="small", bufs=1))
         chn = ctx.enter_context(tc.tile_pool(name="chn", bufs=1))
         keep = ctx.enter_context(tc.tile_pool(name="keep", bufs=1))
-        xraw = ctx.enter_context(tc.tile_pool(name="xraw", bufs=2))
-        xperm = ctx.enter_context(tc.tile_pool(name="xperm", bufs=2))
+        xraw = ctx.enter_context(tc.tile_pool(name="xraw", bufs=4))
         xgrp = ctx.enter_context(tc.tile_pool(name="xgrp", bufs=2))
-        wraw = ctx.enter_context(tc.tile_pool(name="wraw", bufs=3))
+        wraw = ctx.enter_context(tc.tile_pool(name="wraw", bufs=4))
         wsign = ctx.enter_context(tc.tile_pool(name="wsign", bufs=2))
-        wwork = ctx.enter_context(tc.tile_pool(name="wwork", bufs=2))
-        obuf = ctx.enter_context(tc.tile_pool(name="obuf", bufs=6))
+        wscal = ctx.enter_context(tc.tile_pool(name="wscal", bufs=2))
+        wgrp = ctx.enter_context(tc.tile_pool(name="wgrp", bufs=2))
+        obuf = ctx.enter_context(tc.tile_pool(name="obuf", bufs=8))
         ps_t = ctx.enter_context(tc.psum_pool(name="ps_t", bufs=4))
-        ps_s = ctx.enter_context(tc.psum_pool(name="ps_s", bufs=2))
-        ps_a = ctx.enter_context(tc.psum_pool(name="ps_a", bufs=2))
+        ps_a = ctx.enter_context(tc.psum_pool(name="ps_a", bufs=4))
         ctx.enter_context(tc.manual_schedule())
 
-        ident_f = const.tile([P, P], F32, name="ident_f")
-        make_identity(nc, ident_f[:])
-        ident_b = const.tile([P, P], BF16, name="ident_b")
-        make_identity(nc, ident_b[:])
-        sel = const.tile([P, P * 32], BF16, name="sel")
-        nc.gpsimd.tensor_scalar(
-            out=sel[:].rearrange("p (c r) -> p c r", r=32),
-            in0=ident_b[:].unsqueeze(2).to_broadcast([P, P, 32]),
-            scalar1=1.0,
-            scalar2=0.0,
-            op0=ALU.mult,
-            op1=ALU.add,
-        )
-        warm = small.tile([P, 1], F32, name="warm")
+        ident = const.tile([P, P], F32, name="ident")
+        make_identity(nc, ident[:])
+        warm = const.tile([P, 1], F32, name="warm")
         nc.vector.memset(warm[:], 0.0)
-        warm2 = small.tile([P, 1], F32, name="warm2")
-        nc.scalar.activation(out=warm2[:], in_=warm[:], func=ACT.Exp)
+        warm2 = const.tile([P, 1], F32, name="warm2")
+        nc.scalar.activation(out=warm2[:], in_=warm[:], func=ACT.Ln, bias=1.0)
+
+        sraw = const.tile([P, NG * NG], BF16, name="sraw")
+        s2 = const.tile([P, 16, 2, NG, 2], BF16, name="s2")
 
         xc = keep.tile([P, 8, 512], U32, name="xc", align_bytes=64)
         xs = keep.tile([P, 8, 512], U8, name="xs", align_bytes=64)
         wc = []
         ws = []
-        for k in range(8):
+        for k in range(NK):
             wck = keep.tile([P, NPASS, 256], U32, name="wc%d" % k, align_bytes=64)
             wsk = keep.tile([P, NPASS, 256], U8, name="ws%d" % k, align_bytes=64)
             wc.append(wck)
             ws.append(wsk)
-        sraw = small.tile([P, 256], BF16, name="sraw")
 
         xr = {}
-        xp = {}
         xg = {}
         wr = {}
         sg = {}
-        st2 = {}
+        sw = {}
         wg = {}
         ob = {}
         tps = {}
-        stps = {}
         accs = {}
-        rows = {}
-        ch = {}
 
-        def st_lds():
-            nc.sync.dma_start(
-                out=sraw[:].rearrange("p (a g) -> p a g", g=NG),
-                in_=raw_scales.rearrange("(a p) g -> p a g", p=P),
-            )
+        nc.sync.dma_start(
+            out=sraw[:].rearrange("p (a g) -> p a g", g=NG),
+            in_=raw_scales.rearrange("(a p) g -> p a g", p=P),
+        )
 
-        slot_of = {"a1": "xm", "bb": "r1", "mm": "e0", "cr": "xx"}
+        def chain(a0, a1):
+            lo, hi = a0 * NG, a1 * NG
+            v = sraw[:, lo:hi]
+            t = {}
+            for name in (
+                "ab", "e0", "y0", "xm", "r1", "rr", "th", "c1", "t2", "rx", "xx", "x1",
+                "ru", "r2", "yr", "a1", "bb", "mm", "rs", "g4", "cr",
+            ):
+                tl = chn.tile([P, hi - lo], F32, name="%s_%d" % (name, a0))
+                t[name] = tl[:]
+            for name in ("ni", "p2"):
+                tl = chn.tile([P, hi - lo], I32, name="%s_%d" % (name, a0))
+                t[name] = tl[:]
 
-        def cht(name, dtype=F32):
-            t = chn.tile([P, 256], dtype, name=slot_of.get(name, name))
-            ch[name] = t
-            return t
+            def stt(dst, in0, scalar, in1, op0, op1):
+                nc.vector.scalar_tensor_tensor(
+                    out=t[dst], in0=t[in0], scalar=scalar, in1=in1, op0=op0, op1=op1
+                )
 
-        def act(dst, src, func, scale=1.0, bias=0.0):
-            nc.scalar.activation(out=cht(dst)[:], in_=src, func=func, scale=scale, bias=bias)
+            def tsc(dst, in0, s1, s2_, op0, op1):
+                nc.vector.tensor_scalar(
+                    out=t[dst], in0=t[in0], scalar1=s1, scalar2=s2_, op0=op0, op1=op1
+                )
 
-        def stt(dst, in0, scalar, in1, op0, op1):
-            nc.vector.scalar_tensor_tensor(
-                out=cht(dst)[:], in0=ch[in0][:], scalar=scalar, in1=in1, op0=op0, op1=op1
-            )
+            def ttt(dst, in0, in1, op):
+                nc.vector.tensor_tensor(out=t[dst], in0=t[in0], in1=t[in1], op=op)
 
-        def tsc(dst, in0, s1, s2, op0, op1, dtype=F32):
-            nc.vector.tensor_scalar(
-                out=cht(dst, dtype)[:], in0=ch[in0][:], scalar1=s1, scalar2=s2, op0=op0, op1=op1
-            )
+            def act(dst, src, func, scale=1.0, bias=0.0):
+                nc.scalar.activation(out=t[dst], in_=src, func=func, scale=scale, bias=bias)
 
-        def ttt(dst, in0, in1, op):
-            nc.vector.tensor_tensor(out=cht(dst)[:], in0=ch[in0][:], in1=ch[in1][:], op=op)
+            def pairs(name):
+                return (
+                    t[name]
+                    .rearrange("p (a g) -> p a g", g=NG)
+                    .unsqueeze(3)
+                    .to_broadcast([P, a1 - a0, NG, 2])
+                )
 
-        def st_c(name):
-            if name == "abs":
-                act("abs", sraw[:], ACT.Abs)
-            elif name == "relu":
-                act("relu", sraw[:], ACT.Relu)
-            elif name == "e0":
-                act("e0", ch["abs"][:], ACT.Exp, scale=-1.0)
-            elif name == "y0":
-                act("y0", ch["e0"][:], ACT.Ln, bias=1.0)
-            elif name == "xm":
-                tsc("xm", "abs", -LOG2E, MAGIC, ALU.mult, ALU.add)
-            elif name == "ni":
-                tsc("ni", "xm", MAGIC, -120.0, ALU.subtract, ALU.max, I32)
-            elif name == "r1":
-                stt("r1", "ni", -LN2_HI, ch["abs"][:], ALU.mult, ALU.subtract)
-            elif name == "rr":
-                stt("rr", "ni", -LN2_LO, ch["r1"][:], ALU.mult, ALU.add)
-            elif name == "p2":
-                tsc("p2", "ni", 127.0, 8388608.0, ALU.add, ALU.mult, I32)
-            elif name == "th":
-                act("th", ch["rr"][:], ACT.Tanh, scale=0.5)
-            elif name == "c1":
-                act("c1", ch["th"][:], ACT.Identity, scale=-2.0, bias=2.0)
-            elif name == "t2":
-                act("t2", ch["y0"][:], ACT.Tanh, scale=0.5)
-            elif name == "rx":
-                act("rx", ch["rr"][:], ACT.Exp)
-            elif name == "xx":
-                act("xx", ch["y0"][:], ACT.Exp, scale=-1.0)
-            elif name == "x1":
-                act("x1", ch["xx"][:], ACT.Identity, bias=1.0)
-            elif name == "a1":
-                stt("a1", "th", 1.0, ch["p2"][:].bitcast(F32), ALU.add, ALU.mult)
-            elif name == "bb":
-                ttt("bb", "a1", "c1", ALU.add)
-            elif name == "mm":
-                ttt("mm", "bb", "t2", ALU.mult)
-            elif name == "rs":
-                ttt("rs", "mm", "a1", ALU.subtract)
-            elif name == "g4":
-                stt("g4", "rx", 1.0, ch["x1"][:], ALU.add, ALU.mult)
-            elif name == "yr":
-                ttt("yr", "y0", "relu", ALU.add)
-            elif name == "cr":
-                ttt("cr", "rs", "g4", ALU.mult)
-            else:
-                stt("sp", "cr", -0.25, ch["yr"][:], ALU.mult, ALU.add)
+            def fin(u):
+                nc.vector.scalar_tensor_tensor(
+                    out=s2[:, a0:a1, u, :, :],
+                    in0=pairs("cr"), scalar=-0.5, in1=pairs("yr"), op0=ALU.mult, op1=ALU.add,
+                )
 
-        def st_ct(h):
-            t = ps_s.tile([P, P], F32, name="stp")
-            nc.tensor.transpose(t[:], ch["sp"][:, h * P : (h + 1) * P], ident_f[:])
-            stps[("c", h)] = t
+            guess = [
+                lambda: act("ab", v, ACT.Abs),
+                lambda: act("e0", t["ab"], ACT.Exp, scale=-1.0),
+                lambda: act("y0", t["e0"], ACT.Ln, bias=1.0),
+            ]
+            reduce_ = [
+                lambda: tsc("xm", "ab", -LOG2E, MAGIC, ALU.mult, ALU.add),
+                lambda: tsc("ni", "xm", MAGIC, -120.0, ALU.subtract, ALU.max),
+                lambda: stt("r1", "ni", -LN2_HI, t["ab"], ALU.mult, ALU.subtract),
+                lambda: stt("rr", "ni", -LN2_LO, t["r1"], ALU.mult, ALU.add),
+                lambda: tsc("p2", "ni", 127.0, 8388608.0, ALU.add, ALU.mult),
+            ]
+            tables = [
+                lambda: act("th", t["rr"], ACT.Tanh, scale=0.5),
+                lambda: act("c1", t["th"], ACT.Identity, scale=-2.0, bias=2.0),
+                lambda: act("t2", t["y0"], ACT.Tanh, scale=0.5),
+                lambda: act("rx", t["rr"], ACT.Exp),
+                lambda: act("xx", t["y0"], ACT.Exp, scale=-1.0),
+                lambda: act("x1", t["xx"], ACT.Identity, bias=1.0),
+                lambda: act("ru", v, ACT.Relu, scale=2.0),
+                lambda: act("r2", t["ru"], ACT.Identity, bias=2e-6),
+            ]
+            finish = [
+                lambda: stt("a1", "th", 1.0, t["p2"].bitcast(F32), ALU.add, ALU.mult),
+                lambda: ttt("bb", "a1", "c1", ALU.add),
+                lambda: ttt("mm", "bb", "t2", ALU.mult),
+                lambda: ttt("rs", "mm", "a1", ALU.subtract),
+                lambda: stt("g4", "rx", 1.0, t["x1"], ALU.add, ALU.mult),
+                lambda: stt("yr", "y0", 2.0, t["r2"], ALU.mult, ALU.add),
+                lambda: ttt("cr", "rs", "g4", ALU.mult),
+                lambda: fin(0),
+                lambda: fin(1),
+            ]
+            return guess, reduce_, tables, finish
 
-        def st_cr(h):
-            rw = small.tile([P, P], BF16, name="rows%d" % h)
-            nc.scalar.activation(
-                out=rw[:], in_=stps[("c", h)][:], func=ACT.Identity, scale=2.0, bias=2e-6
-            )
-            rows[h] = rw
-
-        def st_lx(m):
+        def load_x(m):
             q = m // 2
             if q not in xr:
-                t = xraw.tile([P, 2 * IN], BF16, name="xr")
+                t = xraw.tile([P, 2, IN], BF16, name="xr")
                 xr[q] = t
-            rows_m = xf[m * P : (m + 1) * P, :]
-            if q in X_BY_DMA:
-                src = rows_m.rearrange("p (g u j) -> p g u j", g=NG, u=2)
-                dst = xr[q][:].rearrange("p (u m g j) -> p u m g j", u=2, m=2, g=NG)
-                for u in range(2):
-                    nc.sync.dma_start(out=dst[:, u, m % 2, :, :], in_=src[:, :, u, :])
-                xp[q] = xr[q]
-            else:
-                lo = (m % 2) * IN
-                nc.sync.dma_start(out=xr[q][:, lo : lo + IN], in_=rows_m)
+            nc.sync.dma_start(out=xr[q][:, m % 2, :], in_=xf[m * P : (m + 1) * P, :])
 
-        def st_x1(q):
-            t = xperm.tile([P, 2 * IN], BF16, name="xp")
-            nc.vector.tensor_copy(
-                out=t[:].rearrange("p (u g j) -> p u g j", u=2, g=2 * NG),
-                in_=xr[q][:].rearrange("p (g u j) -> p u g j", g=2 * NG, u=2),
-            )
-            xp[q] = t
-
-        def st_x2(q, b):
-            xw = xp[q][:].bitcast(F32)
+        def turn_x(q, b):
             tp = ps_t.tile([P, 2, 2, P], F32, name="tp")
+            xw = xr[q][:, b // 2, :].bitcast(F32)
             for ci in range(2):
                 for u in range(2):
-                    lo = u * 1024 + (b // 2) * 512 + (2 * (b % 2) + ci) * P
-                    nc.tensor.transpose(tp[:, ci, u, :], xw[:, lo : lo + P], ident_f[:])
+                    lo = (2 * (b % 2) + ci) * 256
+                    nc.tensor.transpose(tp[:, ci, u, :], xw[:, lo + u : lo + 256 : 2], ident[:])
             tps[("x", q, b)] = tp
 
-        def st_x3(q, b):
+        def lay_x(q, b, copy=nc.scalar.copy):
             if q not in xg:
                 t = xgrp.tile([P, 2 * IN], BF16, name="xg", align_bytes=64)
                 xg[q] = t
             xgw = xg[q][:].bitcast(F32).rearrange("p (c r u) -> p c r u", c=2 * NPASS, u=2)
-            nc.scalar.copy(
+            copy(
                 out=xgw[:, 2 * b : 2 * b + 2, :, :],
                 in_=tps[("x", q, b)][:].rearrange("p c u r -> p c r u"),
             )
 
-        def st_x4(q):
+        def quant_x(q):
             nc.vector.quantize_mx(
                 out=xc[:, 2 * q : 2 * q + 2, :].rearrange("p a b -> p (a b)").bitcast(FP8X4),
                 scales=xs[:, 2 * q : 2 * q + 2, :].rearrange("p a b -> p (a b)"),
                 in_=xg[q][:],
             )
 
-        def st_lw(a):
+        def load_w(a):
             k = a // 2
             if k not in wr:
-                t = wraw.tile([P, 2 * IN], BF16, name="wr")
+                t = wraw.tile([P, 2, IN], BF16, name="wr")
                 wr[k] = t
-            lo = (a % 2) * IN
-            nc.sync.dma_start(out=wr[k][:, lo : lo + IN], in_=wl[a * P : (a + 1) * P, :])
+            nc.sync.dma_start(out=wr[k][:, a % 2, :], in_=wl[a * P : (a + 1) * P, :])
 
-        def st_w1(k):
-            t = wsign.tile([P, 2 * IN], BF16, name="sg")
+        def sign_w(a):
+            k = a // 2
+            if k not in sg:
+                t = wsign.tile([P, 2, IN], BF16, name="sg")
+                sg[k] = t
             nc.vector.tensor_scalar(
-                out=t[:].rearrange("p (u g j) -> p u g j", u=2, g=2 * NG),
-                in0=wr[k][:].rearrange("p (g u j) -> p u g j", g=2 * NG, u=2),
+                out=sg[k][:, a % 2, :].rearrange("p (u q e) -> p u q e", u=2, e=2),
+                in0=wr[k][:, a % 2, :].rearrange("p (q u e) -> p u q e", u=2, e=2),
                 scalar1=0.0,
                 scalar2=0.5,
                 op0=ALU.is_ge,
                 op1=ALU.subtract,
             )
-            sg[k] = t
 
-        def st_ws(a):
-            stp = ps_s.tile([P, NPASS, P], F32, name="stp")
-            for c in range(NPASS):
-                lo = ((a % 8) * NG + 4 * c) * 32
-                nc.tensor.matmul(
-                    stp[:, c, :],
-                    lhsT=sel[:, lo : lo + P],
-                    rhs=rows[a // 8][:],
-                    start=True,
-                    stop=True,
-                )
-            stps[("w", a)] = stp
-
-        def st_w3(a):
+        def scale_w(a):
             k = a // 2
-            if k not in st2:
-                t = wwork.tile([P, NPASS, 2, P, 2], BF16, name="st2")
-                st2[k] = t
-            nc.scalar.copy(
-                out=st2[k][:, :, a % 2, :, :],
-                in_=stps[("w", a)][:].unsqueeze(3).to_broadcast([P, NPASS, P, 2]),
-            )
-
-        def st_w2(k, c):
-            tp = ps_t.tile([P, 2, 2, P], F32, name="tp")
-            sgw = sg[k][:].bitcast(F32)
-            for u in range(2):
-                for a2 in range(2):
-                    lo = u * 1024 + a2 * 512 + c * P
-                    nc.tensor.transpose(tp[:, u, a2, :], sgw[:, lo : lo + P], ident_f[:])
-            tps[("w", k, c)] = tp
-
-        def st_w4(k, c):
-            if k not in wg:
-                t = wwork.tile([P, NPASS, 1024], BF16, name="wg", align_bytes=64)
-                wg[k] = t
+            if k not in sw:
+                t = wscal.tile([P, 2, IN], BF16, name="sw")
+                sw[k] = t
             nc.vector.tensor_tensor(
-                out=wg[k][:, c, :].rearrange("p (o u e) -> p o u e", u=2, e=2),
-                in0=tps[("w", k, c)][:].bitcast(BF16).rearrange("p u a (o e) -> p (a o) u e", e=2),
-                in1=st2[k][:, c]
-                .rearrange("p a o e -> p (a o) e")
-                .unsqueeze(2)
-                .to_broadcast([P, 256, 2, 2]),
+                out=sw[k][:, a % 2, :].rearrange("p (h r e) -> p h r e", r=32, e=2),
+                in0=sg[k][:, a % 2, :].rearrange("p (h r e) -> p h r e", r=32, e=2),
+                in1=s2[:, a, :, :, :].rearrange("p u g e -> p (u g) e").unsqueeze(2).to_broadcast([P, 32, 32, 2]),
                 op=ALU.mult,
             )
 
-        def st_w5(k):
-            nc.vector.quantize_mx(
-                out=wc[k][:].rearrange("p c o -> p (c o)").bitcast(FP8X4),
-                scales=ws[k][:].rearrange("p c o -> p (c o)"),
-                in_=wg[k][:].rearrange("p c o -> p (c o)"),
+        def turn_w(k, c):
+            tp = ps_t.tile([P, 2, 2, P], F32, name="tp")
+            for u in range(2):
+                for a2 in range(2):
+                    lo = u * 512 + c * P
+                    sww = sw[k][:, a2, :].bitcast(F32)
+                    nc.tensor.transpose(tp[:, u, a2, :], sww[:, lo : lo + P], ident[:])
+            tps[("w", k, c)] = tp
+
+        def lay_w(k, c, copy=nc.scalar.copy):
+            if k not in wg:
+                t = wgrp.tile([P, NPASS, 1024], BF16, name="wg", align_bytes=64)
+                wg[k] = t
+            copy(
+                out=wg[k][:, c, :].bitcast(F32).rearrange("p (o u) -> p o u", u=2),
+                in_=tps[("w", k, c)][:].rearrange("p u a o -> p (a o) u"),
             )
 
-        def st_mx(k, mp):
+        def quant_w(k, c0=0, c1=NPASS):
+            nc.vector.quantize_mx(
+                out=wc[k][:, c0:c1, :].rearrange("p c o -> p (c o)").bitcast(FP8X4),
+                scales=ws[k][:, c0:c1, :].rearrange("p c o -> p (c o)"),
+                in_=wg[k][:, c0:c1, :].rearrange("p c o -> p (c o)"),
+            )
+
+        def product(k, q):
             acc = ps_a.tile([P, 2, 256], F32, name="acc")
             for mi in range(2):
-                m = 2 * mp + mi
+                m = 2 * q + mi
                 for c in range(NPASS):
                     nc.tensor.matmul_mx(
                         out=acc[:, mi, :],
@@ -369,26 +268,117 @@ def tile_groupedstelinear_kernel(tc, x, weight_logits, raw_scales, out):
                         start=(c == 0),
                         stop=(c == NPASS - 1),
                     )
-            accs[(k, mp)] = acc
+            accs[(k, q)] = acc
 
-        def st_mc(k, mp):
-            n = k // 2
-            if (n, mp) not in ob:
-                t = obuf.tile([P, 2, 512], F32, name="ob")
-                ob[(n, mp)] = t
-            lo = (k % 2) * 256
-            nc.scalar.copy(out=ob[(n, mp)][:, :, lo : lo + 256], in_=accs[(k, mp)][:])
+        def empty(k, q):
+            t = obuf.tile([P, 2, 256], F32, name="ob")
+            ob[(k, q)] = t
+            nc.scalar.copy(out=t[:], in_=accs[(k, q)][:])
 
-        def st_st(n, mp):
+        def store(k, q):
             nc.sync.dma_start(
-                out=of[:, 2 * mp : 2 * mp + 2, n * 512 : (n + 1) * 512], in_=ob[(n, mp)][:]
+                out=of[:, 2 * q : 2 * q + 2, k * 256 : (k + 1) * 256], in_=ob[(k, q)][:]
             )
 
-        stages = {
-            "LDS": st_lds, "C": st_c,
-            "CT": st_ct, "CR": st_cr, "LX": st_lx, "X1": st_x1, "X2": st_x2, "X3": st_x3,
-            "X4": st_x4, "LW": st_lw, "W1": st_w1, "WS": st_ws, "W3": st_w3, "W2": st_w2,
-            "W4": st_w4, "W5": st_w5, "MX": st_mx, "MC": st_mc, "ST": st_st,
-        }
-        for op in ORDER:
-            stages[op[0]](*op[1:])
+        def pe_x(q):
+            for b in range(4):
+                turn_x(q, b)
+                lay_x(q, b)
+
+        def pe_w(k):
+            for c in range(NPASS):
+                turn_w(k, c)
+                lay_w(k, c)
+
+        def mul(k, q):
+            product(k, q)
+            empty(k, q)
+            store(k, q)
+
+        load_w(0)
+        load_w(1)
+        for m in range(8):
+            load_x(m)
+        for a in range(2, 8):
+            load_w(a)
+        first = chain(0, 4)
+        second = chain(4, 16)
+
+        def both(stage, lo, hi):
+            for i in range(lo, hi):
+                first[stage][i]()
+                second[stage][i]()
+
+        both(0, 0, 3)
+        both(1, 0, 5)
+        sign_w(0)
+        sign_w(1)
+        both(2, 0, 8)
+        both(3, 0, 7)
+        first[3][7]()
+        first[3][8]()
+        pe_x(0)
+        scale_w(0)
+        scale_w(1)
+        pe_x(1)
+        quant_x(0)
+        for c in range(NPASS):
+            turn_w(0, c)
+        lay_w(0, 0)
+        lay_w(0, 1)
+        lay_w(0, 2, nc.vector.tensor_copy)
+        lay_w(0, 3, nc.vector.tensor_copy)
+        pe_x(2)
+        quant_w(0, 0, 1)
+        quant_w(0, 1, 2)
+        quant_w(0, 2, 3)
+        quant_w(0, 3, 4)
+        mul(0, 0)
+        sign_w(2)
+        quant_x(1)
+        sign_w(3)
+        pe_x(3)
+        load_w(8)
+        load_w(9)
+        mul(0, 1)
+        scale_w(2)
+        scale_w(3)
+        quant_x(2)
+        pe_w(1)
+        mul(0, 2)
+        quant_x(3)
+        second[3][7]()
+        sign_w(4)
+        second[3][8]()
+        quant_w(1)
+        mul(0, 3)
+        sign_w(5)
+        scale_w(4)
+        scale_w(5)
+        mul(1, 0)
+        load_w(10)
+        load_w(11)
+        mul(1, 1)
+        pe_w(2)
+        mul(1, 2)
+        mul(1, 3)
+        sign_w(6)
+        sign_w(7)
+        scale_w(6)
+        scale_w(7)
+        quant_w(2)
+        for k in range(2, NK):
+            if k + 4 < NK:
+                load_w(2 * k + 8)
+                load_w(2 * k + 9)
+            if k + 1 < NK:
+                pe_w(k + 1)
+            if k + 2 < NK:
+                sign_w(2 * k + 4)
+                sign_w(2 * k + 5)
+                scale_w(2 * k + 4)
+                scale_w(2 * k + 5)
+            if k + 1 < NK:
+                quant_w(k + 1)
+            for q in range(NQ):
+                mul(k, q)

@@ -26,6 +26,11 @@ LOG2E = 1.4426950408889634
 MAGIC = 12582912.0
 LN2_HI = 0.693145751953125
 LN2_LO = 1.4286068203094172e-06
+Q1_SCALE = 0.1880921133056114
+Q1_BIAS = -0.4383943121398337
+Q1_ADD = 0.06321998156945995
+Q2_BIAS = 0.2963586866440234
+Q2_ADD = 3.826385480469501
 
 
 def tile_groupedstelinear_kernel(tc, x, weight_logits, raw_scales, out):
@@ -54,7 +59,7 @@ def tile_groupedstelinear_kernel(tc, x, weight_logits, raw_scales, out):
         warm = const.tile([P, 1], F32, name="warm")
         nc.vector.memset(warm[:], 0.0)
         warm2 = const.tile([P, 1], F32, name="warm2")
-        nc.scalar.activation(out=warm2[:], in_=warm[:], func=ACT.Ln, bias=1.0)
+        nc.scalar.activation(out=warm2[:], in_=warm[:], func=ACT.Exp)
 
         sraw = const.tile([P, NG * NG], BF16, name="sraw")
         s2 = const.tile([P, 16, 2, NG, 2], BF16, name="s2")
@@ -79,18 +84,19 @@ def tile_groupedstelinear_kernel(tc, x, weight_logits, raw_scales, out):
         tps = {}
         accs = {}
 
-        nc.sync.dma_start(
-            out=sraw[:].rearrange("p (a g) -> p a g", g=NG),
-            in_=raw_scales.rearrange("(a p) g -> p a g", p=P),
-        )
+        def load_scales(a0, a1):
+            nc.sync.dma_start(
+                out=sraw[:, a0 * NG : a1 * NG].rearrange("p (a g) -> p a g", g=NG),
+                in_=raw_scales.rearrange("(a p) g -> p a g", p=P)[:, a0:a1, :],
+            )
 
         def chain(a0, a1):
             lo, hi = a0 * NG, a1 * NG
             v = sraw[:, lo:hi]
             t = {}
             for name in (
-                "ab", "e0", "y0", "xm", "r1", "rr", "th", "c1", "t2", "rx", "xx", "x1",
-                "ru", "r2", "yr", "a1", "bb", "mm", "rs", "g4", "cr",
+                "ab", "e0", "q1", "q2", "y1", "y0", "y2", "xm", "r1", "rr", "th", "t2", "rx", "xx", "x1",
+                "yr", "a1", "bb", "mm", "rs", "g4", "cr",
             ):
                 tl = chn.tile([P, hi - lo], F32, name="%s_%d" % (name, a0))
                 t[name] = tl[:]
@@ -125,38 +131,41 @@ def tile_groupedstelinear_kernel(tc, x, weight_logits, raw_scales, out):
             def fin(u):
                 nc.vector.scalar_tensor_tensor(
                     out=s2[:, a0:a1, u, :, :],
-                    in0=pairs("cr"), scalar=-0.5, in1=pairs("yr"), op0=ALU.mult, op1=ALU.add,
+                    in0=pairs("yr"), scalar=2.0, in1=pairs("cr"), op0=ALU.mult, op1=ALU.add,
                 )
 
             guess = [
                 lambda: act("ab", v, ACT.Abs),
                 lambda: act("e0", t["ab"], ACT.Exp, scale=-1.0),
-                lambda: act("y0", t["e0"], ACT.Ln, bias=1.0),
+                lambda: act("q1", t["e0"], ACT.Square, scale=Q1_SCALE, bias=Q1_BIAS),
+                lambda: act("q2", t["e0"], ACT.Square, bias=Q2_BIAS),
             ]
             reduce_ = [
                 lambda: tsc("xm", "ab", -LOG2E, MAGIC, ALU.mult, ALU.add),
                 lambda: tsc("ni", "xm", MAGIC, -120.0, ALU.subtract, ALU.max),
                 lambda: stt("r1", "ni", -LN2_HI, t["ab"], ALU.mult, ALU.subtract),
                 lambda: stt("rr", "ni", -LN2_LO, t["r1"], ALU.mult, ALU.add),
+                lambda: stt("y1", "q1", Q1_ADD, t["e0"], ALU.add, ALU.mult),
                 lambda: tsc("p2", "ni", 127.0, 8388608.0, ALU.add, ALU.mult),
+                lambda: stt("y0", "q2", Q2_ADD, t["y1"], ALU.add, ALU.mult),
             ]
             tables = [
                 lambda: act("th", t["rr"], ACT.Tanh, scale=0.5),
-                lambda: act("c1", t["th"], ACT.Identity, scale=-2.0, bias=2.0),
-                lambda: act("t2", t["y0"], ACT.Tanh, scale=0.5),
                 lambda: act("rx", t["rr"], ACT.Exp),
+                lambda: act("t2", t["y0"], ACT.Tanh, scale=0.5),
                 lambda: act("xx", t["y0"], ACT.Exp, scale=-1.0),
-                lambda: act("x1", t["xx"], ACT.Identity, bias=1.0),
-                lambda: act("ru", v, ACT.Relu, scale=2.0),
-                lambda: act("r2", t["ru"], ACT.Identity, bias=2e-6),
+                lambda: act("y2", t["y0"], ACT.Identity, bias=1e-6),
+                lambda: act("x1", t["xx"], ACT.Identity, scale=-0.5, bias=-0.5),
             ]
             finish = [
                 lambda: stt("a1", "th", 1.0, t["p2"].bitcast(F32), ALU.add, ALU.mult),
-                lambda: ttt("bb", "a1", "c1", ALU.add),
-                lambda: ttt("mm", "bb", "t2", ALU.mult),
+                lambda: stt("bb", "th", -2.0, t["a1"], ALU.mult, ALU.add),
+                lambda: stt("mm", "bb", 2.0, t["t2"], ALU.add, ALU.mult),
                 lambda: ttt("rs", "mm", "a1", ALU.subtract),
                 lambda: stt("g4", "rx", 1.0, t["x1"], ALU.add, ALU.mult),
-                lambda: stt("yr", "y0", 2.0, t["r2"], ALU.mult, ALU.add),
+                lambda: nc.vector.scalar_tensor_tensor(
+                    out=t["yr"], in0=v, scalar=0.0, in1=t["y2"], op0=ALU.max, op1=ALU.add
+                ),
                 lambda: ttt("cr", "rs", "g4", ALU.mult),
                 lambda: fin(0),
                 lambda: fin(1),
@@ -295,78 +304,118 @@ def tile_groupedstelinear_kernel(tc, x, weight_logits, raw_scales, out):
             empty(k, q)
             store(k, q)
 
+        load_scales(0, 8)
         load_w(0)
         load_w(1)
-        for m in range(8):
-            load_x(m)
-        for a in range(2, 8):
-            load_w(a)
-        first = chain(0, 4)
-        second = chain(4, 16)
+        load_x(0)
+        load_x(1)
+        load_w(2)
+        load_scales(8, 16)
+        load_x(2)
+        load_x(3)
+        load_w(3)
+        load_x(4)
+        load_x(5)
+        load_x(6)
+        load_x(7)
+        load_w(4)
+        load_w(5)
+        load_w(6)
+        load_w(7)
+        one = chain(0, 4)
+        two = chain(4, 8)
+        three = chain(8, 16)
 
-        def both(stage, lo, hi):
-            for i in range(lo, hi):
-                first[stage][i]()
-                second[stage][i]()
+        def each(stage, parts):
+            for i in range(len(one[stage])):
+                for part in parts:
+                    part[stage][i]()
 
-        both(0, 0, 3)
-        both(1, 0, 5)
+        def tables_of_three():
+            each(2, (three,))
+
+        later = two[3] + three[1] + [tables_of_three] + three[3]
+        done = [0]
+
+        def aside(n=1):
+            for i in range(n):
+                if done[0] < len(later):
+                    later[done[0]]()
+                    done[0] += 1
+
+        each(0, (one, two))
+        each(1, (one, two))
+        each(2, (one, two))
         sign_w(0)
-        sign_w(1)
-        both(2, 0, 8)
-        both(3, 0, 7)
-        first[3][7]()
-        first[3][8]()
+        for i in range(9):
+            one[3][i]()
+            if i < 9:
+                aside()
+            if i == 3:
+                sign_w(1)
         pe_x(0)
+        each(0, (three,))
+        sign_w(2)
         scale_w(0)
         scale_w(1)
-        pe_x(1)
-        quant_x(0)
-        for c in range(NPASS):
-            turn_w(0, c)
-        lay_w(0, 0)
-        lay_w(0, 1)
-        lay_w(0, 2, nc.vector.tensor_copy)
-        lay_w(0, 3, nc.vector.tensor_copy)
-        pe_x(2)
-        quant_w(0, 0, 1)
-        quant_w(0, 1, 2)
-        quant_w(0, 2, 3)
-        quant_w(0, 3, 4)
-        mul(0, 0)
-        sign_w(2)
-        quant_x(1)
         sign_w(3)
-        pe_x(3)
+        pe_x(1)
+        pe_w(0)
+        scale_w(2)
+        aside()
+        scale_w(3)
+        aside()
+        quant_x(0)
+        for c in range(4):
+            aside()
+            quant_w(0, c, c + 1)
+        aside()
+        pe_w(1)
         load_w(8)
         load_w(9)
-        mul(0, 1)
-        scale_w(2)
-        scale_w(3)
-        quant_x(2)
-        pe_w(1)
-        mul(0, 2)
-        quant_x(3)
-        second[3][7]()
-        sign_w(4)
-        second[3][8]()
+        pe_x(2)
+        quant_x(1)
+        aside()
+        mul(0, 0)
         quant_w(1)
-        mul(0, 3)
-        sign_w(5)
-        scale_w(4)
-        scale_w(5)
+        aside()
+        pe_x(3)
+        mul(0, 1)
+        quant_x(2)
+        aside()
         mul(1, 0)
+        mul(1, 1)
+        sign_w(4)
+        aside()
         load_w(10)
         load_w(11)
-        mul(1, 1)
-        pe_w(2)
+        sign_w(5)
+        aside()
+        quant_x(3)
+        aside()
+        mul(0, 2)
         mul(1, 2)
-        mul(1, 3)
+        scale_w(4)
+        aside()
+        scale_w(5)
+        aside()
+        mul(0, 3)
+        pe_w(2)
         sign_w(6)
+        aside()
         sign_w(7)
+        aside()
+        mul(1, 3)
         scale_w(6)
+        aside()
         scale_w(7)
+        aside()
         quant_w(2)
+        aside()
+        sign_w(8)
+        aside()
+        sign_w(9)
+        aside(20)
         for k in range(2, NK):
             if k + 4 < NK:
                 load_w(2 * k + 8)
@@ -374,8 +423,9 @@ def tile_groupedstelinear_kernel(tc, x, weight_logits, raw_scales, out):
             if k + 1 < NK:
                 pe_w(k + 1)
             if k + 2 < NK:
-                sign_w(2 * k + 4)
-                sign_w(2 * k + 5)
+                if k > 2:
+                    sign_w(2 * k + 4)
+                    sign_w(2 * k + 5)
                 scale_w(2 * k + 4)
                 scale_w(2 * k + 5)
             if k + 1 < NK:

@@ -23,7 +23,6 @@ NQ = 4
 FLOPS = 2 * TOK * IN * OUT
 
 LOG2E = 1.4426950408889634
-MAGIC = 12582912.0
 LN2_HI = 0.693145751953125
 LN2_LO = 1.4286068203094172e-06
 Q1_SCALE = 0.1880921133056114
@@ -62,7 +61,7 @@ def tile_groupedstelinear_kernel(tc, x, weight_logits, raw_scales, out):
         nc.scalar.activation(out=warm2[:], in_=warm[:], func=ACT.Exp)
 
         sraw = const.tile([P, NG * NG], BF16, name="sraw")
-        s2 = const.tile([P, 16, 2, NG, 2], BF16, name="s2")
+        s2 = const.tile([P, 16, NG, 2], BF16, name="s2")
 
         xc = keep.tile([P, 8, 512], U32, name="xc", align_bytes=64)
         xs = keep.tile([P, 8, 512], U8, name="xs", align_bytes=64)
@@ -95,7 +94,7 @@ def tile_groupedstelinear_kernel(tc, x, weight_logits, raw_scales, out):
             v = sraw[:, lo:hi]
             t = {}
             for name in (
-                "ab", "e0", "q1", "q2", "y1", "y0", "y2", "xm", "r1", "rr", "th", "t2", "rx", "xx", "x1",
+                "ab", "e0", "q1", "q2", "y1", "y0", "y2", "r1", "rr", "th", "t2", "rx", "xx", "x1",
                 "yr", "a1", "bb", "mm", "rs", "g4", "cr",
             ):
                 tl = chn.tile([P, hi - lo], F32, name="%s_%d" % (name, a0))
@@ -121,16 +120,11 @@ def tile_groupedstelinear_kernel(tc, x, weight_logits, raw_scales, out):
                 nc.scalar.activation(out=t[dst], in_=src, func=func, scale=scale, bias=bias)
 
             def pairs(name):
-                return (
-                    t[name]
-                    .rearrange("p (a g) -> p a g", g=NG)
-                    .unsqueeze(3)
-                    .to_broadcast([P, a1 - a0, NG, 2])
-                )
+                return t[name].unsqueeze(2).to_broadcast([P, hi - lo, 2])
 
-            def fin(u):
+            def fin():
                 nc.vector.scalar_tensor_tensor(
-                    out=s2[:, a0:a1, u, :, :],
+                    out=s2[:, a0:a1, :, :].rearrange("p a g e -> p (a g) e"),
                     in0=pairs("yr"), scalar=2.0, in1=pairs("cr"), op0=ALU.mult, op1=ALU.add,
                 )
 
@@ -141,8 +135,7 @@ def tile_groupedstelinear_kernel(tc, x, weight_logits, raw_scales, out):
                 lambda: act("q2", t["e0"], ACT.Square, bias=Q2_BIAS),
             ]
             reduce_ = [
-                lambda: tsc("xm", "ab", -LOG2E, MAGIC, ALU.mult, ALU.add),
-                lambda: tsc("ni", "xm", MAGIC, -120.0, ALU.subtract, ALU.max),
+                lambda: tsc("ni", "ab", -LOG2E, -120.0, ALU.mult, ALU.max),
                 lambda: stt("r1", "ni", -LN2_HI, t["ab"], ALU.mult, ALU.subtract),
                 lambda: stt("rr", "ni", -LN2_LO, t["r1"], ALU.mult, ALU.add),
                 lambda: stt("y1", "q1", Q1_ADD, t["e0"], ALU.add, ALU.mult),
@@ -167,8 +160,7 @@ def tile_groupedstelinear_kernel(tc, x, weight_logits, raw_scales, out):
                     out=t["yr"], in0=v, scalar=0.0, in1=t["y2"], op0=ALU.max, op1=ALU.add
                 ),
                 lambda: ttt("cr", "rs", "g4", ALU.mult),
-                lambda: fin(0),
-                lambda: fin(1),
+                fin,
             ]
             return guess, reduce_, tables, finish
 
@@ -215,10 +207,10 @@ def tile_groupedstelinear_kernel(tc, x, weight_logits, raw_scales, out):
         def sign_w(a):
             k = a // 2
             if k not in sg:
-                t = wsign.tile([P, 2, IN], BF16, name="sg")
+                t = wsign.tile([P, 2, 2, 1024], BF16, name="sg")
                 sg[k] = t
             nc.vector.tensor_scalar(
-                out=sg[k][:, a % 2, :].rearrange("p (u q e) -> p u q e", u=2, e=2),
+                out=sg[k][:, :, a % 2, :].rearrange("p u (q e) -> p u q e", e=2),
                 in0=wr[k][:, a % 2, :].rearrange("p (q u e) -> p u q e", u=2, e=2),
                 scalar1=0.0,
                 scalar2=0.5,
@@ -226,15 +218,17 @@ def tile_groupedstelinear_kernel(tc, x, weight_logits, raw_scales, out):
                 op1=ALU.subtract,
             )
 
-        def scale_w(a):
-            k = a // 2
+        def scale_w(k, u):
             if k not in sw:
-                t = wscal.tile([P, 2, IN], BF16, name="sw")
+                t = wscal.tile([P, 2, 2, 1024], BF16, name="sw")
                 sw[k] = t
             nc.vector.tensor_tensor(
-                out=sw[k][:, a % 2, :].rearrange("p (h r e) -> p h r e", r=32, e=2),
-                in0=sg[k][:, a % 2, :].rearrange("p (h r e) -> p h r e", r=32, e=2),
-                in1=s2[:, a, :, :, :].rearrange("p u g e -> p (u g) e").unsqueeze(2).to_broadcast([P, 32, 32, 2]),
+                out=sw[k][:, u, :, :].rearrange("p a (g r e) -> p (a g) r e", r=32, e=2),
+                in0=sg[k][:, u, :, :].rearrange("p a (g r e) -> p (a g) r e", r=32, e=2),
+                in1=s2[:, 2 * k : 2 * k + 2, :, :]
+                .rearrange("p a g e -> p (a g) e")
+                .unsqueeze(2)
+                .to_broadcast([P, 32, 32, 2]),
                 op=ALU.mult,
             )
 
@@ -242,9 +236,8 @@ def tile_groupedstelinear_kernel(tc, x, weight_logits, raw_scales, out):
             tp = ps_t.tile([P, 2, 2, P], F32, name="tp")
             for u in range(2):
                 for a2 in range(2):
-                    lo = u * 512 + c * P
-                    sww = sw[k][:, a2, :].bitcast(F32)
-                    nc.tensor.transpose(tp[:, u, a2, :], sww[:, lo : lo + P], ident[:])
+                    sww = sw[k][:, u, a2, :].bitcast(F32)
+                    nc.tensor.transpose(tp[:, u, a2, :], sww[:, c * P : (c + 1) * P], ident[:])
             tps[("w", k, c)] = tp
 
         def lay_w(k, c, copy=nc.scalar.copy):
@@ -263,13 +256,13 @@ def tile_groupedstelinear_kernel(tc, x, weight_logits, raw_scales, out):
                 in_=wg[k][:, c0:c1, :].rearrange("p c o -> p (c o)"),
             )
 
-        def product(k, q):
-            acc = ps_a.tile([P, 2, 256], F32, name="acc")
-            for mi in range(2):
+        def product(k, q, m0, m1):
+            acc = ps_a.tile([P, m1 - m0, 256], F32, name="acc")
+            for mi in range(m0, m1):
                 m = 2 * q + mi
                 for c in range(NPASS):
                     nc.tensor.matmul_mx(
-                        out=acc[:, mi, :],
+                        out=acc[:, mi - m0, :],
                         lhsT=xc[:, m, c * P : (c + 1) * P].bitcast(FP8X4),
                         lhsT_scale=xs[:, m, c * P : (c + 1) * P],
                         rhs=wc[k][:, c, :].bitcast(FP8X4),
@@ -277,16 +270,16 @@ def tile_groupedstelinear_kernel(tc, x, weight_logits, raw_scales, out):
                         start=(c == 0),
                         stop=(c == NPASS - 1),
                     )
-            accs[(k, q)] = acc
+            accs[(k, q, m0)] = acc
 
-        def empty(k, q):
-            t = obuf.tile([P, 2, 256], F32, name="ob")
-            ob[(k, q)] = t
-            nc.scalar.copy(out=t[:], in_=accs[(k, q)][:])
+        def empty(k, q, m0, m1):
+            t = obuf.tile([P, m1 - m0, 256], F32, name="ob")
+            ob[(k, q, m0)] = t
+            nc.scalar.copy(out=t[:], in_=accs[(k, q, m0)][:])
 
-        def store(k, q):
+        def store(k, q, m0, m1):
             nc.sync.dma_start(
-                out=of[:, 2 * q : 2 * q + 2, k * 256 : (k + 1) * 256], in_=ob[(k, q)][:]
+                out=of[:, 2 * q + m0 : 2 * q + m1, k * 256 : (k + 1) * 256], in_=ob[(k, q, m0)][:]
             )
 
         def pe_x(q):
@@ -299,10 +292,12 @@ def tile_groupedstelinear_kernel(tc, x, weight_logits, raw_scales, out):
                 turn_w(k, c)
                 lay_w(k, c)
 
-        def mul(k, q):
-            product(k, q)
-            empty(k, q)
-            store(k, q)
+        def mul(k, q, parts=1):
+            for i in range(parts):
+                m0, m1 = 2 * i // parts, 2 * (i + 1) // parts
+                product(k, q, m0, m1)
+                empty(k, q, m0, m1)
+                store(k, q, m0, m1)
 
         load_scales(0, 8)
         load_w(0)
@@ -347,71 +342,73 @@ def tile_groupedstelinear_kernel(tc, x, weight_logits, raw_scales, out):
         each(1, (one, two))
         each(2, (one, two))
         sign_w(0)
-        for i in range(9):
+        for i in range(len(one[3])):
             one[3][i]()
-            if i < 9:
+            if i < 7:
                 aside()
             if i == 3:
                 sign_w(1)
         pe_x(0)
         each(0, (three,))
         sign_w(2)
-        scale_w(0)
-        scale_w(1)
-        sign_w(3)
+        scale_w(0, 0)
+        scale_w(0, 1)
         pe_x(1)
         pe_w(0)
-        scale_w(2)
-        aside()
-        scale_w(3)
-        aside()
         quant_x(0)
-        for c in range(4):
-            aside()
-            quant_w(0, c, c + 1)
+        aside()
+        sign_w(3)
+        aside()
+        scale_w(1, 0)
+        aside()
+        quant_w(0, 0, 1)
+        quant_w(0, 1, 2)
+        aside()
+        quant_w(0, 2, 3)
+        quant_w(0, 3, 4)
+        pe_x(2)
+        scale_w(1, 1)
+        aside()
+        mul(0, 0)
+        quant_x(1)
         aside()
         pe_w(1)
         load_w(8)
         load_w(9)
-        pe_x(2)
-        quant_x(1)
+        quant_x(2)
         aside()
-        mul(0, 0)
-        quant_w(1)
+        mul(0, 1)
+        sign_w(4)
+        aside()
+        sign_w(5)
         aside()
         pe_x(3)
-        mul(0, 1)
-        quant_x(2)
+        mul(0, 2)
+        quant_w(1)
         aside()
         mul(1, 0)
         mul(1, 1)
-        sign_w(4)
-        aside()
-        load_w(10)
-        load_w(11)
-        sign_w(5)
+        scale_w(2, 0)
         aside()
         quant_x(3)
         aside()
-        mul(0, 2)
+        load_w(10)
+        load_w(11)
+        scale_w(2, 1)
+        aside()
         mul(1, 2)
-        scale_w(4)
-        aside()
-        scale_w(5)
-        aside()
         mul(0, 3)
-        pe_w(2)
         sign_w(6)
         aside()
         sign_w(7)
         aside()
+        pe_w(2)
         mul(1, 3)
-        scale_w(6)
+        scale_w(3, 0)
         aside()
-        scale_w(7)
+        scale_w(3, 1)
         aside()
         quant_w(2)
-        aside()
         sign_w(8)
         aside()
         sign_w(9)
@@ -423,12 +420,12 @@ def tile_groupedstelinear_kernel(tc, x, weight_logits, raw_scales, out):
             if k + 1 < NK:
                 pe_w(k + 1)
             if k + 2 < NK:
-                if k > 2:
-                    sign_w(2 * k + 4)
-                    sign_w(2 * k + 5)
-                scale_w(2 * k + 4)
-                scale_w(2 * k + 5)
+                scale_w(k + 2, 0)
+                scale_w(k + 2, 1)
             if k + 1 < NK:
                 quant_w(k + 1)
+            if k + 3 < NK:
+                sign_w(2 * k + 6)
+                sign_w(2 * k + 7)
             for q in range(NQ):
-                mul(k, q)
+                mul(k, q, 2 if (k, q) == (NK - 1, NQ - 1) else 1)

@@ -48,7 +48,7 @@ def tile_groupedstelinear_kernel(tc, x, weight_logits, raw_scales, out):
         wsign = ctx.enter_context(tc.tile_pool(name="wsign", bufs=2))
         wscal = ctx.enter_context(tc.tile_pool(name="wscal", bufs=2))
         wgrp = ctx.enter_context(tc.tile_pool(name="wgrp", bufs=2))
-        obuf = ctx.enter_context(tc.tile_pool(name="obuf", bufs=8))
+        obuf = ctx.enter_context(tc.tile_pool(name="obuf", bufs=6))
         ps_t = ctx.enter_context(tc.psum_pool(name="ps_t", bufs=4))
         ps_a = ctx.enter_context(tc.psum_pool(name="ps_a", bufs=4))
         ctx.enter_context(tc.manual_schedule())
@@ -60,8 +60,8 @@ def tile_groupedstelinear_kernel(tc, x, weight_logits, raw_scales, out):
         warm2 = const.tile([P, 1], F32, name="warm2")
         nc.scalar.activation(out=warm2[:], in_=warm[:], func=ACT.Exp)
 
-        sraw = const.tile([P, NG * NG], BF16, name="sraw")
-        s2 = const.tile([P, 16, NG, 2], BF16, name="s2")
+        sraw = const.tile([P, 14 * NG], BF16, name="sraw")
+        s2 = const.tile([P, 14, NG, 2], BF16, name="s2")
 
         xc = keep.tile([P, 8, 512], U32, name="xc", align_bytes=64)
         xs = keep.tile([P, 8, 512], U8, name="xs", align_bytes=64)
@@ -72,6 +72,11 @@ def tile_groupedstelinear_kernel(tc, x, weight_logits, raw_scales, out):
             wsk = keep.tile([P, NPASS, 256], U8, name="ws%d" % k, align_bytes=64)
             wc.append(wck)
             ws.append(wsk)
+
+        s4 = const.tile([P, 8, NG], BF16, name="s4")
+        sq = const.tile([P, 32], BF16, name="sq")
+        t2q = const.tile([P, 32, 2], BF16, name="t2q")
+        tq = keep.tile([P, 2, 8, NPASS, 32], F32, name="tq", align_bytes=64)
 
         xr = {}
         xg = {}
@@ -89,18 +94,16 @@ def tile_groupedstelinear_kernel(tc, x, weight_logits, raw_scales, out):
                 in_=raw_scales.rearrange("(a p) g -> p a g", p=P)[:, a0:a1, :],
             )
 
-        def chain(a0, a1):
-            lo, hi = a0 * NG, a1 * NG
-            v = sraw[:, lo:hi]
+        def chain(v, n, made, tag):
             t = {}
             for name in (
                 "ab", "e0", "q1", "q2", "y1", "y0", "y2", "r1", "rr", "th", "t2", "rx", "xx", "x1",
                 "yr", "a1", "bb", "mm", "rs", "g4", "cr",
             ):
-                tl = chn.tile([P, hi - lo], F32, name="%s_%d" % (name, a0))
+                tl = chn.tile([P, n], F32, name="%s_%s" % (name, tag))
                 t[name] = tl[:]
             for name in ("ni", "p2"):
-                tl = chn.tile([P, hi - lo], I32, name="%s_%d" % (name, a0))
+                tl = chn.tile([P, n], I32, name="%s_%s" % (name, tag))
                 t[name] = tl[:]
 
             def stt(dst, in0, scalar, in1, op0, op1):
@@ -120,11 +123,11 @@ def tile_groupedstelinear_kernel(tc, x, weight_logits, raw_scales, out):
                 nc.scalar.activation(out=t[dst], in_=src, func=func, scale=scale, bias=bias)
 
             def pairs(name):
-                return t[name].unsqueeze(2).to_broadcast([P, hi - lo, 2])
+                return t[name].unsqueeze(2).to_broadcast([P, n, 2])
 
             def fin():
                 nc.vector.scalar_tensor_tensor(
-                    out=s2[:, a0:a1, :, :].rearrange("p a g e -> p (a g) e"),
+                    out=made,
                     in0=pairs("yr"), scalar=2.0, in1=pairs("cr"), op0=ALU.mult, op1=ALU.add,
                 )
 
@@ -163,6 +166,10 @@ def tile_groupedstelinear_kernel(tc, x, weight_logits, raw_scales, out):
                 fin,
             ]
             return guess, reduce_, tables, finish
+
+        def chain_of_tiles(a0, a1):
+            made = s2[:, a0:a1, :, :].rearrange("p a g e -> p (a g) e")
+            return chain(sraw[:, a0 * NG : a1 * NG], (a1 - a0) * NG, made, "t%d" % a0)
 
         def load_x(m):
             q = m // 2
@@ -220,7 +227,7 @@ def tile_groupedstelinear_kernel(tc, x, weight_logits, raw_scales, out):
 
         def scale_w(k, u):
             if k not in sw:
-                t = wscal.tile([P, 2, 2, 1024], BF16, name="sw")
+                t = wscal.tile([P, 2, 2, 1024], BF16, name="sw", align_bytes=64)
                 sw[k] = t
             nc.vector.tensor_tensor(
                 out=sw[k][:, u, :, :].rearrange("p a (g r e) -> p (a g) r e", r=32, e=2),
@@ -254,6 +261,69 @@ def tile_groupedstelinear_kernel(tc, x, weight_logits, raw_scales, out):
                 out=wc[k][:, c0:c1, :].rearrange("p c o -> p (c o)").bitcast(FP8X4),
                 scales=ws[k][:, c0:c1, :].rearrange("p c o -> p (c o)"),
                 in_=wg[k][:, c0:c1, :].rearrange("p c o -> p (c o)"),
+            )
+
+        def load_last_scales():
+            for a in range(4):
+                nc.sync.dma_start(
+                    out=s4[32 * a : 32 * a + 32, :, :],
+                    in_=raw_scales[OUT - 256 : OUT, :].rearrange("(b i) g -> i b g", i=32),
+                )
+
+        def pick_last_scales():
+            for a in range(4):
+                rows = slice(32 * a, 32 * a + 32)
+                nc.gpsimd.tensor_copy(
+                    out=sq[rows, :].rearrange("p (b c) -> p b c", c=NPASS),
+                    in_=s4[rows, :, a:NG:4],
+                )
+
+        def load_last_w(c):
+            if NK - 1 not in wr:
+                t = wraw.tile([P, 8, NPASS, P], BF16, name="wr")
+                wr[NK - 1] = t
+            for a in range(4):
+                lo = (4 * c + a) * P
+                nc.sync.dma_start(
+                    out=wr[NK - 1][32 * a : 32 * a + 32, :, c, :],
+                    in_=wl[OUT - 256 : OUT, lo : lo + P].rearrange("(b i) e -> i b e", i=32),
+                )
+
+        def sign_last():
+            t = wsign.tile([P, 2, 2048], BF16, name="sg")
+            sg[NK - 1] = t
+            nc.vector.tensor_scalar(
+                out=t[:].rearrange("p u (h e) -> p u h e", e=2),
+                in0=wr[NK - 1][:].rearrange("p b c e -> p (b c e)").rearrange("p (h u e) -> p u h e", u=2, e=2),
+                scalar1=0.0,
+                scalar2=0.5,
+                op0=ALU.is_ge,
+                op1=ALU.subtract,
+            )
+
+        def scale_last(u):
+            if NK - 1 not in sw:
+                t = wscal.tile([P, 2, 2048], BF16, name="sw", align_bytes=64)
+                sw[NK - 1] = t
+            nc.vector.tensor_tensor(
+                out=sw[NK - 1][:, u, :].rearrange("p (g r e) -> p g r e", r=32, e=2),
+                in0=sg[NK - 1][:, u, :].rearrange("p (g r e) -> p g r e", r=32, e=2),
+                in1=t2q[:].unsqueeze(2).to_broadcast([P, 32, 32, 2]),
+                op=ALU.mult,
+            )
+
+        def turn_last(u):
+            nc.vector.transpose(
+                tq[:, u, :, :, :].rearrange("p b c i -> p (b c i)"), sw[NK - 1][:, u, :].bitcast(F32)
+            )
+
+        def lay_last(c):
+            if NK - 1 not in wg:
+                t = wgrp.tile([P, NPASS, 1024], BF16, name="wg", align_bytes=64)
+                wg[NK - 1] = t
+            nc.vector.tensor_copy(
+                out=wg[NK - 1][:, c, :].bitcast(F32).rearrange("p (b i u) -> p b i u", i=32, u=2),
+                in_=tq[:, :, :, c, :].rearrange("p u b i -> p b i u"),
             )
 
         def product(k, q, m0, m1):
@@ -305,7 +375,7 @@ def tile_groupedstelinear_kernel(tc, x, weight_logits, raw_scales, out):
         load_x(0)
         load_x(1)
         load_w(2)
-        load_scales(8, 16)
+        load_scales(8, 14)
         load_x(2)
         load_x(3)
         load_w(3)
@@ -317,9 +387,10 @@ def tile_groupedstelinear_kernel(tc, x, weight_logits, raw_scales, out):
         load_w(5)
         load_w(6)
         load_w(7)
-        one = chain(0, 4)
-        two = chain(4, 8)
-        three = chain(8, 16)
+        one = chain_of_tiles(0, 4)
+        two = chain_of_tiles(4, 8)
+        three = chain_of_tiles(8, 14)
+        four = chain(sq[:], 32, t2q[:], "q")
 
         def each(stage, parts):
             for i in range(len(one[stage])):
@@ -329,7 +400,13 @@ def tile_groupedstelinear_kernel(tc, x, weight_logits, raw_scales, out):
         def tables_of_three():
             each(2, (three,))
 
-        later = two[3] + three[1] + [tables_of_three] + three[3]
+        def guess_of_four():
+            each(0, (four,))
+
+        def tables_of_four():
+            each(2, (four,))
+
+        later = two[3] + three[1] + [tables_of_three] + three[3] + [guess_of_four] + four[1] + [tables_of_four] + four[3]
         done = [0]
 
         def aside(n=1):
@@ -375,6 +452,8 @@ def tile_groupedstelinear_kernel(tc, x, weight_logits, raw_scales, out):
         pe_w(1)
         load_w(8)
         load_w(9)
+        load_last_scales()
+        pick_last_scales()
         quant_x(2)
         aside()
         mul(0, 1)
@@ -394,6 +473,8 @@ def tile_groupedstelinear_kernel(tc, x, weight_logits, raw_scales, out):
         aside()
         load_w(10)
         load_w(11)
+        load_w(12)
+        load_w(13)
         scale_w(2, 1)
         aside()
         mul(1, 2)
@@ -402,6 +483,8 @@ def tile_groupedstelinear_kernel(tc, x, weight_logits, raw_scales, out):
         aside()
         sign_w(7)
         aside()
+        for c in range(NPASS):
+            load_last_w(c)
         pe_w(2)
         mul(1, 3)
         scale_w(3, 0)
@@ -412,20 +495,33 @@ def tile_groupedstelinear_kernel(tc, x, weight_logits, raw_scales, out):
         sign_w(8)
         aside()
         sign_w(9)
-        aside(20)
+        aside(2)
         for k in range(2, NK):
-            if k + 4 < NK:
-                load_w(2 * k + 8)
-                load_w(2 * k + 9)
-            if k + 1 < NK:
+            if k + 1 < NK - 1:
                 pe_w(k + 1)
-            if k + 2 < NK:
+            if k + 2 < NK - 1:
                 scale_w(k + 2, 0)
+                aside(2)
                 scale_w(k + 2, 1)
+                aside(2)
+            if k + 2 == NK - 1:
+                scale_last(0)
+                scale_last(1)
             if k + 1 < NK:
                 quant_w(k + 1)
-            if k + 3 < NK:
+                aside(2)
+            if k + 2 == NK - 1:
+                turn_last(0)
+                turn_last(1)
+                for c in range(NPASS):
+                    lay_last(c)
+            if k + 3 < NK - 1:
                 sign_w(2 * k + 6)
+                aside(2)
                 sign_w(2 * k + 7)
+                aside(2)
+            if k + 3 == NK - 1:
+                aside(30)
+                sign_last()
             for q in range(NQ):
                 mul(k, q, 2 if (k, q) == (NK - 1, NQ - 1) else 1)

@@ -23,8 +23,7 @@ NQ = 4
 FLOPS = 2 * TOK * IN * OUT
 
 LOG2E = 1.4426950408889634
-LN2_HI = 0.693145751953125
-LN2_LO = 1.4286068203094172e-06
+LN2 = 0.6931471805599453
 Q1_SCALE = 0.1880921133056114
 Q1_BIAS = -0.4383943121398337
 Q1_ADD = 0.06321998156945995
@@ -97,8 +96,8 @@ def tile_groupedstelinear_kernel(tc, x, weight_logits, raw_scales, out):
         def chain(v, n, made, tag):
             t = {}
             for name in (
-                "ab", "e0", "q1", "q2", "y1", "y0", "y2", "r1", "rr", "th", "t2", "rx", "xx", "x1",
-                "yr", "a1", "bb", "mm", "rs", "g4", "cr",
+                "ab", "e0", "q1", "q2", "y1", "y0", "y2", "rr", "th", "c1", "t2", "rx", "xx", "x1",
+                "yr", "a1", "pp", "qq", "rs", "g4", "cr",
             ):
                 tl = chn.tile([P, n], F32, name="%s_%s" % (name, tag))
                 t[name] = tl[:]
@@ -139,14 +138,14 @@ def tile_groupedstelinear_kernel(tc, x, weight_logits, raw_scales, out):
             ]
             reduce_ = [
                 lambda: tsc("ni", "ab", -LOG2E, -120.0, ALU.mult, ALU.max),
-                lambda: stt("r1", "ni", -LN2_HI, t["ab"], ALU.mult, ALU.subtract),
-                lambda: stt("rr", "ni", -LN2_LO, t["r1"], ALU.mult, ALU.add),
+                lambda: stt("rr", "ni", -LN2, t["ab"], ALU.mult, ALU.subtract),
                 lambda: stt("y1", "q1", Q1_ADD, t["e0"], ALU.add, ALU.mult),
                 lambda: tsc("p2", "ni", 127.0, 8388608.0, ALU.add, ALU.mult),
                 lambda: stt("y0", "q2", Q2_ADD, t["y1"], ALU.add, ALU.mult),
             ]
             tables = [
                 lambda: act("th", t["rr"], ACT.Tanh, scale=0.5),
+                lambda: act("c1", t["th"], ACT.Identity, scale=-2.0, bias=2.0),
                 lambda: act("rx", t["rr"], ACT.Exp),
                 lambda: act("t2", t["y0"], ACT.Tanh, scale=0.5),
                 lambda: act("xx", t["y0"], ACT.Exp, scale=-1.0),
@@ -155,10 +154,10 @@ def tile_groupedstelinear_kernel(tc, x, weight_logits, raw_scales, out):
             ]
             finish = [
                 lambda: stt("a1", "th", 1.0, t["p2"].bitcast(F32), ALU.add, ALU.mult),
-                lambda: stt("bb", "th", -2.0, t["a1"], ALU.mult, ALU.add),
-                lambda: stt("mm", "bb", 2.0, t["t2"], ALU.add, ALU.mult),
-                lambda: ttt("rs", "mm", "a1", ALU.subtract),
+                lambda: ttt("qq", "c1", "t2", ALU.mult),
+                lambda: stt("pp", "t2", 1.0, t["a1"], ALU.subtract, ALU.mult),
                 lambda: stt("g4", "rx", 1.0, t["x1"], ALU.add, ALU.mult),
+                lambda: ttt("rs", "pp", "qq", ALU.add),
                 lambda: nc.vector.scalar_tensor_tensor(
                     out=t["yr"], in0=v, scalar=0.0, in1=t["y2"], op0=ALU.max, op1=ALU.add
                 ),
@@ -219,6 +218,18 @@ def tile_groupedstelinear_kernel(tc, x, weight_logits, raw_scales, out):
             nc.vector.tensor_scalar(
                 out=sg[k][:, :, a % 2, :].rearrange("p u (q e) -> p u q e", e=2),
                 in0=wr[k][:, a % 2, :].rearrange("p (q u e) -> p u q e", u=2, e=2),
+                scalar1=0.0,
+                scalar2=0.5,
+                op0=ALU.is_ge,
+                op1=ALU.subtract,
+            )
+
+        def sign_pair(k):
+            t = wsign.tile([P, 2, 2, 1024], BF16, name="sg")
+            sg[k] = t
+            nc.vector.tensor_scalar(
+                out=t[:].rearrange("p u a (q e) -> p u (a q) e", e=2),
+                in0=wr[k][:].rearrange("p a (q u e) -> p u (a q) e", u=2, e=2),
                 scalar1=0.0,
                 scalar2=0.5,
                 op0=ALU.is_ge,
@@ -369,15 +380,15 @@ def tile_groupedstelinear_kernel(tc, x, weight_logits, raw_scales, out):
                 empty(k, q, m0, m1)
                 store(k, q, m0, m1)
 
-        load_scales(0, 8)
+        load_scales(0, 4)
+        load_scales(4, 14)
         load_w(0)
         load_w(1)
         load_x(0)
         load_x(1)
-        load_w(2)
-        load_scales(8, 14)
         load_x(2)
         load_x(3)
+        load_w(2)
         load_w(3)
         load_x(4)
         load_x(5)
@@ -388,8 +399,7 @@ def tile_groupedstelinear_kernel(tc, x, weight_logits, raw_scales, out):
         load_w(6)
         load_w(7)
         one = chain_of_tiles(0, 4)
-        two = chain_of_tiles(4, 8)
-        three = chain_of_tiles(8, 14)
+        two = chain_of_tiles(4, 14)
         four = chain(sq[:], 32, t2q[:], "q")
 
         def each(stage, parts):
@@ -397,16 +407,13 @@ def tile_groupedstelinear_kernel(tc, x, weight_logits, raw_scales, out):
                 for part in parts:
                     part[stage][i]()
 
-        def tables_of_three():
-            each(2, (three,))
-
         def guess_of_four():
             each(0, (four,))
 
         def tables_of_four():
             each(2, (four,))
 
-        later = two[3] + three[1] + [tables_of_three] + three[3] + [guess_of_four] + four[1] + [tables_of_four] + four[3]
+        later = two[3] + [guess_of_four] + four[1] + [tables_of_four] + four[3]
         done = [0]
 
         def aside(n=1):
@@ -417,109 +424,90 @@ def tile_groupedstelinear_kernel(tc, x, weight_logits, raw_scales, out):
 
         each(0, (one, two))
         each(1, (one, two))
-        each(2, (one, two))
+        each(2, (one,))
         sign_w(0)
+        each(2, (two,))
         for i in range(len(one[3])):
             one[3][i]()
-            if i < 7:
+            if i >= 5:
                 aside()
             if i == 3:
                 sign_w(1)
         pe_x(0)
-        each(0, (three,))
-        sign_w(2)
-        scale_w(0, 0)
-        scale_w(0, 1)
         pe_x(1)
+        scale_w(0, 0)
+        aside(1)
+        scale_w(0, 1)
         pe_w(0)
         quant_x(0)
-        aside()
+        sign_w(2)
+        aside(1)
         sign_w(3)
-        aside()
-        scale_w(1, 0)
-        aside()
         quant_w(0, 0, 1)
         quant_w(0, 1, 2)
-        aside()
         quant_w(0, 2, 3)
         quant_w(0, 3, 4)
         pe_x(2)
-        scale_w(1, 1)
-        aside()
         mul(0, 0)
         quant_x(1)
+        pe_x(3)
+        scale_w(1, 0)
+        scale_w(1, 1)
         aside()
         pe_w(1)
+        mul(0, 1)
+        quant_x(2)
+        aside()
         load_w(8)
         load_w(9)
         load_last_scales()
         pick_last_scales()
-        quant_x(2)
-        aside()
-        mul(0, 1)
-        sign_w(4)
-        aside()
-        sign_w(5)
-        aside()
-        pe_x(3)
+        quant_x(3)
         mul(0, 2)
-        quant_w(1)
+        mul(0, 3)
         aside()
+        sign_pair(2)
+        quant_w(1)
         mul(1, 0)
         mul(1, 1)
-        scale_w(2, 0)
-        aside()
-        quant_x(3)
-        aside()
         load_w(10)
         load_w(11)
         load_w(12)
         load_w(13)
+        scale_w(2, 0)
         scale_w(2, 1)
-        aside()
+        pe_w(2)
         mul(1, 2)
-        mul(0, 3)
-        sign_w(6)
-        aside()
-        sign_w(7)
-        aside()
+        mul(1, 3)
+        sign_pair(3)
         for c in range(NPASS):
             load_last_w(c)
-        pe_w(2)
-        mul(1, 3)
         scale_w(3, 0)
-        aside()
         scale_w(3, 1)
-        aside()
         quant_w(2)
-        sign_w(8)
-        aside()
-        sign_w(9)
-        aside(2)
+        sign_pair(4)
         for k in range(2, NK):
             if k + 1 < NK - 1:
                 pe_w(k + 1)
             if k + 2 < NK - 1:
                 scale_w(k + 2, 0)
-                aside(2)
+                aside()
                 scale_w(k + 2, 1)
-                aside(2)
+                aside()
             if k + 2 == NK - 1:
                 scale_last(0)
                 scale_last(1)
             if k + 1 < NK:
                 quant_w(k + 1)
-                aside(2)
+                aside()
             if k + 2 == NK - 1:
                 turn_last(0)
                 turn_last(1)
                 for c in range(NPASS):
                     lay_last(c)
             if k + 3 < NK - 1:
-                sign_w(2 * k + 6)
-                aside(2)
-                sign_w(2 * k + 7)
-                aside(2)
+                sign_pair(k + 3)
+                aside()
             if k + 3 == NK - 1:
                 aside(30)
                 sign_last()

@@ -59,8 +59,8 @@ def tile_groupedstelinear_kernel(tc, x, weight_logits, raw_scales, out):
         warm2 = const.tile([P, 1], F32, name="warm2")
         nc.scalar.activation(out=warm2[:], in_=warm[:], func=ACT.Exp)
 
-        sraw = const.tile([P, 14 * NG], BF16, name="sraw")
-        s2 = const.tile([P, 14, NG, 2], BF16, name="s2")
+        sraw = const.tile([P, 10 * NG], BF16, name="sraw")
+        s2 = const.tile([P, 10, NG, 2], BF16, name="s2")
 
         xc = keep.tile([P, 8, 512], U32, name="xc", align_bytes=64)
         xs = keep.tile([P, 8, 512], U8, name="xs", align_bytes=64)
@@ -73,8 +73,8 @@ def tile_groupedstelinear_kernel(tc, x, weight_logits, raw_scales, out):
             ws.append(wsk)
 
         s4 = const.tile([P, 8, NG], BF16, name="s4")
-        sq = const.tile([P, 32], BF16, name="sq")
-        t2q = const.tile([P, 32, 2], BF16, name="t2q")
+        sq = const.tile([P, 96], BF16, name="sq")
+        t2q = const.tile([P, 96, 2], BF16, name="t2q")
         tq = keep.tile([P, 2, 8, NPASS, 32], F32, name="tq", align_bytes=64)
 
         xr = {}
@@ -96,7 +96,7 @@ def tile_groupedstelinear_kernel(tc, x, weight_logits, raw_scales, out):
         def chain(v, n, made, tag):
             t = {}
             for name in (
-                "ab", "e0", "q1", "q2", "y1", "y0", "y2", "rr", "th", "c1", "t2", "rx", "xx", "x1",
+                "ab", "e0", "q1", "q2", "y1", "y0", "y2", "rr", "th", "t2", "rx", "xx", "x1",
                 "yr", "a1", "pp", "qq", "rs", "g4", "cr",
             ):
                 tl = chn.tile([P, n], F32, name="%s_%s" % (name, tag))
@@ -140,24 +140,23 @@ def tile_groupedstelinear_kernel(tc, x, weight_logits, raw_scales, out):
                 lambda: tsc("ni", "ab", -LOG2E, -120.0, ALU.mult, ALU.max),
                 lambda: stt("rr", "ni", -LN2, t["ab"], ALU.mult, ALU.subtract),
                 lambda: stt("y1", "q1", Q1_ADD, t["e0"], ALU.add, ALU.mult),
-                lambda: tsc("p2", "ni", 127.0, 8388608.0, ALU.add, ALU.mult),
+                lambda: tsc("p2", "ni", 126.0, 8388608.0, ALU.add, ALU.mult),
                 lambda: stt("y0", "q2", Q2_ADD, t["y1"], ALU.add, ALU.mult),
             ]
             tables = [
                 lambda: act("th", t["rr"], ACT.Tanh, scale=0.5),
-                lambda: act("c1", t["th"], ACT.Identity, scale=-2.0, bias=2.0),
                 lambda: act("rx", t["rr"], ACT.Exp),
                 lambda: act("t2", t["y0"], ACT.Tanh, scale=0.5),
                 lambda: act("xx", t["y0"], ACT.Exp, scale=-1.0),
                 lambda: act("y2", t["y0"], ACT.Identity, bias=1e-6),
-                lambda: act("x1", t["xx"], ACT.Identity, scale=-0.5, bias=-0.5),
+                lambda: act("x1", t["xx"], ACT.Identity, bias=1.0),
             ]
             finish = [
                 lambda: stt("a1", "th", 1.0, t["p2"].bitcast(F32), ALU.add, ALU.mult),
-                lambda: ttt("qq", "c1", "t2", ALU.mult),
+                lambda: stt("qq", "th", 1.0, t["t2"], ALU.subtract, ALU.mult),
                 lambda: stt("pp", "t2", 1.0, t["a1"], ALU.subtract, ALU.mult),
                 lambda: stt("g4", "rx", 1.0, t["x1"], ALU.add, ALU.mult),
-                lambda: ttt("rs", "pp", "qq", ALU.add),
+                lambda: ttt("rs", "qq", "pp", ALU.subtract),
                 lambda: nc.vector.scalar_tensor_tensor(
                     out=t["yr"], in0=v, scalar=0.0, in1=t["y2"], op0=ALU.max, op1=ALU.add
                 ),
@@ -236,6 +235,12 @@ def tile_groupedstelinear_kernel(tc, x, weight_logits, raw_scales, out):
                 op1=ALU.subtract,
             )
 
+        def scales_of(k):
+            if k >= 5:
+                lo = (2 * k - 10) * NG
+                return t2q[:, lo : lo + 32, :]
+            return s2[:, 2 * k : 2 * k + 2, :, :].rearrange("p a g e -> p (a g) e")
+
         def scale_w(k, u):
             if k not in sw:
                 t = wscal.tile([P, 2, 2, 1024], BF16, name="sw", align_bytes=64)
@@ -243,10 +248,7 @@ def tile_groupedstelinear_kernel(tc, x, weight_logits, raw_scales, out):
             nc.vector.tensor_tensor(
                 out=sw[k][:, u, :, :].rearrange("p a (g r e) -> p (a g) r e", r=32, e=2),
                 in0=sg[k][:, u, :, :].rearrange("p a (g r e) -> p (a g) r e", r=32, e=2),
-                in1=s2[:, 2 * k : 2 * k + 2, :, :]
-                .rearrange("p a g e -> p (a g) e")
-                .unsqueeze(2)
-                .to_broadcast([P, 32, 32, 2]),
+                in1=scales_of(k).unsqueeze(2).to_broadcast([P, 32, 32, 2]),
                 op=ALU.mult,
             )
 
@@ -275,6 +277,10 @@ def tile_groupedstelinear_kernel(tc, x, weight_logits, raw_scales, out):
             )
 
         def load_last_scales():
+            nc.sync.dma_start(
+                out=sq[:, 0:64].rearrange("p (a g) -> p a g", g=NG),
+                in_=raw_scales.rearrange("(a p) g -> p a g", p=P)[:, 10:14, :],
+            )
             for a in range(4):
                 nc.sync.dma_start(
                     out=s4[32 * a : 32 * a + 32, :, :],
@@ -285,7 +291,7 @@ def tile_groupedstelinear_kernel(tc, x, weight_logits, raw_scales, out):
             for a in range(4):
                 rows = slice(32 * a, 32 * a + 32)
                 nc.gpsimd.tensor_copy(
-                    out=sq[rows, :].rearrange("p (b c) -> p b c", c=NPASS),
+                    out=sq[rows, 64:96].rearrange("p (b c) -> p b c", c=NPASS),
                     in_=s4[rows, :, a:NG:4],
                 )
 
@@ -319,7 +325,7 @@ def tile_groupedstelinear_kernel(tc, x, weight_logits, raw_scales, out):
             nc.vector.tensor_tensor(
                 out=sw[NK - 1][:, u, :].rearrange("p (g r e) -> p g r e", r=32, e=2),
                 in0=sg[NK - 1][:, u, :].rearrange("p (g r e) -> p g r e", r=32, e=2),
-                in1=t2q[:].unsqueeze(2).to_broadcast([P, 32, 32, 2]),
+                in1=t2q[:, 64:96, :].unsqueeze(2).to_broadcast([P, 32, 32, 2]),
                 op=ALU.mult,
             )
 
@@ -381,16 +387,16 @@ def tile_groupedstelinear_kernel(tc, x, weight_logits, raw_scales, out):
                 store(k, q, m0, m1)
 
         load_scales(0, 4)
-        load_scales(4, 14)
+        load_scales(4, 10)
         load_w(0)
-        load_w(1)
         load_x(0)
+        load_w(1)
         load_x(1)
         load_x(2)
         load_x(3)
         load_w(2)
-        load_w(3)
         load_x(4)
+        load_w(3)
         load_x(5)
         load_x(6)
         load_x(7)
@@ -399,8 +405,8 @@ def tile_groupedstelinear_kernel(tc, x, weight_logits, raw_scales, out):
         load_w(6)
         load_w(7)
         one = chain_of_tiles(0, 4)
-        two = chain_of_tiles(4, 14)
-        four = chain(sq[:], 32, t2q[:], "q")
+        two = chain_of_tiles(4, 10)
+        four = chain(sq[:], 96, t2q[:], "q")
 
         def each(stage, parts):
             for i in range(len(one[stage])):
@@ -443,10 +449,8 @@ def tile_groupedstelinear_kernel(tc, x, weight_logits, raw_scales, out):
         sign_w(2)
         aside(1)
         sign_w(3)
-        quant_w(0, 0, 1)
-        quant_w(0, 1, 2)
-        quant_w(0, 2, 3)
-        quant_w(0, 3, 4)
+        quant_w(0, 0, 2)
+        quant_w(0, 2, 4)
         pe_x(2)
         mul(0, 0)
         quant_x(1)
@@ -485,21 +489,23 @@ def tile_groupedstelinear_kernel(tc, x, weight_logits, raw_scales, out):
         scale_w(3, 0)
         scale_w(3, 1)
         quant_w(2)
+        aside(2)
         sign_pair(4)
+        aside(2)
         for k in range(2, NK):
             if k + 1 < NK - 1:
                 pe_w(k + 1)
             if k + 2 < NK - 1:
                 scale_w(k + 2, 0)
-                aside()
+                aside(3)
                 scale_w(k + 2, 1)
-                aside()
+                aside(3)
             if k + 2 == NK - 1:
                 scale_last(0)
                 scale_last(1)
             if k + 1 < NK:
                 quant_w(k + 1)
-                aside()
+                aside(3)
             if k + 2 == NK - 1:
                 turn_last(0)
                 turn_last(1)
@@ -507,7 +513,7 @@ def tile_groupedstelinear_kernel(tc, x, weight_logits, raw_scales, out):
                     lay_last(c)
             if k + 3 < NK - 1:
                 sign_pair(k + 3)
-                aside()
+                aside(3)
             if k + 3 == NK - 1:
                 aside(30)
                 sign_last()

from contextlib import ExitStack

import concourse.mybir as mybir
from concourse.masks import make_identity

F32 = mybir.dt.float32
BF16 = mybir.dt.bfloat16
I32 = mybir.dt.int32
U8 = mybir.dt.uint8
U32 = mybir.dt.uint32
FP8X4 = mybir.dt.float8_e4m3fn_x4
ALU = mybir.AluOpType
ACT = mybir.ActivationFunctionType

P = 128
TOK = 1024
IN = 2048
OUT = 2048
NG = 16
NPASS = 4
NK = 8
NQ = 4
FLOPS = 2 * TOK * IN * OUT

LOG2E = 1.4426950408889634
LN2 = 0.6931471805599453
Q1_SCALE = 0.1880921133056114
Q1_BIAS = -0.4383943121398337
Q1_ADD = 0.06321998156945995
Q2_BIAS = 0.2963586866440234
Q2_ADD = 3.826385480469501


def tile_groupedstelinear_kernel(tc, x, weight_logits, raw_scales, out):
    nc = tc.nc
    xf = x.flatten_outer_dims()
    of = out.flatten_outer_dims().rearrange("(m p) o -> p m o", p=P)
    wl = weight_logits

    with ExitStack() as ctx:
        const = ctx.enter_context(tc.tile_pool(name="const", bufs=1))
        chn = ctx.enter_context(tc.tile_pool(name="chn", bufs=1))
        keep = ctx.enter_context(tc.tile_pool(name="keep", bufs=1))
        xraw = ctx.enter_context(tc.tile_pool(name="xraw", bufs=4))
        xgrp = ctx.enter_context(tc.tile_pool(name="xgrp", bufs=2))
        wraw = ctx.enter_context(tc.tile_pool(name="wraw", bufs=4))
        wsign = ctx.enter_context(tc.tile_pool(name="wsign", bufs=2))
        wscal = ctx.enter_context(tc.tile_pool(name="wscal", bufs=2))
        wgrp = ctx.enter_context(tc.tile_pool(name="wgrp", bufs=2))
        obuf = ctx.enter_context(tc.tile_pool(name="obuf", bufs=6))
        ps_t = ctx.enter_context(tc.psum_pool(name="ps_t", bufs=4))
        ps_a = ctx.enter_context(tc.psum_pool(name="ps_a", bufs=4))
        ctx.enter_context(tc.manual_schedule())

        ident = const.tile([P, P], F32, name="ident")
        make_identity(nc, ident[:])
        warm = const.tile([P, 1], F32, name="warm")
        nc.vector.memset(warm[:], 0.0)
        warm2 = const.tile([P, 1], F32, name="warm2")
        nc.scalar.activation(out=warm2[:], in_=warm[:], func=ACT.Exp)

        sraw = const.tile([P, 10 * NG], BF16, name="sraw")
        s2 = const.tile([P, 10, NG, 2], BF16, name="s2")

        xc = keep.tile([P, 8, 512], U32, name="xc", align_bytes=64)
        xs = keep.tile([P, 8, 512], U8, name="xs", align_bytes=64)
        wc = []
        ws = []
        for k in range(NK):
            wck = keep.tile([P, NPASS, 256], U32, name="wc%d" % k, align_bytes=64)
            wsk = keep.tile([P, NPASS, 256], U8, name="ws%d" % k, align_bytes=64)
            wc.append(wck)
            ws.append(wsk)

        s4 = const.tile([P, 8, NG], BF16, name="s4")
        sq = const.tile([P, 96], BF16, name="sq")
        t2q = const.tile([P, 96, 2], BF16, name="t2q")
        tq = keep.tile([P, 2, 8, NPASS, 32], F32, name="tq", align_bytes=64)

        xr = {}
        xg = {}
        wr = {}
        sg = {}
        sw = {}
        wg = {}
        ob = {}
        tps = {}
        accs = {}

        def load_scales(a0, a1):
            nc.sync.dma_start(
                out=sraw[:, a0 * NG : a1 * NG].rearrange("p (a g) -> p a g", g=NG),
                in_=raw_scales.rearrange("(a p) g -> p a g", p=P)[:, a0:a1, :],
            )

        def chain(v, n, made, tag):
            t = {}
            for name in (
                "ab", "e0", "q1", "q2", "y1", "y0", "y2", "rr", "th", "t2", "rx", "xx", "x1",
                "yr", "a1", "pp", "qq", "rs", "g4", "cr",
            ):
                tl = chn.tile([P, n], F32, name="%s_%s" % (name, tag))
                t[name] = tl[:]
            for name in ("ni", "p2"):
                tl = chn.tile([P, n], I32, name="%s_%s" % (name, tag))
                t[name] = tl[:]

            def stt(dst, in0, scalar, in1, op0, op1):
                nc.vector.scalar_tensor_tensor(
                    out=t[dst], in0=t[in0], scalar=scalar, in1=in1, op0=op0, op1=op1
                )

            def tsc(dst, in0, s1, s2_, op0, op1):
                nc.vector.tensor_scalar(
                    out=t[dst], in0=t[in0], scalar1=s1, scalar2=s2_, op0=op0, op1=op1
                )

            def ttt(dst, in0, in1, op):
                nc.vector.tensor_tensor(out=t[dst], in0=t[in0], in1=t[in1], op=op)

            def act(dst, src, func, scale=1.0, bias=0.0):
                nc.scalar.activation(out=t[dst], in_=src, func=func, scale=scale, bias=bias)

            def pairs(name):
                return t[name].unsqueeze(2).to_broadcast([P, n, 2])

            def fin():
                nc.vector.scalar_tensor_tensor(
                    out=made,
                    in0=pairs("yr"), scalar=2.0, in1=pairs("cr"), op0=ALU.mult, op1=ALU.add,
                )

            guess = [
                lambda: act("ab", v, ACT.Abs),
                lambda: act("e0", t["ab"], ACT.Exp, scale=-1.0),
                lambda: act("q1", t["e0"], ACT.Square, scale=Q1_SCALE, bias=Q1_BIAS),
                lambda: act("q2", t["e0"], ACT.Square, bias=Q2_BIAS),
            ]
            reduce_ = [
                lambda: tsc("ni", "ab", -LOG2E, -120.0, ALU.mult, ALU.max),
                lambda: stt("rr", "ni", -LN2, t["ab"], ALU.mult, ALU.subtract),
                lambda: stt("y1", "q1", Q1_ADD, t["e0"], ALU.add, ALU.mult),
                lambda: tsc("p2", "ni", 126.0, 8388608.0, ALU.add, ALU.mult),
                lambda: stt("y0", "q2", Q2_ADD, t["y1"], ALU.add, ALU.mult),
            ]
            tables = [
                lambda: act("th", t["rr"], ACT.Tanh, scale=0.5),
                lambda: act("rx", t["rr"], ACT.Exp),
                lambda: act("t2", t["y0"], ACT.Tanh, scale=0.5),
                lambda: act("xx", t["y0"], ACT.Exp, scale=-1.0),
                lambda: act("y2", t["y0"], ACT.Identity, bias=1e-6),
                lambda: act("x1", t["xx"], ACT.Identity, bias=1.0),
            ]
            finish = [
                lambda: stt("a1", "th", 1.0, t["p2"].bitcast(F32), ALU.add, ALU.mult),
                lambda: stt("qq", "th", 1.0, t["t2"], ALU.subtract, ALU.mult),
                lambda: stt("pp", "t2", 1.0, t["a1"], ALU.subtract, ALU.mult),
                lambda: stt("g4", "rx", 1.0, t["x1"], ALU.add, ALU.mult),
                lambda: ttt("rs", "qq", "pp", ALU.subtract),
                lambda: nc.vector.scalar_tensor_tensor(
                    out=t["yr"], in0=v, scalar=0.0, in1=t["y2"], op0=ALU.max, op1=ALU.add
                ),
                lambda: ttt("cr", "rs", "g4", ALU.mult),
                fin,
            ]
            return guess, reduce_, tables, finish

        def chain_of_tiles(a0, a1):
            made = s2[:, a0:a1, :, :].rearrange("p a g e -> p (a g) e")
            return chain(sraw[:, a0 * NG : a1 * NG], (a1 - a0) * NG, made, "t%d" % a0)

        def load_x(m):
            q = m // 2
            if q not in xr:
                t = xraw.tile([P, 2, IN], BF16, name="xr")
                xr[q] = t
            nc.sync.dma_start(out=xr[q][:, m % 2, :], in_=xf[m * P : (m + 1) * P, :])

        def turn_x(q, b):
            tp = ps_t.tile([P, 2, 2, P], F32, name="tp")
            xw = xr[q][:, b // 2, :].bitcast(F32)
            for ci in range(2):
                for u in range(2):
                    lo = (2 * (b % 2) + ci) * 256
                    nc.tensor.transpose(tp[:, ci, u, :], xw[:, lo + u : lo + 256 : 2], ident[:])
            tps[("x", q, b)] = tp

        def lay_x(q, b, copy=nc.scalar.copy):
            if q not in xg:
                t = xgrp.tile([P, 2 * IN], BF16, name="xg", align_bytes=64)
                xg[q] = t
            xgw = xg[q][:].bitcast(F32).rearrange("p (c r u) -> p c r u", c=2 * NPASS, u=2)
            copy(
                out=xgw[:, 2 * b : 2 * b + 2, :, :],
                in_=tps[("x", q, b)][:].rearrange("p c u r -> p c r u"),
            )

        def quant_x(q):
            nc.vector.quantize_mx(
                out=xc[:, 2 * q : 2 * q + 2, :].rearrange("p a b -> p (a b)").bitcast(FP8X4),
                scales=xs[:, 2 * q : 2 * q + 2, :].rearrange("p a b -> p (a b)"),
                in_=xg[q][:],
            )

        def load_w(a):
            k = a // 2
            if k not in wr:
                t = wraw.tile([P, 2, IN], BF16, name="wr")
                wr[k] = t
            nc.sync.dma_start(out=wr[k][:, a % 2, :], in_=wl[a * P : (a + 1) * P, :])

        def sign_w(a):
            k = a // 2
            if k not in sg:
                t = wsign.tile([P, 2, 2, 1024], BF16, name="sg")
                sg[k] = t
            nc.vector.tensor_scalar(
                out=sg[k][:, :, a % 2, :].rearrange("p u (q e) -> p u q e", e=2),
                in0=wr[k][:, a % 2, :].rearrange("p (q u e) -> p u q e", u=2, e=2),
                scalar1=0.0,
                scalar2=0.5,
                op0=ALU.is_ge,
                op1=ALU.subtract,
            )

        def sign_pair(k):
            t = wsign.tile([P, 2, 2, 1024], BF16, name="sg")
            sg[k] = t
            nc.vector.tensor_scalar(
                out=t[:].rearrange("p u a (q e) -> p u (a q) e", e=2),
                in0=wr[k][:].rearrange("p a (q u e) -> p u (a q) e", u=2, e=2),
                scalar1=0.0,
                scalar2=0.5,
                op0=ALU.is_ge,
                op1=ALU.subtract,
            )

        def scales_of(k):
            if k >= 5:
                lo = (2 * k - 10) * NG
                return t2q[:, lo : lo + 32, :]
            return s2[:, 2 * k : 2 * k + 2, :, :].rearrange("p a g e -> p (a g) e")

        def scale_w(k, u):
            if k not in sw:
                t = wscal.tile([P, 2, 2, 1024], BF16, name="sw", align_bytes=64)
                sw[k] = t
            nc.vector.tensor_tensor(
                out=sw[k][:, u, :, :].rearrange("p a (g r e) -> p (a g) r e", r=32, e=2),
                in0=sg[k][:, u, :, :].rearrange("p a (g r e) -> p (a g) r e", r=32, e=2),
                in1=scales_of(k).unsqueeze(2).to_broadcast([P, 32, 32, 2]),
                op=ALU.mult,
            )

        def turn_w(k, c):
            tp = ps_t.tile([P, 2, 2, P], F32, name="tp")
            for u in range(2):
                for a2 in range(2):
                    sww = sw[k][:, u, a2, :].bitcast(F32)
                    nc.tensor.transpose(tp[:, u, a2, :], sww[:, c * P : (c + 1) * P], ident[:])
            tps[("w", k, c)] = tp

        def lay_w(k, c, copy=nc.scalar.copy):
            if k not in wg:
                t = wgrp.tile([P, NPASS, 1024], BF16, name="wg", align_bytes=64)
                wg[k] = t
            copy(
                out=wg[k][:, c, :].bitcast(F32).rearrange("p (o u) -> p o u", u=2),
                in_=tps[("w", k, c)][:].rearrange("p u a o -> p (a o) u"),
            )

        def quant_w(k, c0=0, c1=NPASS):
            nc.vector.quantize_mx(
                out=wc[k][:, c0:c1, :].rearrange("p c o -> p (c o)").bitcast(FP8X4),
                scales=ws[k][:, c0:c1, :].rearrange("p c o -> p (c o)"),
                in_=wg[k][:, c0:c1, :].rearrange("p c o -> p (c o)"),
            )

        def load_last_scales():
            nc.sync.dma_start(
                out=sq[:, 0:64].rearrange("p (a g) -> p a g", g=NG),
                in_=raw_scales.rearrange("(a p) g -> p a g", p=P)[:, 10:14, :],
            )
            for a in range(4):
                nc.sync.dma_start(
                    out=s4[32 * a : 32 * a + 32, :, :],
                    in_=raw_scales[OUT - 256 : OUT, :].rearrange("(b i) g -> i b g", i=32),
                )

        def pick_last_scales():
            for a in range(4):
                rows = slice(32 * a, 32 * a + 32)
                nc.gpsimd.tensor_copy(
                    out=sq[rows, 64:96].rearrange("p (b c) -> p b c", c=NPASS),
                    in_=s4[rows, :, a:NG:4],
                )

        def load_last_w(c):
            if NK - 1 not in wr:
                t = wraw.tile([P, 8, NPASS, P], BF16, name="wr")
                wr[NK - 1] = t
            for a in range(4):
                lo = (4 * c + a) * P
                nc.sync.dma_start(
                    out=wr[NK - 1][32 * a : 32 * a + 32, :, c, :],
                    in_=wl[OUT - 256 : OUT, lo : lo + P].rearrange("(b i) e -> i b e", i=32),
                )

        def sign_last():
            t = wsign.tile([P, 2, 2048], BF16, name="sg")
            sg[NK - 1] = t
            nc.vector.tensor_scalar(
                out=t[:].rearrange("p u (h e) -> p u h e", e=2),
                in0=wr[NK - 1][:].rearrange("p b c e -> p (b c e)").rearrange("p (h u e) -> p u h e", u=2, e=2),
                scalar1=0.0,
                scalar2=0.5,
                op0=ALU.is_ge,
                op1=ALU.subtract,
            )

        def scale_last(u):
            if NK - 1 not in sw:
                t = wscal.tile([P, 2, 2048], BF16, name="sw", align_bytes=64)
                sw[NK - 1] = t
            nc.vector.tensor_tensor(
                out=sw[NK - 1][:, u, :].rearrange("p (g r e) -> p g r e", r=32, e=2),
                in0=sg[NK - 1][:, u, :].rearrange("p (g r e) -> p g r e", r=32, e=2),
                in1=t2q[:, 64:96, :].unsqueeze(2).to_broadcast([P, 32, 32, 2]),
                op=ALU.mult,
            )

        def turn_last(u):
            nc.vector.transpose(
                tq[:, u, :, :, :].rearrange("p b c i -> p (b c i)"), sw[NK - 1][:, u, :].bitcast(F32)
            )

        def lay_last(c):
            if NK - 1 not in wg:
                t = wgrp.tile([P, NPASS, 1024], BF16, name="wg", align_bytes=64)
                wg[NK - 1] = t
            nc.vector.tensor_copy(
                out=wg[NK - 1][:, c, :].bitcast(F32).rearrange("p (b i u) -> p b i u", i=32, u=2),
                in_=tq[:, :, :, c, :].rearrange("p u b i -> p b i u"),
            )

        def product(k, q, m0, m1):
            acc = ps_a.tile([P, m1 - m0, 256], F32, name="acc")
            for mi in range(m0, m1):
                m = 2 * q + mi
                for c in range(NPASS):
                    nc.tensor.matmul_mx(
                        out=acc[:, mi - m0, :],
                        lhsT=xc[:, m, c * P : (c + 1) * P].bitcast(FP8X4),
                        lhsT_scale=xs[:, m, c * P : (c + 1) * P],
                        rhs=wc[k][:, c, :].bitcast(FP8X4),
                        rhs_scale=ws[k][:, c, :],
                        start=(c == 0),
                        stop=(c == NPASS - 1),
                    )
            accs[(k, q, m0)] = acc

        def empty(k, q, m0, m1):
            t = obuf.tile([P, m1 - m0, 256], F32, name="ob")
            ob[(k, q, m0)] = t
            nc.scalar.copy(out=t[:], in_=accs[(k, q, m0)][:])

        def store(k, q, m0, m1):
            nc.sync.dma_start(
                out=of[:, 2 * q + m0 : 2 * q + m1, k * 256 : (k + 1) * 256], in_=ob[(k, q, m0)][:]
            )

        def pe_x(q):
            for b in range(4):
                turn_x(q, b)
                lay_x(q, b)

        def pe_w(k):
            for c in range(NPASS):
                turn_w(k, c)
                lay_w(k, c)

        def mul(k, q, parts=1):
            for i in range(parts):
                m0, m1 = 2 * i // parts, 2 * (i + 1) // parts
                product(k, q, m0, m1)
                empty(k, q, m0, m1)
                store(k, q, m0, m1)

        load_scales(0, 4)
        load_scales(4, 10)
        load_w(0)
        load_x(0)
        load_w(1)
        load_x(1)
        load_x(2)
        load_x(3)
        load_w(2)
        load_x(4)
        load_w(3)
        load_x(5)
        load_x(6)
        load_x(7)
        load_w(4)
        load_w(5)
        load_w(6)
        load_w(7)
        one = chain_of_tiles(0, 4)
        two = chain_of_tiles(4, 10)
        four = chain(sq[:], 96, t2q[:], "q")

        def each(stage, parts):
            for i in range(len(one[stage])):
                for part in parts:
                    part[stage][i]()

        def guess_of_four():
            each(0, (four,))

        def tables_of_four():
            each(2, (four,))

        later = two[3] + [guess_of_four] + four[1] + [tables_of_four] + four[3]
        done = [0]

        def aside(n=1):
            for i in range(n):
                if done[0] < len(later):
                    later[done[0]]()
                    done[0] += 1

        each(0, (one, two))
        each(1, (one, two))
        each(2, (one,))
        sign_w(0)
        each(2, (two,))
        for i in range(len(one[3])):
            one[3][i]()
            if i >= 5:
                aside()
            if i == 3:
                sign_w(1)
        pe_x(0)
        pe_x(1)
        scale_w(0, 0)
        aside(1)
        scale_w(0, 1)
        pe_w(0)
        quant_x(0)
        sign_w(2)
        aside(1)
        sign_w(3)
        quant_w(0, 0, 2)
        quant_w(0, 2, 4)
        pe_x(2)
        mul(0, 0)
        quant_x(1)
        pe_x(3)
        scale_w(1, 0)
        scale_w(1, 1)
        aside()
        pe_w(1)
        mul(0, 1)
        quant_x(2)
        aside()
        load_w(8)
        load_w(9)
        load_last_scales()
        pick_last_scales()
        quant_x(3)
        mul(0, 2)
        mul(0, 3)
        aside()
        sign_pair(2)
        quant_w(1)
        mul(1, 0)
        mul(1, 1)
        load_w(10)
        load_w(11)
        load_w(12)
        load_w(13)
        scale_w(2, 0)
        scale_w(2, 1)
        pe_w(2)
        mul(1, 2)
        mul(1, 3)
        sign_pair(3)
        for c in range(NPASS):
            load_last_w(c)
        scale_w(3, 0)
        scale_w(3, 1)
        quant_w(2)
        aside(2)
        sign_pair(4)
        aside(2)
        for k in range(2, NK):
            if k + 1 < NK - 1:
                pe_w(k + 1)
            if k + 2 < NK - 1:
                scale_w(k + 2, 0)
                aside(3)
                scale_w(k + 2, 1)
                aside(3)
            if k + 2 == NK - 1:
                scale_last(0)
                scale_last(1)
            if k + 1 < NK:
                quant_w(k + 1)
                aside(3)
            if k + 2 == NK - 1:
                turn_last(0)
                turn_last(1)
                for c in range(NPASS):
                    lay_last(c)
            if k + 3 < NK - 1:
                sign_pair(k + 3)
                aside(3)
            if k + 3 == NK - 1:
                aside(30)
                sign_last()
            for q in range(NQ):
                mul(k, q, 2 if (k, q) == (NK - 1, NQ - 1) else 1)
